import numpy as np
import ml_dtypes


def mxq(x, axis, fmt="e4m3"):
    dtype, down = {"e4m3": (ml_dtypes.float8_e4m3fn, 7), "e5m2": (ml_dtypes.float8_e5m2, 14)}[fmt]
    v = np.moveaxis(np.asarray(x, np.float32).astype(ml_dtypes.bfloat16).astype(np.float64), axis, -1)
    blocks = v.reshape(v.shape[:-1] + (-1, 32))
    amax = np.abs(blocks).max(-1, keepdims=True)
    byte = np.maximum(np.where(amax > 0, np.frexp(amax)[1] - 1 + 127, 0) - down, 1)
    scale = np.exp2(byte - 127.0)
    codes = (blocks / scale).astype(np.float32).astype(dtype).astype(np.float64)
    return np.moveaxis((codes * scale).reshape(v.shape), -1, axis)


WIDE = False


def mx_kscale(k):
    if not WIDE:
        return np.ones(k)
    levels = np.array([20, -20, 10, -10, 0])
    a = np.random.permutation(np.resize(levels, k // 512 * 4)).reshape(k // 512, 4)
    idx = np.arange(k)
    return np.exp2(a[idx // 512, idx % 128 // 32])


BF16 = ml_dtypes.bfloat16


def bf(x):
    return np.asarray(x, np.float32).astype(BF16)


def f64(x):
    return np.asarray(x).astype(np.float64)


B, I, O = 16384, 64, 512
GRID_SIZE = 5
SPLINE_ORDER = 3
NUM_BASIS = GRID_SIZE + SPLINE_ORDER
K = I * NUM_BASIS
GRID = np.linspace(-1.0, 1.0, GRID_SIZE + 2 * SPLINE_ORDER + 1)
EPS = 1e-6


def bspline(t, order):
    te = t[..., None]
    bas = ((te >= GRID[:-1]) & (te < GRID[1:])).astype(np.float64)
    for k in range(1, order + 1):
        nb = bas.shape[-1] - 1
        g_i = GRID[:nb]
        g_i1 = GRID[1:1 + nb]
        g_ik = GRID[k:k + nb]
        g_ik1 = GRID[k + 1:k + 1 + nb]
        dl = g_ik - g_i
        dr = g_ik1 - g_i1
        left = np.where(dl > EPS, (te - g_i) / np.where(dl > EPS, dl, 1.0), 0.0) * bas[..., :nb]
        right = np.where(dr > EPS, (g_ik1 - te) / np.where(dr > EPS, dr, 1.0), 0.0) * bas[..., 1:nb + 1]
        bas = left + right
    return bas


def setup_inputs():
    u = mx_kscale(O)
    x = np.random.standard_normal((B, I))
    c = np.random.standard_normal((O, I, NUM_BASIS)) * (2.0 / np.sqrt(I)) / u[:, None, None]
    g = np.random.standard_normal((B, O)) * np.exp2(np.random.randint(-12, 1, (B, 1))) * u
    return {"x": bf(x), "spline_coeffs": bf(c), "grad_out": bf(g)}


def reference(x, spline_coeffs, grad_out):
    gq = mxq(f64(grad_out), 1, "e5m2")
    cq = mxq(f64(spline_coeffs).reshape(O, K), 0, "e4m3")
    gb = (gq @ cq).reshape(B, I, NUM_BASIS)
    xn = np.tanh(f64(x))
    q = bspline(xn, SPLINE_ORDER - 1)
    p = SPLINE_ORDER
    dbas = p * (q[..., :NUM_BASIS] / (GRID[p:p + NUM_BASIS] - GRID[:NUM_BASIS])
                - q[..., 1:NUM_BASIS + 1] / (GRID[p + 1:p + 1 + NUM_BASIS] - GRID[1:1 + NUM_BASIS]))
    return (gb * dbas).sum(axis=-1) * (1.0 - xn * xn)

@@ -1,0 +1,204 @@
+import math
+from contextlib import ExitStack
+
+import concourse.mybir as mybir
+from concourse.masks import make_identity
+
+F32 = mybir.dt.float32
+BF16 = mybir.dt.bfloat16
+I32 = mybir.dt.int32
+U32 = mybir.dt.uint32
+U8 = mybir.dt.uint8
+E4X4 = mybir.dt.float8_e4m3fn_x4
+E5X4 = mybir.dt.float8_e5m2_x4
+ALU = mybir.AluOpType
+ACT = mybir.ActivationFunctionType
+
+B, I, O, NB = 16384, 64, 512, 8
+FLOPS = 2 * B * O * I * NB
+P = 128
+GROUP_TILES = 8
+GROUP = P * GROUP_TILES
+N_GROUPS = B // GROUP
+CHUNK_TILES = 4
+CHUNK = P * CHUNK_TILES
+INV_H = 5.5
+
+
+def tile_kan_layer_t_kernel(tc, x, spline_coeffs, grad_out, out):
+    nc = tc.nc
+    with ExitStack() as ctx:
+        const = ctx.enter_context(tc.tile_pool(name="const", bufs=1))
+        gpool = ctx.enter_context(tc.tile_pool(name="gpool", bufs=3))
+        prep = ctx.enter_context(tc.tile_pool(name="prep", bufs=2))
+        work = ctx.enter_context(tc.tile_pool(name="work", bufs=2))
+        blk = ctx.enter_context(tc.tile_pool(name="blk", bufs=4))
+        ps_g = ctx.enter_context(tc.psum_pool(name="ps_g", bufs=2))
+        ps_t = ctx.enter_context(tc.psum_pool(name="ps_t", bufs=1))
+        ps_m = ctx.enter_context(tc.psum_pool(name="ps_m", bufs=3))
+        ps_a = ctx.enter_context(tc.psum_pool(name="ps_a", bufs=1))
+
+        c2d = spline_coeffs.rearrange("o i k -> o (i k)")
+        craw = const.tile([P, 4, O], BF16)
+        for u in range(2):
+            nc.sync.dma_start(
+                out=craw[:, 2 * u : 2 * u + 2, :],
+                in_=c2d[256 * u : 256 * u + 256, :].rearrange("(q e) c -> q e c", e=2),
+            )
+        x_sb = const.tile([P, N_GROUPS, GROUP_TILES, I], BF16)
+        x_v = x.rearrange("(g p t) i -> p g t i", p=P, t=GROUP_TILES)
+        nc.sync.dma_start(out=x_sb[:, 0:4, :, :], in_=x_v[:, 0:4, :, :])
+
+        ident = const.tile([P, P], F32)
+        make_identity(nc, ident[:])
+        sel = const.tile([P, I], F32)
+        nc.vector.tensor_add(out=sel[:], in0=ident[:, 0:I], in1=ident[:, I : 2 * I])
+        lo = const.tile([P, 4], F32)
+        hi = const.tile([P, 4], F32)
+        nb = const.tile([P, 4], F32)
+        for c in range(4):
+            for k2 in range(2):
+                k = 2 * c + k2
+                rows = slice(64 * k2, 64 * k2 + 64)
+                nc.vector.memset(lo[rows, c : c + 1], 0.5 * k)
+                nc.vector.memset(hi[rows, c : c + 1], 0.5 * k + 2.0)
+                nc.vector.memset(nb[rows, c : c + 1], -(k + 1.0))
+
+        cgrp = const.tile([P, O, 4], BF16, align_bytes=64)
+        cgrp_v = cgrp[:].rearrange("q (k i) t -> q k i t", k=NB)
+        craw_v = craw[:].rearrange("q t (i k) -> q k i t", k=NB)
+        for k in range(NB):
+            nc.vector.tensor_copy(out=cgrp_v[:, k, :, :], in_=craw_v[:, k, :, :])
+        ccodes = const.tile([P, O], U32, align_bytes=64)
+        cscales = const.tile([P, O], U8, align_bytes=64)
+        nc.vector.quantize_mx(
+            out=ccodes[:].bitcast(E4X4),
+            scales=cscales[:],
+            in_=cgrp[:].rearrange("q c t -> q (c t)"),
+        )
+
+        for g in range(N_GROUPS):
+            g_sb = gpool.tile([P, GROUP_TILES, O], BF16)
+            nc.sync.dma_start(
+                out=g_sb[:],
+                in_=grad_out[g * GROUP : (g + 1) * GROUP, :].rearrange("(p t) o -> p t o", t=GROUP_TILES),
+            )
+            if g % 4 == 0 and g + 4 < N_GROUPS:
+                nc.sync.dma_start(out=x_sb[:, g + 4 : g + 8, :, :], in_=x_v[:, g + 4 : g + 8, :, :])
+
+            W = GROUP_TILES * I
+            th = prep.tile([P, W], F32)
+            nc.scalar.activation(out=th[:], in_=x_sb[:, g, :, :].rearrange("p t i -> p (t i)"), func=ACT.Tanh)
+            uu = prep.tile([P, W], F32)
+            nc.scalar.activation(out=uu[:], in_=th[:], func=ACT.Copy, bias=INV_H, scale=INV_H)
+            wq = prep.tile([P, W], F32)
+            nc.scalar.activation(out=wq[:], in_=th[:], func=ACT.Square, scale=math.sqrt(INV_H))
+            mi = prep.tile([P, W], I32)
+            nc.vector.tensor_scalar(
+                out=mi[:], in0=th[:], scalar1=0.5 * INV_H, scalar2=0.5 * INV_H, op0=ALU.mult, op1=ALU.add
+            )
+            yy = prep.tile([P, W], F32)
+            nc.vector.scalar_tensor_tensor(out=yy[:], in0=mi[:], scalar=-2.0, in1=uu[:], op0=ALU.mult, op1=ALU.add)
+            ay = prep.tile([P, W], F32)
+            nc.scalar.activation(out=ay[:], in_=yy[:], func=ACT.Abs)
+            zz = prep.tile([P, W], F32)
+            nc.vector.tensor_tensor(out=zz[:], in0=yy[:], in1=ay[:], op=ALU.mult)
+            xt = prep.tile([P, GROUP_TILES, 3 * I], F32)
+            nc.vector.scalar_tensor_tensor(
+                out=xt[:, :, 0:I],
+                in0=mi[:].rearrange("p (t i) -> p t i", i=I),
+                scalar=2.0,
+                in1=zz[:].rearrange("p (t i) -> p t i", i=I),
+                op0=ALU.mult,
+                op1=ALU.add,
+            )
+            nc.vector.scalar_tensor_tensor(
+                out=xt[:, :, I : 2 * I],
+                in0=uu[:].rearrange("p (t i) -> p t i", i=I),
+                scalar=2.0,
+                in1=xt[:, :, 0:I],
+                op0=ALU.mult,
+                op1=ALU.subtract,
+            )
+            nc.scalar.copy(out=xt[:, :, 2 * I : 3 * I], in_=xt[:, :, 0:I])
+
+            o_sb = work.tile([P, GROUP_TILES, I], F32)
+            for h in range(GROUP_TILES // CHUNK_TILES):
+                t0 = h * CHUNK_TILES
+                grp = work.tile([P, 4 * CHUNK], BF16, align_bytes=64)
+                grp_w = grp[:].bitcast(F32)
+                for b in range(2):
+                    g_t = ps_g.tile([P, 2, 2, P], F32)
+                    for a in range(2):
+                        words = g_sb[:, t0 + 2 * b + a, :].bitcast(F32)
+                        for u in range(2):
+                            nc.tensor.transpose(g_t[:, a, u, :], words[:, P * u : P * u + P], ident[:])
+                    nc.scalar.copy(
+                        out=grp_w[:, 512 * b : 512 * b + 512].rearrange("p (a r u) -> p a r u", a=2, u=2),
+                        in_=g_t[:].rearrange("p a u r -> p a r u"),
+                    )
+                gcodes = work.tile([P, CHUNK], U32, align_bytes=64)
+                gscales = work.tile([P, CHUNK], U8, align_bytes=64)
+                nc.vector.quantize_mx(out=gcodes[:].bitcast(E5X4), scales=gscales[:], in_=grp[:])
+
+                t1 = ps_t.tile([P, CHUNK], F32)
+                t2 = ps_t.tile([P, CHUNK], F32)
+                for a in range(CHUNK_TILES):
+                    nc.tensor.transpose(t1[:, P * a : P * a + P], xt[:, t0 + a, 0 : 2 * I], ident[:])
+                for a in range(CHUNK_TILES):
+                    nc.tensor.transpose(t2[:, P * a : P * a + P], xt[:, t0 + a, I : 3 * I], ident[:])
+                t1h = work.tile([P, CHUNK], F32)
+                nc.scalar.activation(out=t1h[:], in_=t1[:], func=ACT.Copy, scale=0.5)
+
+                prods = []
+                for c in range(4):
+                    gb = ps_m.tile([P, CHUNK], F32)
+                    nc.tensor.matmul_mx(
+                        out=gb[:],
+                        lhsT=ccodes[:, P * c : P * c + P].bitcast(E4X4),
+                        lhsT_scale=cscales[:, P * c : P * c + P],
+                        rhs=gcodes[:].bitcast(E5X4),
+                        rhs_scale=gscales[:],
+                        start=True,
+                        stop=True,
+                    )
+                    r_b = blk.tile([P, CHUNK], F32)
+                    nc.scalar.activation(out=r_b[:], in_=t2[:], func=ACT.Relu, bias=nb[:, c : c + 1], scale=1.0)
+                    c_a = blk.tile([P, CHUNK], F32)
+                    nc.gpsimd.tensor_scalar(
+                        out=c_a[:], in0=t1h[:], scalar1=hi[:, c : c + 1], scalar2=lo[:, c : c + 1],
+                        op0=ALU.min, op1=ALU.max,
+                    )
+                    nd = blk.tile([P, CHUNK], F32)
+                    nc.vector.scalar_tensor_tensor(
+                        out=nd[:], in0=r_b[:], scalar=2.0, in1=c_a[:], op0=ALU.min, op1=ALU.subtract
+                    )
+                    pr = blk.tile([P, CHUNK], F32, name="pr%d" % c)
+                    nc.vector.scalar_tensor_tensor(
+                        out=pr[:], in0=nd[:], scalar=lo[:, c : c + 1], in1=gb[:], op0=ALU.add, op1=ALU.mult
+                    )
+                    prods.append(pr)
+                nc.vector.tensor_add(out=prods[1][:], in0=prods[0][:], in1=prods[1][:])
+
+                acc = ps_a.tile([P, CHUNK_TILES, I], F32)
+                for a in range(CHUNK_TILES):
+                    for j in range(1, 4):
+                        nc.tensor.matmul(
+                            acc[:, a, :],
+                            lhsT=prods[j][:, P * a : P * a + P],
+                            rhs=sel[:],
+                            start=(j == 1),
+                            stop=(j == 3),
+                        )
+                nc.vector.scalar_tensor_tensor(
+                    out=o_sb[:, t0 : t0 + CHUNK_TILES, :].rearrange("p a i -> p (a i)"),
+                    in0=wq[:, t0 * I : (t0 + CHUNK_TILES) * I],
+                    scalar=INV_H,
+                    in1=acc[:].rearrange("p a i -> p (a i)"),
+                    op0=ALU.subtract,
+                    op1=ALU.mult,
+                )
+            nc.sync.dma_start(
+                out=out[g * GROUP : (g + 1) * GROUP, :].rearrange("(p t) i -> p t i", t=GROUP_TILES),
+                in_=o_sb[:],
+            )

@@ -53,16 +53,13 @@ def tile_kan_layer_t_kernel(tc, x, spline_coeffs, grad_out, out):
         make_identity(nc, ident[:])
         sel = const.tile([P, I], F32)
         nc.vector.tensor_add(out=sel[:], in0=ident[:, 0:I], in1=ident[:, I : 2 * I])
-        lo = const.tile([P, 4], F32)
-        hi = const.tile([P, 4], F32)
         nb = const.tile([P, 4], F32)
-        for c in range(4):
-            for k2 in range(2):
-                k = 2 * c + k2
-                rows = slice(64 * k2, 64 * k2 + 64)
-                nc.vector.memset(lo[rows, c : c + 1], 0.5 * k)
-                nc.vector.memset(hi[rows, c : c + 1], 0.5 * k + 2.0)
-                nc.vector.memset(nb[rows, c : c + 1], -(k + 1.0))
+        nh = const.tile([P, 1], F32)
+        for k2 in range(2):
+            rows = slice(64 * k2, 64 * k2 + 64)
+            nc.vector.memset(nh[rows, :], -0.5 * k2)
+            for c in range(4):
+                nc.vector.memset(nb[rows, c : c + 1], -(2 * c + k2 + 1.0))
 
         cgrp = const.tile([P, O, 4], BF16, align_bytes=64)
         cgrp_v = cgrp[:].rearrange("q (k i) t -> q k i t", k=NB)
@@ -148,7 +145,7 @@ def tile_kan_layer_t_kernel(tc, x, spline_coeffs, grad_out, out):
                 for a in range(CHUNK_TILES):
                     nc.tensor.transpose(t2[:, P * a : P * a + P], xt[:, t0 + a, I : 3 * I], ident[:])
                 t1h = work.tile([P, CHUNK], F32)
-                nc.scalar.activation(out=t1h[:], in_=t1[:], func=ACT.Copy, scale=0.5)
+                nc.scalar.activation(out=t1h[:], in_=t1[:], func=ACT.Identity, bias=nh[:, 0:1], scale=0.5)
 
                 prods = []
                 for c in range(4):
@@ -166,7 +163,7 @@ def tile_kan_layer_t_kernel(tc, x, spline_coeffs, grad_out, out):
                     nc.scalar.activation(out=r_b[:], in_=t2[:], func=ACT.Relu, bias=nb[:, c : c + 1], scale=1.0)
                     c_a = blk.tile([P, CHUNK], F32)
                     nc.gpsimd.tensor_scalar(
-                        out=c_a[:], in0=t1h[:], scalar1=hi[:, c : c + 1], scalar2=lo[:, c : c + 1],
+                        out=c_a[:], in0=t1h[:], scalar1=c + 2.0, scalar2=1.0 * c,
                         op0=ALU.min, op1=ALU.max,
                     )
                     nd = blk.tile([P, CHUNK], F32)
@@ -175,7 +172,7 @@ def tile_kan_layer_t_kernel(tc, x, spline_coeffs, grad_out, out):
                     )
                     pr = blk.tile([P, CHUNK], F32, name="pr%d" % c)
                     nc.vector.scalar_tensor_tensor(
-                        out=pr[:], in0=nd[:], scalar=lo[:, c : c + 1], in1=gb[:], op0=ALU.add, op1=ALU.mult
+                        out=pr[:], in0=nd[:], scalar=1.0 * c, in1=gb[:], op0=ALU.add, op1=ALU.mult
                     )
                     prods.append(pr)
                 nc.vector.tensor_add(out=prods[1][:], in0=prods[0][:], in1=prods[1][:])

@@ -29,10 +29,12 @@ def tile_kan_layer_t_kernel(tc, x, spline_coeffs, grad_out, out):
     nc = tc.nc
     with ExitStack() as ctx:
         const = ctx.enter_context(tc.tile_pool(name="const", bufs=1))
-        gpool = ctx.enter_context(tc.tile_pool(name="gpool", bufs=3))
+        gpool = ctx.enter_context(tc.tile_pool(name="gpool", bufs=4))
         prep = ctx.enter_context(tc.tile_pool(name="prep", bufs=2))
+        keep = ctx.enter_context(tc.tile_pool(name="keep", bufs=4))
         work = ctx.enter_context(tc.tile_pool(name="work", bufs=2))
-        blk = ctx.enter_context(tc.tile_pool(name="blk", bufs=4))
+        ahead = ctx.enter_context(tc.tile_pool(name="ahead", bufs=8))
+        four = ctx.enter_context(tc.tile_pool(name="four", bufs=4))
         ps_g = ctx.enter_context(tc.psum_pool(name="ps_g", bufs=2))
         ps_t = ctx.enter_context(tc.psum_pool(name="ps_t", bufs=1))
         ps_m = ctx.enter_context(tc.psum_pool(name="ps_m", bufs=3))
@@ -47,7 +49,7 @@ def tile_kan_layer_t_kernel(tc, x, spline_coeffs, grad_out, out):
             )
         x_sb = const.tile([P, N_GROUPS, GROUP_TILES, I], BF16)
         x_v = x.rearrange("(g p t) i -> p g t i", p=P, t=GROUP_TILES)
-        nc.sync.dma_start(out=x_sb[:, 0:4, :, :], in_=x_v[:, 0:4, :, :])
+        nc.sync.dma_start(out=x_sb[:, 0:2, :, :], in_=x_v[:, 0:2, :, :])
 
         ident = const.tile([P, P], F32)
         make_identity(nc, ident[:])
@@ -74,128 +76,263 @@ def tile_kan_layer_t_kernel(tc, x, spline_coeffs, grad_out, out):
             in_=cgrp[:].rearrange("q c t -> q (c t)"),
         )
 
-        for g in range(N_GROUPS):
-            g_sb = gpool.tile([P, GROUP_TILES, O], BF16)
+        W = GROUP_TILES * I
+        N_CHUNKS = B // CHUNK
+        g_tiles = {}
+        pre = {}
+        chk = {}
+
+        def load_group(g):
+            g_sb = gpool.tile([P, GROUP_TILES, O], BF16, name="g_sb")
             nc.sync.dma_start(
                 out=g_sb[:],
                 in_=grad_out[g * GROUP : (g + 1) * GROUP, :].rearrange("(p t) o -> p t o", t=GROUP_TILES),
             )
-            if g % 4 == 0 and g + 4 < N_GROUPS:
-                nc.sync.dma_start(out=x_sb[:, g + 4 : g + 8, :, :], in_=x_v[:, g + 4 : g + 8, :, :])
+            g_tiles[g] = g_sb
 
-            W = GROUP_TILES * I
-            th = prep.tile([P, W], F32)
+        def v3(t):
+            return t[:].rearrange("p (t i) -> p t i", i=I)
+
+        def prep_s1(g):
+            th = prep.tile([P, W], F32, name="th")
             nc.scalar.activation(out=th[:], in_=x_sb[:, g, :, :].rearrange("p t i -> p (t i)"), func=ACT.Tanh)
-            uu = prep.tile([P, W], F32)
+            uu = prep.tile([P, W], F32, name="uu")
             nc.scalar.activation(out=uu[:], in_=th[:], func=ACT.Copy, bias=INV_H, scale=INV_H)
-            wq = prep.tile([P, W], F32)
+            wq = keep.tile([P, W], F32, name="wq")
             nc.scalar.activation(out=wq[:], in_=th[:], func=ACT.Square, scale=math.sqrt(INV_H))
-            mi = prep.tile([P, W], I32)
+            pre[g] = {"th": th, "uu": uu, "wq": wq}
+
+        def prep_v1(g):
+            mi = prep.tile([P, W], I32, name="mi")
             nc.vector.tensor_scalar(
-                out=mi[:], in0=th[:], scalar1=0.5 * INV_H, scalar2=0.5 * INV_H, op0=ALU.mult, op1=ALU.add
+                out=mi[:], in0=pre[g]["th"][:], scalar1=0.5 * INV_H, scalar2=0.5 * INV_H, op0=ALU.mult, op1=ALU.add
             )
-            yy = prep.tile([P, W], F32)
-            nc.vector.scalar_tensor_tensor(out=yy[:], in0=mi[:], scalar=-2.0, in1=uu[:], op0=ALU.mult, op1=ALU.add)
-            ay = prep.tile([P, W], F32)
-            nc.scalar.activation(out=ay[:], in_=yy[:], func=ACT.Abs)
-            zz = prep.tile([P, W], F32)
-            nc.vector.tensor_tensor(out=zz[:], in0=yy[:], in1=ay[:], op=ALU.mult)
-            xt = prep.tile([P, GROUP_TILES, 3 * I], F32)
+            pre[g]["mi"] = mi
+
+        def prep_v2(g):
+            yy = prep.tile([P, W], F32, name="yy")
             nc.vector.scalar_tensor_tensor(
-                out=xt[:, :, 0:I],
-                in0=mi[:].rearrange("p (t i) -> p t i", i=I),
-                scalar=2.0,
-                in1=zz[:].rearrange("p (t i) -> p t i", i=I),
-                op0=ALU.mult,
-                op1=ALU.add,
+                out=yy[:], in0=pre[g]["mi"][:], scalar=-2.0, in1=pre[g]["uu"][:], op0=ALU.mult, op1=ALU.add
             )
+            pre[g]["yy"] = yy
+
+        def prep_s2(g):
+            ay = prep.tile([P, W], F32, name="ay")
+            nc.scalar.activation(out=ay[:], in_=pre[g]["yy"][:], func=ACT.Abs)
+            pre[g]["ay"] = ay
+
+        def prep_v3(g):
+            zz = prep.tile([P, W], F32, name="zz")
+            nc.vector.tensor_tensor(out=zz[:], in0=pre[g]["yy"][:], in1=pre[g]["ay"][:], op=ALU.mult)
+            pre[g]["zz"] = zz
+
+        def prep_v4(g):
+            xt = prep.tile([P, GROUP_TILES, 3 * I], F32, name="xt")
             nc.vector.scalar_tensor_tensor(
-                out=xt[:, :, I : 2 * I],
-                in0=uu[:].rearrange("p (t i) -> p t i", i=I),
-                scalar=2.0,
-                in1=xt[:, :, 0:I],
-                op0=ALU.mult,
-                op1=ALU.subtract,
+                out=xt[:, :, 0:I], in0=v3(pre[g]["mi"]), scalar=2.0, in1=v3(pre[g]["zz"]), op0=ALU.mult, op1=ALU.add
             )
+            pre[g]["xt"] = xt
+
+        def prep_v5(g):
+            xt = pre[g]["xt"]
+            nc.vector.scalar_tensor_tensor(
+                out=xt[:, :, I : 2 * I], in0=v3(pre[g]["uu"]), scalar=2.0, in1=xt[:, :, 0:I],
+                op0=ALU.mult, op1=ALU.subtract,
+            )
+
+        def prep_s3(g):
+            xt = pre[g]["xt"]
             nc.scalar.copy(out=xt[:, :, 2 * I : 3 * I], in_=xt[:, :, 0:I])
 
-            o_sb = work.tile([P, GROUP_TILES, I], F32)
-            for h in range(GROUP_TILES // CHUNK_TILES):
-                t0 = h * CHUNK_TILES
-                grp = work.tile([P, 4 * CHUNK], BF16, align_bytes=64)
-                grp_w = grp[:].bitcast(F32)
-                for b in range(2):
-                    g_t = ps_g.tile([P, 2, 2, P], F32)
-                    for a in range(2):
-                        words = g_sb[:, t0 + 2 * b + a, :].bitcast(F32)
-                        for u in range(2):
-                            nc.tensor.transpose(g_t[:, a, u, :], words[:, P * u : P * u + P], ident[:])
-                    nc.scalar.copy(
-                        out=grp_w[:, 512 * b : 512 * b + 512].rearrange("p (a r u) -> p a r u", a=2, u=2),
-                        in_=g_t[:].rearrange("p a u r -> p a r u"),
-                    )
-                gcodes = work.tile([P, CHUNK], U32, align_bytes=64)
-                gscales = work.tile([P, CHUNK], U8, align_bytes=64)
-                nc.vector.quantize_mx(out=gcodes[:].bitcast(E5X4), scales=gscales[:], in_=grp[:])
+        def pe_grad(n):
+            g, t0 = n // 2, (n % 2) * CHUNK_TILES
+            g_sb = g_tiles[g]
+            banks = []
+            for b in range(2):
+                g_t = ps_g.tile([P, 2, 2, P], F32, name="g_t")
+                for a in range(2):
+                    words = g_sb[:, t0 + 2 * b + a, :].bitcast(F32)
+                    for u in range(2):
+                        nc.tensor.transpose(g_t[:, a, u, :], words[:, P * u : P * u + P], ident[:])
+                banks.append(g_t)
+            chk[n] = {"banks": banks, "rb": {}, "gb": {}, "pr": {}, "ca": {}, "nd": {}}
 
-                t1 = ps_t.tile([P, CHUNK], F32)
-                t2 = ps_t.tile([P, CHUNK], F32)
-                for a in range(CHUNK_TILES):
-                    nc.tensor.transpose(t1[:, P * a : P * a + P], xt[:, t0 + a, 0 : 2 * I], ident[:])
-                for a in range(CHUNK_TILES):
-                    nc.tensor.transpose(t2[:, P * a : P * a + P], xt[:, t0 + a, I : 3 * I], ident[:])
-                t1h = work.tile([P, CHUNK], F32)
-                nc.scalar.activation(out=t1h[:], in_=t1[:], func=ACT.Identity, bias=nh[:, 0:1], scale=0.5)
+        def pe_tau(n):
+            g, t0 = n // 2, (n % 2) * CHUNK_TILES
+            xt = pre[g]["xt"]
+            t1 = ps_t.tile([P, CHUNK], F32, name="t1")
+            t2 = ps_t.tile([P, CHUNK], F32, name="t2")
+            for a in range(CHUNK_TILES):
+                nc.tensor.transpose(t1[:, P * a : P * a + P], xt[:, t0 + a, 0 : 2 * I], ident[:])
+            for a in range(CHUNK_TILES):
+                nc.tensor.transpose(t2[:, P * a : P * a + P], xt[:, t0 + a, I : 3 * I], ident[:])
+            chk[n]["t1"] = t1
+            chk[n]["t2"] = t2
 
-                prods = []
-                for c in range(4):
-                    gb = ps_m.tile([P, CHUNK], F32)
-                    nc.tensor.matmul_mx(
-                        out=gb[:],
-                        lhsT=ccodes[:, P * c : P * c + P].bitcast(E4X4),
-                        lhsT_scale=cscales[:, P * c : P * c + P],
-                        rhs=gcodes[:].bitcast(E5X4),
-                        rhs_scale=gscales[:],
-                        start=True,
-                        stop=True,
-                    )
-                    r_b = blk.tile([P, CHUNK], F32)
-                    nc.scalar.activation(out=r_b[:], in_=t2[:], func=ACT.Relu, bias=nb[:, c : c + 1], scale=1.0)
-                    c_a = blk.tile([P, CHUNK], F32)
-                    nc.gpsimd.tensor_scalar(
-                        out=c_a[:], in0=t1h[:], scalar1=c + 2.0, scalar2=1.0 * c,
-                        op0=ALU.min, op1=ALU.max,
-                    )
-                    nd = blk.tile([P, CHUNK], F32)
-                    nc.vector.scalar_tensor_tensor(
-                        out=nd[:], in0=r_b[:], scalar=2.0, in1=c_a[:], op0=ALU.min, op1=ALU.subtract
-                    )
-                    pr = blk.tile([P, CHUNK], F32, name="pr%d" % c)
-                    nc.vector.scalar_tensor_tensor(
-                        out=pr[:], in0=nd[:], scalar=1.0 * c, in1=gb[:], op0=ALU.add, op1=ALU.mult
-                    )
-                    prods.append(pr)
-                nc.vector.tensor_add(out=prods[1][:], in0=prods[0][:], in1=prods[1][:])
-
-                acc = ps_a.tile([P, CHUNK_TILES, I], F32)
-                for a in range(CHUNK_TILES):
-                    for j in range(1, 4):
-                        nc.tensor.matmul(
-                            acc[:, a, :],
-                            lhsT=prods[j][:, P * a : P * a + P],
-                            rhs=sel[:],
-                            start=(j == 1),
-                            stop=(j == 3),
-                        )
-                nc.vector.scalar_tensor_tensor(
-                    out=o_sb[:, t0 : t0 + CHUNK_TILES, :].rearrange("p a i -> p (a i)"),
-                    in0=wq[:, t0 * I : (t0 + CHUNK_TILES) * I],
-                    scalar=INV_H,
-                    in1=acc[:].rearrange("p a i -> p (a i)"),
-                    op0=ALU.subtract,
-                    op1=ALU.mult,
+        def s_evac(n):
+            grp = work.tile([P, 4 * CHUNK], BF16, align_bytes=64, name="grp")
+            grp_w = grp[:].bitcast(F32)
+            for b in range(2):
+                nc.scalar.copy(
+                    out=grp_w[:, 512 * b : 512 * b + 512].rearrange("p (a r u) -> p a r u", a=2, u=2),
+                    in_=chk[n]["banks"][b][:].rearrange("p a u r -> p a r u"),
                 )
-            nc.sync.dma_start(
-                out=out[g * GROUP : (g + 1) * GROUP, :].rearrange("(p t) i -> p t i", t=GROUP_TILES),
-                in_=o_sb[:],
+            chk[n]["grp"] = grp
+
+        def v_quant(n):
+            gcodes = work.tile([P, CHUNK], U32, align_bytes=64, name="gcodes")
+            gscales = work.tile([P, CHUNK], U8, align_bytes=64, name="gscales")
+            nc.vector.quantize_mx(out=gcodes[:].bitcast(E5X4), scales=gscales[:], in_=chk[n]["grp"][:])
+            chk[n]["gcodes"] = gcodes
+            chk[n]["gscales"] = gscales
+
+        def s_t1h(n):
+            t1h = work.tile([P, CHUNK], F32, name="t1h")
+            nc.scalar.activation(out=t1h[:], in_=chk[n]["t1"][:], func=ACT.Identity, bias=nh[:, 0:1], scale=0.5)
+            chk[n]["t1h"] = t1h
+
+        def s_rb(n, c):
+            r_b = ahead.tile([P, CHUNK], F32, name="r_b")
+            nc.scalar.activation(out=r_b[:], in_=chk[n]["t2"][:], func=ACT.Relu, bias=nb[:, c : c + 1], scale=1.0)
+            chk[n]["rb"][c] = r_b
+
+        def pe_mx(n, c):
+            gb = ps_m.tile([P, CHUNK], F32, name="gb")
+            nc.tensor.matmul_mx(
+                out=gb[:],
+                lhsT=ccodes[:, P * c : P * c + P].bitcast(E4X4),
+                lhsT_scale=cscales[:, P * c : P * c + P],
+                rhs=chk[n]["gcodes"][:].bitcast(E5X4),
+                rhs_scale=chk[n]["gscales"][:],
+                start=True,
+                stop=True,
             )
+            chk[n]["gb"][c] = gb
+
+        def v_ca(n, c):
+            c_a = four.tile([P, CHUNK], F32, name="c_a")
+            CLAMP_ENGINE.tensor_scalar(
+                out=c_a[:], in0=chk[n]["t1h"][:], scalar1=c + 2.0, scalar2=1.0 * c, op0=ALU.min, op1=ALU.max
+            )
+            chk[n]["ca"][c] = c_a
+
+        def v_nd(n, c):
+            nd = four.tile([P, CHUNK], F32, name="nd")
+            nc.vector.scalar_tensor_tensor(
+                out=nd[:], in0=chk[n]["rb"][c][:], scalar=2.0, in1=chk[n]["ca"][c][:], op0=ALU.min, op1=ALU.subtract
+            )
+            chk[n]["nd"][c] = nd
+
+        def v_pr(n, c):
+            nd = chk[n]["nd"][c]
+            pr = work.tile([P, CHUNK], F32, name="pr%d" % c)
+            nc.vector.scalar_tensor_tensor(
+                out=pr[:], in0=nd[:], scalar=1.0 * c, in1=chk[n]["gb"][c][:], op0=ALU.add, op1=ALU.mult
+            )
+            chk[n]["pr"][c] = pr
+
+        def v_preadd(n):
+            pr = chk[n]["pr"]
+            nc.vector.tensor_add(out=pr[1][:], in0=pr[0][:], in1=pr[1][:])
+
+        def pe_sel(n):
+            acc = ps_a.tile([P, CHUNK_TILES, I], F32, name="acc")
+            for a in range(CHUNK_TILES):
+                for j in range(1, 4):
+                    nc.tensor.matmul(
+                        acc[:, a, :], lhsT=chk[n]["pr"][j][:, P * a : P * a + P], rhs=sel[:],
+                        start=(j == 1), stop=(j == 3),
+                    )
+            chk[n]["acc"] = acc
+
+        def v_final(n):
+            g, t0 = n // 2, (n % 2) * CHUNK_TILES
+            if t0 == 0:
+                o_new = work.tile([P, GROUP_TILES, I], F32, name="o_sb")
+                pre[g]["o_sb"] = o_new
+            o_sb = pre[g]["o_sb"]
+            nc.vector.scalar_tensor_tensor(
+                out=o_sb[:, t0 : t0 + CHUNK_TILES, :].rearrange("p a i -> p (a i)"),
+                in0=pre[g]["wq"][:, t0 * I : (t0 + CHUNK_TILES) * I],
+                scalar=INV_H,
+                in1=chk[n]["acc"][:].rearrange("p a i -> p (a i)"),
+                op0=ALU.subtract,
+                op1=ALU.mult,
+            )
+            if t0 != 0:
+                nc.sync.dma_start(
+                    out=out[g * GROUP : (g + 1) * GROUP, :].rearrange("(p t) i -> p t i", t=GROUP_TILES),
+                    in_=o_sb[:],
+                )
+
+        def ok(n):
+            return 0 <= n < N_CHUNKS
+
+        CLAMP_ENGINE = nc.vector
+        loaded = [0]
+
+        def grp_at(num):
+            if num % 2 == 0 and 0 <= num // 2 < N_GROUPS:
+                return num // 2
+            return -1
+
+        with tc.manual_schedule():
+            for n in range(-4, N_CHUNKS + 1):
+                while loaded[0] < N_GROUPS and 2 * loaded[0] - 7 <= n:
+                    load_group(loaded[0])
+                    if loaded[0] == 0:
+                        nc.sync.dma_start(out=x_sb[:, 2:N_GROUPS, :, :], in_=x_v[:, 2:N_GROUPS, :, :])
+                    loaded[0] += 1
+                ga, gb_, gc = grp_at(n + 4), grp_at(n + 3), grp_at(n + 2)
+                if ok(n + 1):
+                    pe_tau(n + 1)
+                if ok(n + 2):
+                    pe_grad(n + 2)
+                if ok(n - 1):
+                    pe_sel(n - 1)
+                if ok(n + 1):
+                    s_t1h(n + 1)
+                    for c in range(4):
+                        s_rb(n + 1, c)
+                if ok(n + 2):
+                    s_evac(n + 2)
+                if ok(n):
+                    for c in range(4):
+                        v_ca(n, c)
+                if gb_ >= 0:
+                    prep_v1(gb_)
+                if gc >= 0:
+                    prep_v3(gc)
+                if ok(n):
+                    for c in range(4):
+                        v_nd(n, c)
+                if ok(n + 1):
+                    v_quant(n + 1)
+                if ok(n):
+                    v_pr(n, 0)
+                    pe_mx(n, 3)
+                    v_pr(n, 1)
+                if ok(n + 1):
+                    pe_mx(n + 1, 0)
+                if ok(n):
+                    v_pr(n, 2)
+                if ok(n + 1):
+                    pe_mx(n + 1, 1)
+                if ok(n):
+                    v_pr(n, 3)
+                if ok(n + 1):
+                    pe_mx(n + 1, 2)
+                if gb_ >= 0:
+                    prep_v2(gb_)
+                    prep_s2(gb_)
+                if gc >= 0:
+                    prep_v4(gc)
+                if ok(n):
+                    v_preadd(n)
+                if ok(n - 1):
+                    v_final(n - 1)
+                if gc >= 0:
+                    prep_v5(gc)
+                    prep_s3(gc)
+                if ga >= 0:
+                    prep_s1(ga)

@@ -33,13 +33,14 @@ def tile_kan_layer_t_kernel(tc, x, spline_coeffs, grad_out, out):
         prep = ctx.enter_context(tc.tile_pool(name="prep", bufs=2))
         keep = ctx.enter_context(tc.tile_pool(name="keep", bufs=4))
         work = ctx.enter_context(tc.tile_pool(name="work", bufs=2))
-        ahead = ctx.enter_context(tc.tile_pool(name="ahead", bufs=8))
-        four = ctx.enter_context(tc.tile_pool(name="four", bufs=4))
         ps_g = ctx.enter_context(tc.psum_pool(name="ps_g", bufs=2))
         ps_t = ctx.enter_context(tc.psum_pool(name="ps_t", bufs=1))
         ps_m = ctx.enter_context(tc.psum_pool(name="ps_m", bufs=3))
         ps_a = ctx.enter_context(tc.psum_pool(name="ps_a", bufs=1))
 
+        x_sb = const.tile([P, N_GROUPS, GROUP_TILES, I], BF16)
+        x_v = x.rearrange("(g p t) i -> p g t i", p=P, t=GROUP_TILES)
+        nc.sync.dma_start(out=x_sb[:, 0:2, :, :], in_=x_v[:, 0:2, :, :])
         c2d = spline_coeffs.rearrange("o i k -> o (i k)")
         craw = const.tile([P, 4, O], BF16)
         for u in range(2):
@@ -47,9 +48,6 @@ def tile_kan_layer_t_kernel(tc, x, spline_coeffs, grad_out, out):
                 out=craw[:, 2 * u : 2 * u + 2, :],
                 in_=c2d[256 * u : 256 * u + 256, :].rearrange("(q e) c -> q e c", e=2),
             )
-        x_sb = const.tile([P, N_GROUPS, GROUP_TILES, I], BF16)
-        x_v = x.rearrange("(g p t) i -> p g t i", p=P, t=GROUP_TILES)
-        nc.sync.dma_start(out=x_sb[:, 0:2, :, :], in_=x_v[:, 0:2, :, :])
 
         ident = const.tile([P, P], F32)
         make_identity(nc, ident[:])
@@ -66,15 +64,18 @@ def tile_kan_layer_t_kernel(tc, x, spline_coeffs, grad_out, out):
         cgrp = const.tile([P, O, 4], BF16, align_bytes=64)
         cgrp_v = cgrp[:].rearrange("q (k i) t -> q k i t", k=NB)
         craw_v = craw[:].rearrange("q t (i k) -> q k i t", k=NB)
-        for k in range(NB):
-            nc.vector.tensor_copy(out=cgrp_v[:, k, :, :], in_=craw_v[:, k, :, :])
         ccodes = const.tile([P, O], U32, align_bytes=64)
         cscales = const.tile([P, O], U8, align_bytes=64)
-        nc.vector.quantize_mx(
-            out=ccodes[:].bitcast(E4X4),
-            scales=cscales[:],
-            in_=cgrp[:].rearrange("q c t -> q (c t)"),
-        )
+
+        def c_copy(k):
+            nc.vector.tensor_copy(out=cgrp_v[:, k, :, :], in_=craw_v[:, k, :, :])
+
+        def c_quant():
+            nc.vector.quantize_mx(
+                out=ccodes[:].bitcast(E4X4),
+                scales=cscales[:],
+                in_=cgrp[:].rearrange("q c t -> q (c t)"),
+            )
 
         W = GROUP_TILES * I
         N_CHUNKS = B // CHUNK
@@ -96,23 +97,18 @@ def tile_kan_layer_t_kernel(tc, x, spline_coeffs, grad_out, out):
         def prep_s1(g):
             th = prep.tile([P, W], F32, name="th")
             nc.scalar.activation(out=th[:], in_=x_sb[:, g, :, :].rearrange("p t i -> p (t i)"), func=ACT.Tanh)
+            mu = prep.tile([P, W], U32, name="mu")
+            nc.scalar.activation(out=mu[:], in_=th[:], func=ACT.Copy, bias=0.5 * INV_H, scale=0.5 * INV_H)
             uu = prep.tile([P, W], F32, name="uu")
             nc.scalar.activation(out=uu[:], in_=th[:], func=ACT.Copy, bias=INV_H, scale=INV_H)
             wq = keep.tile([P, W], F32, name="wq")
             nc.scalar.activation(out=wq[:], in_=th[:], func=ACT.Square, scale=math.sqrt(INV_H))
-            pre[g] = {"th": th, "uu": uu, "wq": wq}
-
-        def prep_v1(g):
-            mi = prep.tile([P, W], I32, name="mi")
-            nc.vector.tensor_scalar(
-                out=mi[:], in0=pre[g]["th"][:], scalar1=0.5 * INV_H, scalar2=0.5 * INV_H, op0=ALU.mult, op1=ALU.add
-            )
-            pre[g]["mi"] = mi
+            pre[g] = {"th": th, "uu": uu, "wq": wq, "mu": mu}
 
         def prep_v2(g):
             yy = prep.tile([P, W], F32, name="yy")
             nc.vector.scalar_tensor_tensor(
-                out=yy[:], in0=pre[g]["mi"][:], scalar=-2.0, in1=pre[g]["uu"][:], op0=ALU.mult, op1=ALU.add
+                out=yy[:], in0=pre[g]["mu"][:].bitcast(I32), scalar=-2.0, in1=pre[g]["uu"][:], op0=ALU.mult, op1=ALU.add
             )
             pre[g]["yy"] = yy
 
@@ -129,7 +125,7 @@ def tile_kan_layer_t_kernel(tc, x, spline_coeffs, grad_out, out):
         def prep_v4(g):
             xt = prep.tile([P, GROUP_TILES, 3 * I], F32, name="xt")
             nc.vector.scalar_tensor_tensor(
-                out=xt[:, :, 0:I], in0=v3(pre[g]["mi"]), scalar=2.0, in1=v3(pre[g]["zz"]), op0=ALU.mult, op1=ALU.add
+                out=xt[:, :, 0:I], in0=pre[g]["mu"][:].bitcast(I32).rearrange("p (t i) -> p t i", i=I), scalar=2.0, in1=v3(pre[g]["zz"]), op0=ALU.mult, op1=ALU.add
             )
             pre[g]["xt"] = xt
 
@@ -192,9 +188,12 @@ def tile_kan_layer_t_kernel(tc, x, spline_coeffs, grad_out, out):
             chk[n]["t1h"] = t1h
 
         def s_rb(n, c):
-            r_b = ahead.tile([P, CHUNK], F32, name="r_b")
-            nc.scalar.activation(out=r_b[:], in_=chk[n]["t2"][:], func=ACT.Relu, bias=nb[:, c : c + 1], scale=1.0)
-            chk[n]["rb"][c] = r_b
+            if c == 0:
+                r_new = work.tile([P, 4, CHUNK], F32, name="r_b")
+                chk[n]["rb"] = r_new
+            nc.scalar.activation(
+                out=chk[n]["rb"][:, c, :], in_=chk[n]["t2"][:], func=ACT.Relu, bias=nb[:, c : c + 1], scale=1.0
+            )
 
         def pe_mx(n, c):
             gb = ps_m.tile([P, CHUNK], F32, name="gb")
@@ -210,30 +209,39 @@ def tile_kan_layer_t_kernel(tc, x, spline_coeffs, grad_out, out):
             chk[n]["gb"][c] = gb
 
         def v_ca(n, c):
-            c_a = four.tile([P, CHUNK], F32, name="c_a")
+            if c == 0:
+                c_new = work.tile([P, 4, CHUNK], F32, name="c_a")
+                chk[n]["ca"] = c_new
             CLAMP_ENGINE.tensor_scalar(
-                out=c_a[:], in0=chk[n]["t1h"][:], scalar1=c + 2.0, scalar2=1.0 * c, op0=ALU.min, op1=ALU.max
+                out=chk[n]["ca"][:, c, :], in0=chk[n]["t1h"][:], scalar1=c + 2.0, scalar2=1.0 * c,
+                op0=ALU.min, op1=ALU.max,
             )
-            chk[n]["ca"][c] = c_a
 
-        def v_nd(n, c):
-            nd = four.tile([P, CHUNK], F32, name="nd")
+        def v_nd(n):
+            nd = work.tile([P, 4, CHUNK], F32, name="nd")
             nc.vector.scalar_tensor_tensor(
-                out=nd[:], in0=chk[n]["rb"][c][:], scalar=2.0, in1=chk[n]["ca"][c][:], op0=ALU.min, op1=ALU.subtract
+                out=nd[:].rearrange("p c n -> p (c n)"),
+                in0=chk[n]["rb"][:].rearrange("p c n -> p (c n)"),
+                scalar=2.0,
+                in1=chk[n]["ca"][:].rearrange("p c n -> p (c n)"),
+                op0=ALU.min,
+                op1=ALU.subtract,
             )
-            chk[n]["nd"][c] = nd
+            chk[n]["nd"] = nd
 
         def v_pr(n, c):
-            nd = chk[n]["nd"][c]
+            nd = chk[n]["nd"][:, c, :]
             pr = work.tile([P, CHUNK], F32, name="pr%d" % c)
             nc.vector.scalar_tensor_tensor(
-                out=pr[:], in0=nd[:], scalar=1.0 * c, in1=chk[n]["gb"][c][:], op0=ALU.add, op1=ALU.mult
+                out=pr[:], in0=nd, scalar=1.0 * c, in1=chk[n]["gb"][c][:], op0=ALU.add, op1=ALU.mult
             )
             chk[n]["pr"][c] = pr
 
         def v_preadd(n):
             pr = chk[n]["pr"]
-            nc.vector.tensor_add(out=pr[1][:], in0=pr[0][:], in1=pr[1][:])
+            p01 = work.tile([P, CHUNK], F32, name="p01")
+            nc.gpsimd.tensor_tensor(out=p01[:], in0=pr[0][:], in1=pr[1][:], op=ALU.add)
+            pr[1] = p01
 
         def pe_sel(n):
             acc = ps_a.tile([P, CHUNK_TILES, I], F32, name="acc")
@@ -271,19 +279,19 @@ def tile_kan_layer_t_kernel(tc, x, spline_coeffs, grad_out, out):
         CLAMP_ENGINE = nc.vector
         loaded = [0]
 
-        def grp_at(num):
-            if num % 2 == 0 and 0 <= num // 2 < N_GROUPS:
-                return num // 2
-            return -1
+        def groups_at(n, lead, floor_of):
+            return [g for g in range(N_GROUPS) if max(2 * g - lead, floor_of.get(g, -99)) == n]
 
         with tc.manual_schedule():
-            for n in range(-4, N_CHUNKS + 1):
+            for n in range(-6, N_CHUNKS + 1):
                 while loaded[0] < N_GROUPS and 2 * loaded[0] - 7 <= n:
                     load_group(loaded[0])
                     if loaded[0] == 0:
                         nc.sync.dma_start(out=x_sb[:, 2:N_GROUPS, :, :], in_=x_v[:, 2:N_GROUPS, :, :])
                     loaded[0] += 1
-                ga, gb_, gc = grp_at(n + 4), grp_at(n + 3), grp_at(n + 2)
+                first = groups_at(n, 6, {2: -1})
+                second = groups_at(n, 4, {})
+                third = groups_at(n, 3, {})
                 if ok(n + 1):
                     pe_tau(n + 1)
                 if ok(n + 2):
@@ -296,22 +304,18 @@ def tile_kan_layer_t_kernel(tc, x, spline_coeffs, grad_out, out):
                         s_rb(n + 1, c)
                 if ok(n + 2):
                     s_evac(n + 2)
+                if n == -6:
+                    for k in range(4):
+                        c_copy(k)
                 if ok(n):
-                    for c in range(4):
-                        v_ca(n, c)
-                if gb_ >= 0:
-                    prep_v1(gb_)
-                if gc >= 0:
-                    prep_v3(gc)
-                if ok(n):
-                    for c in range(4):
-                        v_nd(n, c)
+                    v_nd(n)
                 if ok(n + 1):
                     v_quant(n + 1)
                 if ok(n):
                     v_pr(n, 0)
                     pe_mx(n, 3)
                     v_pr(n, 1)
+                    v_preadd(n)
                 if ok(n + 1):
                     pe_mx(n + 1, 0)
                 if ok(n):
@@ -322,17 +326,27 @@ def tile_kan_layer_t_kernel(tc, x, spline_coeffs, grad_out, out):
                     v_pr(n, 3)
                 if ok(n + 1):
                     pe_mx(n + 1, 2)
-                if gb_ >= 0:
-                    prep_v2(gb_)
-                    prep_s2(gb_)
-                if gc >= 0:
-                    prep_v4(gc)
-                if ok(n):
-                    v_preadd(n)
+                    v_ca(n + 1, 0)
+                    v_ca(n + 1, 1)
+                for g in second:
+                    prep_v2(g)
+                    prep_s2(g)
+                if n == -4:
+                    for k in range(4, NB):
+                        c_copy(k)
+                for g in third:
+                    prep_v3(g)
+                if n == -3:
+                    c_quant()
+                if ok(n + 1):
+                    v_ca(n + 1, 2)
+                    v_ca(n + 1, 3)
+                for g in third:
+                    prep_v4(g)
                 if ok(n - 1):
                     v_final(n - 1)
-                if gc >= 0:
-                    prep_v5(gc)
-                    prep_s3(gc)
-                if ga >= 0:
-                    prep_s1(ga)
+                for g in third:
+                    prep_v5(g)
+                    prep_s3(g)
+                for g in first:
+                    prep_s1(g)

@@ -31,7 +31,8 @@ def tile_kan_layer_t_kernel(tc, x, spline_coeffs, grad_out, out):
         const = ctx.enter_context(tc.tile_pool(name="const", bufs=1))
         gpool = ctx.enter_context(tc.tile_pool(name="gpool", bufs=4))
         prep = ctx.enter_context(tc.tile_pool(name="prep", bufs=2))
-        keep = ctx.enter_context(tc.tile_pool(name="keep", bufs=4))
+        keep = ctx.enter_context(tc.tile_pool(name="keep", bufs=5))
+        three = ctx.enter_context(tc.tile_pool(name="three", bufs=3))
         work = ctx.enter_context(tc.tile_pool(name="work", bufs=2))
         ps_g = ctx.enter_context(tc.psum_pool(name="ps_g", bufs=2))
         ps_t = ctx.enter_context(tc.psum_pool(name="ps_t", bufs=1))
@@ -51,8 +52,6 @@ def tile_kan_layer_t_kernel(tc, x, spline_coeffs, grad_out, out):
 
         ident = const.tile([P, P], F32)
         make_identity(nc, ident[:])
-        sel = const.tile([P, I], F32)
-        nc.vector.tensor_add(out=sel[:], in0=ident[:, 0:I], in1=ident[:, I : 2 * I])
         nb = const.tile([P, 4], F32)
         nh = const.tile([P, 1], F32)
         for k2 in range(2):
@@ -237,21 +236,32 @@ def tile_kan_layer_t_kernel(tc, x, spline_coeffs, grad_out, out):
             )
             chk[n]["pr"][c] = pr
 
-        def v_preadd(n):
-            pr = chk[n]["pr"]
-            p01 = work.tile([P, CHUNK], F32, name="p01")
-            nc.gpsimd.tensor_tensor(out=p01[:], in0=pr[0][:], in1=pr[1][:], op=ALU.add)
-            pr[1] = p01
-
         def pe_sel(n):
-            acc = ps_a.tile([P, CHUNK_TILES, I], F32, name="acc")
+            acc = ps_a.tile([P, CHUNK_TILES, 2, I], F32, name="acc")
             for a in range(CHUNK_TILES):
-                for j in range(1, 4):
+                for j in range(4):
                     nc.tensor.matmul(
-                        acc[:, a, :], lhsT=chk[n]["pr"][j][:, P * a : P * a + P], rhs=sel[:],
-                        start=(j == 1), stop=(j == 3),
+                        acc[:, a, :, :].rearrange("p h i -> p (h i)"),
+                        lhsT=chk[n]["pr"][j][:, P * a : P * a + P],
+                        rhs=ident[:],
+                        is_transpose=True,
+                        start=(j == 0),
+                        stop=(j == 3),
                     )
             chk[n]["acc"] = acc
+
+        def s_half(n):
+            halves = three.tile([P, CHUNK_TILES, 2, I], F32, name="halves")
+            nc.scalar.copy(
+                out=halves[:].rearrange("p a h i -> p (a h i)"), in_=chk[n]["acc"][:].rearrange("p a h i -> p (a h i)")
+            )
+            chk[n]["halves"] = halves
+
+        def v_pair(n):
+            both = work.tile([P, CHUNK_TILES, I], F32, name="both")
+            halves = chk[n]["halves"]
+            nc.vector.tensor_tensor(out=both[:], in0=halves[:, :, 0, :], in1=halves[:, :, 1, :], op=ALU.add)
+            chk[n]["both"] = both
 
         def v_final(n):
             g, t0 = n // 2, (n % 2) * CHUNK_TILES
@@ -263,7 +273,7 @@ def tile_kan_layer_t_kernel(tc, x, spline_coeffs, grad_out, out):
                 out=o_sb[:, t0 : t0 + CHUNK_TILES, :].rearrange("p a i -> p (a i)"),
                 in0=pre[g]["wq"][:, t0 * I : (t0 + CHUNK_TILES) * I],
                 scalar=INV_H,
-                in1=chk[n]["acc"][:].rearrange("p a i -> p (a i)"),
+                in1=chk[n]["both"][:].rearrange("p a i -> p (a i)"),
                 op0=ALU.subtract,
                 op1=ALU.mult,
             )
@@ -283,7 +293,7 @@ def tile_kan_layer_t_kernel(tc, x, spline_coeffs, grad_out, out):
             return [g for g in range(N_GROUPS) if max(2 * g - lead, floor_of.get(g, -99)) == n]
 
         with tc.manual_schedule():
-            for n in range(-6, N_CHUNKS + 1):
+            for n in range(-6, N_CHUNKS + 2):
                 while loaded[0] < N_GROUPS and 2 * loaded[0] - 7 <= n:
                     load_group(loaded[0])
                     if loaded[0] == 0:
@@ -304,6 +314,8 @@ def tile_kan_layer_t_kernel(tc, x, spline_coeffs, grad_out, out):
                         s_rb(n + 1, c)
                 if ok(n + 2):
                     s_evac(n + 2)
+                if ok(n - 1):
+                    s_half(n - 1)
                 if n == -6:
                     for k in range(4):
                         c_copy(k)
@@ -315,7 +327,6 @@ def tile_kan_layer_t_kernel(tc, x, spline_coeffs, grad_out, out):
                     v_pr(n, 0)
                     pe_mx(n, 3)
                     v_pr(n, 1)
-                    v_preadd(n)
                 if ok(n + 1):
                     pe_mx(n + 1, 0)
                 if ok(n):
@@ -338,13 +349,15 @@ def tile_kan_layer_t_kernel(tc, x, spline_coeffs, grad_out, out):
                     prep_v3(g)
                 if n == -3:
                     c_quant()
+                if ok(n - 2):
+                    v_pair(n - 2)
                 if ok(n + 1):
                     v_ca(n + 1, 2)
                     v_ca(n + 1, 3)
                 for g in third:
                     prep_v4(g)
-                if ok(n - 1):
-                    v_final(n - 1)
+                if ok(n - 2):
+                    v_final(n - 2)
                 for g in third:
                     prep_v5(g)
                     prep_s3(g)

@@ -33,6 +33,7 @@ def tile_kan_layer_t_kernel(tc, x, spline_coeffs, grad_out, out):
         prep = ctx.enter_context(tc.tile_pool(name="prep", bufs=2))
         keep = ctx.enter_context(tc.tile_pool(name="keep", bufs=5))
         three = ctx.enter_context(tc.tile_pool(name="three", bufs=3))
+        one = ctx.enter_context(tc.tile_pool(name="one", bufs=1))
         work = ctx.enter_context(tc.tile_pool(name="work", bufs=2))
         ps_g = ctx.enter_context(tc.psum_pool(name="ps_g", bufs=2))
         ps_t = ctx.enter_context(tc.psum_pool(name="ps_t", bufs=1))
@@ -209,9 +210,10 @@ def tile_kan_layer_t_kernel(tc, x, spline_coeffs, grad_out, out):
 
         def v_ca(n, c):
             if c == 0:
-                c_new = work.tile([P, 4, CHUNK], F32, name="c_a")
+                c_new = one.tile([P, 4, CHUNK], F32, name="c_a")
                 chk[n]["ca"] = c_new
-            CLAMP_ENGINE.tensor_scalar(
+            engine = nc.gpsimd if c < 2 else nc.vector
+            engine.tensor_scalar(
                 out=chk[n]["ca"][:, c, :], in0=chk[n]["t1h"][:], scalar1=c + 2.0, scalar2=1.0 * c,
                 op0=ALU.min, op1=ALU.max,
             )
@@ -286,7 +288,6 @@ def tile_kan_layer_t_kernel(tc, x, spline_coeffs, grad_out, out):
         def ok(n):
             return 0 <= n < N_CHUNKS
 
-        CLAMP_ENGINE = nc.vector
         loaded = [0]
 
         def groups_at(n, lead, floor_of):
@@ -319,10 +320,15 @@ def tile_kan_layer_t_kernel(tc, x, spline_coeffs, grad_out, out):
                 if n == -6:
                     for k in range(4):
                         c_copy(k)
+                if ok(n + 1):
+                    v_quant(n + 1)
                 if ok(n):
                     v_nd(n)
                 if ok(n + 1):
-                    v_quant(n + 1)
+                    v_ca(n + 1, 0)
+                    v_ca(n + 1, 1)
+                if ok(n - 2):
+                    v_pair(n - 2)
                 if ok(n):
                     v_pr(n, 0)
                     pe_mx(n, 3)
@@ -337,8 +343,8 @@ def tile_kan_layer_t_kernel(tc, x, spline_coeffs, grad_out, out):
                     v_pr(n, 3)
                 if ok(n + 1):
                     pe_mx(n + 1, 2)
-                    v_ca(n + 1, 0)
-                    v_ca(n + 1, 1)
+                if ok(n - 2):
+                    v_final(n - 2)
                 for g in second:
                     prep_v2(g)
                     prep_s2(g)
@@ -349,15 +355,12 @@ def tile_kan_layer_t_kernel(tc, x, spline_coeffs, grad_out, out):
                     prep_v3(g)
                 if n == -3:
                     c_quant()
-                if ok(n - 2):
-                    v_pair(n - 2)
                 if ok(n + 1):
                     v_ca(n + 1, 2)
-                    v_ca(n + 1, 3)
                 for g in third:
                     prep_v4(g)
-                if ok(n - 2):
-                    v_final(n - 2)
+                if ok(n + 1):
+                    v_ca(n + 1, 3)
                 for g in third:
                     prep_v5(g)
                     prep_s3(g)

@@ -212,7 +212,7 @@ def tile_kan_layer_t_kernel(tc, x, spline_coeffs, grad_out, out):
             if c == 0:
                 c_new = one.tile([P, 4, CHUNK], F32, name="c_a")
                 chk[n]["ca"] = c_new
-            engine = nc.gpsimd if c < 2 else nc.vector
+            engine = nc.gpsimd if c < 3 else nc.vector
             engine.tensor_scalar(
                 out=chk[n]["ca"][:, c, :], in0=chk[n]["t1h"][:], scalar1=c + 2.0, scalar2=1.0 * c,
                 op0=ALU.min, op1=ALU.max,
@@ -220,14 +220,15 @@ def tile_kan_layer_t_kernel(tc, x, spline_coeffs, grad_out, out):
 
         def v_nd(n):
             nd = work.tile([P, 4, CHUNK], F32, name="nd")
-            nc.vector.scalar_tensor_tensor(
-                out=nd[:].rearrange("p c n -> p (c n)"),
-                in0=chk[n]["rb"][:].rearrange("p c n -> p (c n)"),
-                scalar=2.0,
-                in1=chk[n]["ca"][:].rearrange("p c n -> p (c n)"),
-                op0=ALU.min,
-                op1=ALU.subtract,
-            )
+            for c in (0, 2):
+                nc.vector.scalar_tensor_tensor(
+                    out=nd[:, c : c + 2, :].rearrange("p c n -> p (c n)"),
+                    in0=chk[n]["rb"][:, c : c + 2, :].rearrange("p c n -> p (c n)"),
+                    scalar=2.0,
+                    in1=chk[n]["ca"][:, c : c + 2, :].rearrange("p c n -> p (c n)"),
+                    op0=ALU.min,
+                    op1=ALU.subtract,
+                )
             chk[n]["nd"] = nd
 
         def v_pr(n, c):
@@ -322,13 +323,14 @@ def tile_kan_layer_t_kernel(tc, x, spline_coeffs, grad_out, out):
                         c_copy(k)
                 if ok(n + 1):
                     v_quant(n + 1)
+                if ok(n - 2):
+                    v_pair(n - 2)
                 if ok(n):
                     v_nd(n)
                 if ok(n + 1):
                     v_ca(n + 1, 0)
                     v_ca(n + 1, 1)
-                if ok(n - 2):
-                    v_pair(n - 2)
+                    v_ca(n + 1, 2)
                 if ok(n):
                     v_pr(n, 0)
                     pe_mx(n, 3)
@@ -343,8 +345,6 @@ def tile_kan_layer_t_kernel(tc, x, spline_coeffs, grad_out, out):
                     v_pr(n, 3)
                 if ok(n + 1):
                     pe_mx(n + 1, 2)
-                if ok(n - 2):
-                    v_final(n - 2)
                 for g in second:
                     prep_v2(g)
                     prep_s2(g)
@@ -356,13 +356,13 @@ def tile_kan_layer_t_kernel(tc, x, spline_coeffs, grad_out, out):
                 if n == -3:
                     c_quant()
                 if ok(n + 1):
-                    v_ca(n + 1, 2)
-                for g in third:
-                    prep_v4(g)
-                if ok(n + 1):
                     v_ca(n + 1, 3)
                 for g in third:
-                    prep_v5(g)
+                    prep_v4(g)
                     prep_s3(g)
                 for g in first:
                     prep_s1(g)
+                if ok(n - 2):
+                    v_final(n - 2)
+                for g in third:
+                    prep_v5(g)

@@ -9,20 +9,34 @@ BF16 = mybir.dt.bfloat16
 I32 = mybir.dt.int32
 U32 = mybir.dt.uint32
 U8 = mybir.dt.uint8
-E4X4 = mybir.dt.float8_e4m3fn_x4
-E5X4 = mybir.dt.float8_e5m2_x4
+E4M3_X4 = mybir.dt.float8_e4m3fn_x4
+E5M2_X4 = mybir.dt.float8_e5m2_x4
 ALU = mybir.AluOpType
 ACT = mybir.ActivationFunctionType
 
-B, I, O, NB = 16384, 64, 512, 8
-FLOPS = 2 * B * O * I * NB
+TOKENS, FEATURES, OUT_FEATURES, BASES = 16384, 64, 512, 8
+FLOPS = 2 * TOKENS * OUT_FEATURES * FEATURES * BASES
 P = 128
+PACK = 4
 GROUP_TILES = 8
 GROUP = P * GROUP_TILES
-N_GROUPS = B // GROUP
+N_GROUPS = TOKENS // GROUP
+GROUP_COLS = GROUP_TILES * FEATURES
 CHUNK_TILES = 4
 CHUNK = P * CHUNK_TILES
+N_CHUNKS = TOKENS // CHUNK
+BLOCKS = 4
 INV_H = 5.5
+GPSIMD_CLAMPS = 2
+VECTOR_CLAMPS = 1
+SCALAR_BLOCK = 3
+
+LEAD_LOAD = 7
+LEAD_TANH = 6
+LEAD_WRAP = 4
+LEAD_WARP = 3
+FIRST_ROUND = -LEAD_TANH
+TANH_NOT_BEFORE = {2: -1}
 
 
 def tile_kan_layer_t_kernel(tc, x, spline_coeffs, grad_out, out):
@@ -35,334 +49,358 @@ def tile_kan_layer_t_kernel(tc, x, spline_coeffs, grad_out, out):
         three = ctx.enter_context(tc.tile_pool(name="three", bufs=3))
         one = ctx.enter_context(tc.tile_pool(name="one", bufs=1))
         work = ctx.enter_context(tc.tile_pool(name="work", bufs=2))
-        ps_g = ctx.enter_context(tc.psum_pool(name="ps_g", bufs=2))
-        ps_t = ctx.enter_context(tc.psum_pool(name="ps_t", bufs=1))
-        ps_m = ctx.enter_context(tc.psum_pool(name="ps_m", bufs=3))
-        ps_a = ctx.enter_context(tc.psum_pool(name="ps_a", bufs=1))
+        ps_grad = ctx.enter_context(tc.psum_pool(name="ps_grad", bufs=2))
+        ps_tau = ctx.enter_context(tc.psum_pool(name="ps_tau", bufs=1))
+        ps_gb = ctx.enter_context(tc.psum_pool(name="ps_gb", bufs=3))
+        ps_sum = ctx.enter_context(tc.psum_pool(name="ps_sum", bufs=1))
 
-        x_sb = const.tile([P, N_GROUPS, GROUP_TILES, I], BF16)
-        x_v = x.rearrange("(g p t) i -> p g t i", p=P, t=GROUP_TILES)
-        nc.sync.dma_start(out=x_sb[:, 0:2, :, :], in_=x_v[:, 0:2, :, :])
-        c2d = spline_coeffs.rearrange("o i k -> o (i k)")
-        craw = const.tile([P, 4, O], BF16)
+        x_sb = const.tile([P, N_GROUPS, GROUP_TILES, FEATURES], BF16)
+        x_view = x.rearrange("(g p t) i -> p g t i", p=P, t=GROUP_TILES)
+        nc.sync.dma_start(out=x_sb[:, 0:2, :, :], in_=x_view[:, 0:2, :, :])
+        coeffs = spline_coeffs.rearrange("o i k -> o (i k)")
+        c_rows = const.tile([P, PACK, OUT_FEATURES], BF16)
         for u in range(2):
             nc.sync.dma_start(
-                out=craw[:, 2 * u : 2 * u + 2, :],
-                in_=c2d[256 * u : 256 * u + 256, :].rearrange("(q e) c -> q e c", e=2),
+                out=c_rows[:, 2 * u : 2 * u + 2, :],
+                in_=coeffs[256 * u : 256 * u + 256, :].rearrange("(q e) c -> q e c", e=2),
             )
 
         ident = const.tile([P, P], F32)
         make_identity(nc, ident[:])
-        nb = const.tile([P, 4], F32)
-        nh = const.tile([P, 1], F32)
+        five_half = const.tile([P, 1], F32)
+        nc.vector.memset(five_half[:], INV_H)
+        two = const.tile([P, 1], F32)
+        nc.vector.memset(two[:], 2.0)
+        ramp_bias = const.tile([P, BLOCKS], F32)
+        half_bias = const.tile([P, 1], F32)
+        rise_bias = const.tile([P, 1], F32)
         for k2 in range(2):
             rows = slice(64 * k2, 64 * k2 + 64)
-            nc.vector.memset(nh[rows, :], -0.5 * k2)
-            for c in range(4):
-                nc.vector.memset(nb[rows, c : c + 1], -(2 * c + k2 + 1.0))
+            own_shift = 0.5 * (2.0 * INV_H * k2 - k2)
+            nc.vector.memset(half_bias[rows, :], own_shift)
+            nc.vector.memset(rise_bias[rows, :], own_shift - SCALAR_BLOCK)
+            for c in range(BLOCKS):
+                nc.vector.memset(ramp_bias[rows, c : c + 1], 2.0 * INV_H * (1 - k2) - (2 * c + k2 + 1.0))
 
-        cgrp = const.tile([P, O, 4], BF16, align_bytes=64)
-        cgrp_v = cgrp[:].rearrange("q (k i) t -> q k i t", k=NB)
-        craw_v = craw[:].rearrange("q t (i k) -> q k i t", k=NB)
-        ccodes = const.tile([P, O], U32, align_bytes=64)
-        cscales = const.tile([P, O], U8, align_bytes=64)
+        c_grouped = const.tile([P, OUT_FEATURES, PACK], BF16, align_bytes=64)
+        c_grouped_by_k = c_grouped[:].rearrange("q (k i) t -> q k i t", k=BASES)
+        c_rows_by_k = c_rows[:].rearrange("q t (i k) -> q k i t", k=BASES)
+        c_codes = const.tile([P, OUT_FEATURES], U32, align_bytes=64)
+        c_scales = const.tile([P, OUT_FEATURES], U8, align_bytes=64)
 
-        def c_copy(k):
-            nc.vector.tensor_copy(out=cgrp_v[:, k, :, :], in_=craw_v[:, k, :, :])
+        def regroup_coeffs(k):
+            nc.vector.tensor_copy(out=c_grouped_by_k[:, k, :, :], in_=c_rows_by_k[:, k, :, :])
 
-        def c_quant():
+        def quantise_coeffs():
             nc.vector.quantize_mx(
-                out=ccodes[:].bitcast(E4X4),
-                scales=cscales[:],
-                in_=cgrp[:].rearrange("q c t -> q (c t)"),
+                out=c_codes[:].bitcast(E4M3_X4),
+                scales=c_scales[:],
+                in_=c_grouped[:].rearrange("q c t -> q (c t)"),
             )
 
-        W = GROUP_TILES * I
-        N_CHUNKS = B // CHUNK
-        g_tiles = {}
-        pre = {}
-        chk = {}
+        grad_tiles = {}
+        groups = {}
+        chunks = {}
 
-        def load_group(g):
-            g_sb = gpool.tile([P, GROUP_TILES, O], BF16, name="g_sb")
+        def load_grad(g):
+            grad_sb = gpool.tile([P, GROUP_TILES, OUT_FEATURES], BF16, name="grad_sb")
             nc.sync.dma_start(
-                out=g_sb[:],
+                out=grad_sb[:],
                 in_=grad_out[g * GROUP : (g + 1) * GROUP, :].rearrange("(p t) o -> p t o", t=GROUP_TILES),
             )
-            g_tiles[g] = g_sb
+            grad_tiles[g] = grad_sb
 
-        def v3(t):
-            return t[:].rearrange("p (t i) -> p t i", i=I)
+        def by_tile(ap):
+            return ap.rearrange("p (t i) -> p t i", i=FEATURES)
 
-        def prep_s1(g):
-            th = prep.tile([P, W], F32, name="th")
+        def tanh_step(g):
+            th = prep.tile([P, GROUP_COLS], F32, name="th")
             nc.scalar.activation(out=th[:], in_=x_sb[:, g, :, :].rearrange("p t i -> p (t i)"), func=ACT.Tanh)
-            mu = prep.tile([P, W], U32, name="mu")
-            nc.scalar.activation(out=mu[:], in_=th[:], func=ACT.Copy, bias=0.5 * INV_H, scale=0.5 * INV_H)
-            uu = prep.tile([P, W], F32, name="uu")
-            nc.scalar.activation(out=uu[:], in_=th[:], func=ACT.Copy, bias=INV_H, scale=INV_H)
-            wq = keep.tile([P, W], F32, name="wq")
-            nc.scalar.activation(out=wq[:], in_=th[:], func=ACT.Square, scale=math.sqrt(INV_H))
-            pre[g] = {"th": th, "uu": uu, "wq": wq, "mu": mu}
+            m_int = prep.tile([P, GROUP_COLS], U32, name="m_int")
+            nc.scalar.activation(out=m_int[:], in_=th[:], func=ACT.Copy, bias=0.5 * INV_H, scale=0.5 * INV_H)
+            factor = keep.tile([P, GROUP_COLS], F32, name="factor")
+            nc.scalar.activation(out=factor[:], in_=th[:], func=ACT.Square, scale=math.sqrt(INV_H))
+            groups[g] = {"th": th, "factor": factor, "m_int": m_int}
 
-        def prep_v2(g):
-            yy = prep.tile([P, W], F32, name="yy")
+        def wrap_step(g):
+            y = prep.tile([P, GROUP_COLS], F32, name="y")
             nc.vector.scalar_tensor_tensor(
-                out=yy[:], in0=pre[g]["mu"][:].bitcast(I32), scalar=-2.0, in1=pre[g]["uu"][:], op0=ALU.mult, op1=ALU.add
+                out=y[:], in0=groups[g]["m_int"][:].bitcast(I32), scalar=-2.0 / INV_H, in1=groups[g]["th"][:],
+                op0=ALU.mult, op1=ALU.add,
             )
-            pre[g]["yy"] = yy
+            groups[g]["y"] = y
 
-        def prep_s2(g):
-            ay = prep.tile([P, W], F32, name="ay")
-            nc.scalar.activation(out=ay[:], in_=pre[g]["yy"][:], func=ACT.Abs)
-            pre[g]["ay"] = ay
+        def abs_step(g):
+            abs_y = prep.tile([P, GROUP_COLS], F32, name="abs_y")
+            nc.scalar.activation(out=abs_y[:], in_=groups[g]["y"][:], func=ACT.Abs, bias=five_half[:, 0:1], scale=INV_H)
+            groups[g]["abs_y"] = abs_y
 
-        def prep_v3(g):
-            zz = prep.tile([P, W], F32, name="zz")
-            nc.vector.tensor_tensor(out=zz[:], in0=pre[g]["yy"][:], in1=pre[g]["ay"][:], op=ALU.mult)
-            pre[g]["zz"] = zz
-
-        def prep_v4(g):
-            xt = prep.tile([P, GROUP_TILES, 3 * I], F32, name="xt")
+        def parabola_step(g):
+            y_abs_y = prep.tile([P, GROUP_COLS], F32, name="y_abs_y")
             nc.vector.scalar_tensor_tensor(
-                out=xt[:, :, 0:I], in0=pre[g]["mu"][:].bitcast(I32).rearrange("p (t i) -> p t i", i=I), scalar=2.0, in1=v3(pre[g]["zz"]), op0=ALU.mult, op1=ALU.add
+                out=y_abs_y[:], in0=groups[g]["y"][:], scalar=1.0, in1=groups[g]["abs_y"][:], op0=ALU.add, op1=ALU.mult
             )
-            pre[g]["xt"] = xt
+            groups[g]["y_abs_y"] = y_abs_y
 
-        def prep_v5(g):
-            xt = pre[g]["xt"]
+        def tau_even_step(g):
+            tau = prep.tile([P, GROUP_TILES, 3 * FEATURES], F32, name="tau")
             nc.vector.scalar_tensor_tensor(
-                out=xt[:, :, I : 2 * I], in0=v3(pre[g]["uu"]), scalar=2.0, in1=xt[:, :, 0:I],
-                op0=ALU.mult, op1=ALU.subtract,
+                out=tau[:, :, 0:FEATURES], in0=by_tile(groups[g]["m_int"][:].bitcast(I32)), scalar=2.0 / INV_H,
+                in1=by_tile(groups[g]["y_abs_y"][:]), op0=ALU.mult, op1=ALU.add,
+            )
+            groups[g]["tau"] = tau
+
+        def tau_odd_step(g):
+            tau = groups[g]["tau"]
+            nc.vector.scalar_tensor_tensor(
+                out=tau[:, :, FEATURES : 2 * FEATURES], in0=by_tile(groups[g]["th"][:]), scalar=2.0,
+                in1=tau[:, :, 0:FEATURES], op0=ALU.mult, op1=ALU.subtract,
             )
 
-        def prep_s3(g):
-            xt = pre[g]["xt"]
-            nc.scalar.copy(out=xt[:, :, 2 * I : 3 * I], in_=xt[:, :, 0:I])
+        def tau_copy_step(g):
+            tau = groups[g]["tau"]
+            nc.scalar.copy(out=tau[:, :, 2 * FEATURES : 3 * FEATURES], in_=tau[:, :, 0:FEATURES])
 
-        def pe_grad(n):
-            g, t0 = n // 2, (n % 2) * CHUNK_TILES
-            g_sb = g_tiles[g]
+        def first_tile(n):
+            return n // 2, (n % 2) * CHUNK_TILES
+
+        def transpose_grad(n):
+            g, t0 = first_tile(n)
             banks = []
             for b in range(2):
-                g_t = ps_g.tile([P, 2, 2, P], F32, name="g_t")
+                grad_t = ps_grad.tile([P, 2, 2, P], F32, name="grad_t")
                 for a in range(2):
-                    words = g_sb[:, t0 + 2 * b + a, :].bitcast(F32)
+                    words = grad_tiles[g][:, t0 + 2 * b + a, :].bitcast(F32)
                     for u in range(2):
-                        nc.tensor.transpose(g_t[:, a, u, :], words[:, P * u : P * u + P], ident[:])
-                banks.append(g_t)
-            chk[n] = {"banks": banks, "rb": {}, "gb": {}, "pr": {}, "ca": {}, "nd": {}}
+                        nc.tensor.transpose(grad_t[:, a, u, :], words[:, P * u : P * u + P], ident[:])
+                banks.append(grad_t)
+            chunks[n] = {"grad_t": banks, "gb": {}, "product": {}}
 
-        def pe_tau(n):
-            g, t0 = n // 2, (n % 2) * CHUNK_TILES
-            xt = pre[g]["xt"]
-            t1 = ps_t.tile([P, CHUNK], F32, name="t1")
-            t2 = ps_t.tile([P, CHUNK], F32, name="t2")
+        def transpose_tau(n):
+            g, t0 = first_tile(n)
+            tau = groups[g]["tau"]
+            tau_own = ps_tau.tile([P, CHUNK], F32, name="tau_own")
+            tau_next = ps_tau.tile([P, CHUNK], F32, name="tau_next")
             for a in range(CHUNK_TILES):
-                nc.tensor.transpose(t1[:, P * a : P * a + P], xt[:, t0 + a, 0 : 2 * I], ident[:])
+                nc.tensor.transpose(tau_own[:, P * a : P * a + P], tau[:, t0 + a, 0 : 2 * FEATURES], ident[:])
             for a in range(CHUNK_TILES):
-                nc.tensor.transpose(t2[:, P * a : P * a + P], xt[:, t0 + a, I : 3 * I], ident[:])
-            chk[n]["t1"] = t1
-            chk[n]["t2"] = t2
+                nc.tensor.transpose(
+                    tau_next[:, P * a : P * a + P], tau[:, t0 + a, FEATURES : 3 * FEATURES], ident[:]
+                )
+            chunks[n]["tau_own"] = tau_own
+            chunks[n]["tau_next"] = tau_next
 
-        def s_evac(n):
-            grp = work.tile([P, 4 * CHUNK], BF16, align_bytes=64, name="grp")
-            grp_w = grp[:].bitcast(F32)
+        def group_grad(n):
+            grouped = work.tile([P, PACK * CHUNK], BF16, align_bytes=64, name="grouped")
+            grouped_words = grouped[:].bitcast(F32)
             for b in range(2):
                 nc.scalar.copy(
-                    out=grp_w[:, 512 * b : 512 * b + 512].rearrange("p (a r u) -> p a r u", a=2, u=2),
-                    in_=chk[n]["banks"][b][:].rearrange("p a u r -> p a r u"),
+                    out=grouped_words[:, 512 * b : 512 * b + 512].rearrange("p (a r u) -> p a r u", a=2, u=2),
+                    in_=chunks[n]["grad_t"][b][:].rearrange("p a u r -> p a r u"),
                 )
-            chk[n]["grp"] = grp
+            chunks[n]["grouped"] = grouped
 
-        def v_quant(n):
-            gcodes = work.tile([P, CHUNK], U32, align_bytes=64, name="gcodes")
-            gscales = work.tile([P, CHUNK], U8, align_bytes=64, name="gscales")
-            nc.vector.quantize_mx(out=gcodes[:].bitcast(E5X4), scales=gscales[:], in_=chk[n]["grp"][:])
-            chk[n]["gcodes"] = gcodes
-            chk[n]["gscales"] = gscales
+        def quantise_grad(n):
+            g_codes = work.tile([P, CHUNK], U32, align_bytes=64, name="g_codes")
+            g_scales = work.tile([P, CHUNK], U8, align_bytes=64, name="g_scales")
+            nc.vector.quantize_mx(out=g_codes[:].bitcast(E5M2_X4), scales=g_scales[:], in_=chunks[n]["grouped"][:])
+            chunks[n]["g_codes"] = g_codes
+            chunks[n]["g_scales"] = g_scales
 
-        def s_t1h(n):
-            t1h = work.tile([P, CHUNK], F32, name="t1h")
-            nc.scalar.activation(out=t1h[:], in_=chk[n]["t1"][:], func=ACT.Identity, bias=nh[:, 0:1], scale=0.5)
-            chk[n]["t1h"] = t1h
-
-        def s_rb(n, c):
-            if c == 0:
-                r_new = work.tile([P, 4, CHUNK], F32, name="r_b")
-                chk[n]["rb"] = r_new
+        def halve_tau(n):
+            half_tau = work.tile([P, CHUNK], F32, name="half_tau")
             nc.scalar.activation(
-                out=chk[n]["rb"][:, c, :], in_=chk[n]["t2"][:], func=ACT.Relu, bias=nb[:, c : c + 1], scale=1.0
+                out=half_tau[:], in_=chunks[n]["tau_own"][:], func=ACT.Identity, bias=half_bias[:, 0:1], scale=0.5 * INV_H
+            )
+            chunks[n]["half_tau"] = half_tau
+
+        def rise_first(n):
+            rise = work.tile([P, CHUNK], F32, name="rise")
+            nc.scalar.activation(
+                out=rise[:], in_=chunks[n]["tau_own"][:], func=ACT.Relu, bias=rise_bias[:, 0:1], scale=0.5 * INV_H
+            )
+            chunks[n]["rise"] = rise
+
+        def rest_first(n):
+            rest = work.tile([P, CHUNK], F32, name="rest")
+            nc.scalar.activation(out=rest[:], in_=chunks[n]["rise"][:], func=ACT.Relu, bias=two[:, 0:1], scale=-1.0)
+            chunks[n]["rest"] = rest
+
+        def ramp_second(n, c):
+            if c == 0:
+                ramp = work.tile([P, BLOCKS, CHUNK], F32, name="ramp")
+                chunks[n]["ramp"] = ramp
+            nc.scalar.activation(
+                out=chunks[n]["ramp"][:, c, :], in_=chunks[n]["tau_next"][:], func=ACT.Relu,
+                bias=ramp_bias[:, c : c + 1], scale=INV_H,
             )
 
-        def pe_mx(n, c):
-            gb = ps_m.tile([P, CHUNK], F32, name="gb")
+        def multiply_mx(n, c):
+            gb = ps_gb.tile([P, CHUNK], F32, name="gb")
             nc.tensor.matmul_mx(
                 out=gb[:],
-                lhsT=ccodes[:, P * c : P * c + P].bitcast(E4X4),
-                lhsT_scale=cscales[:, P * c : P * c + P],
-                rhs=chk[n]["gcodes"][:].bitcast(E5X4),
-                rhs_scale=chk[n]["gscales"][:],
+                lhsT=c_codes[:, P * c : P * c + P].bitcast(E4M3_X4),
+                lhsT_scale=c_scales[:, P * c : P * c + P],
+                rhs=chunks[n]["g_codes"][:].bitcast(E5M2_X4),
+                rhs_scale=chunks[n]["g_scales"][:],
                 start=True,
                 stop=True,
             )
-            chk[n]["gb"][c] = gb
+            chunks[n]["gb"][c] = gb
 
-        def v_ca(n, c):
+        def clamp_first(n, c):
             if c == 0:
-                c_new = one.tile([P, 4, CHUNK], F32, name="c_a")
-                chk[n]["ca"] = c_new
-            engine = nc.gpsimd if c < 3 else nc.vector
+                clamped = one.tile([P, SCALAR_BLOCK, CHUNK], F32, name="clamped")
+                chunks[n]["clamped"] = clamped
+            engine = nc.gpsimd if c < GPSIMD_CLAMPS else nc.vector
             engine.tensor_scalar(
-                out=chk[n]["ca"][:, c, :], in0=chk[n]["t1h"][:], scalar1=c + 2.0, scalar2=1.0 * c,
+                out=chunks[n]["clamped"][:, c, :], in0=chunks[n]["half_tau"][:], scalar1=c + 2.0, scalar2=1.0 * c,
                 op0=ALU.min, op1=ALU.max,
             )
 
-        def v_nd(n):
-            nd = work.tile([P, 4, CHUNK], F32, name="nd")
-            for c in (0, 2):
-                nc.vector.scalar_tensor_tensor(
-                    out=nd[:, c : c + 2, :].rearrange("p c n -> p (c n)"),
-                    in0=chk[n]["rb"][:, c : c + 2, :].rearrange("p c n -> p (c n)"),
-                    scalar=2.0,
-                    in1=chk[n]["ca"][:, c : c + 2, :].rearrange("p c n -> p (c n)"),
-                    op0=ALU.min,
-                    op1=ALU.subtract,
-                )
-            chk[n]["nd"] = nd
-
-        def v_pr(n, c):
-            nd = chk[n]["nd"][:, c, :]
-            pr = work.tile([P, CHUNK], F32, name="pr%d" % c)
+        def difference(n):
+            nd = work.tile([P, BLOCKS, CHUNK], F32, name="nd")
             nc.vector.scalar_tensor_tensor(
-                out=pr[:], in0=nd, scalar=1.0 * c, in1=chk[n]["gb"][c][:], op0=ALU.add, op1=ALU.mult
+                out=nd[:, 0:SCALAR_BLOCK, :].rearrange("p c n -> p (c n)"),
+                in0=chunks[n]["ramp"][:, 0:SCALAR_BLOCK, :].rearrange("p c n -> p (c n)"),
+                scalar=2.0,
+                in1=chunks[n]["clamped"][:].rearrange("p c n -> p (c n)"),
+                op0=ALU.min,
+                op1=ALU.subtract,
             )
-            chk[n]["pr"][c] = pr
+            nc.vector.scalar_tensor_tensor(
+                out=nd[:, SCALAR_BLOCK, :], in0=chunks[n]["ramp"][:, SCALAR_BLOCK, :], scalar=2.0,
+                in1=chunks[n]["rest"][:], op0=ALU.min, op1=ALU.add,
+            )
+            chunks[n]["nd"] = nd
 
-        def pe_sel(n):
-            acc = ps_a.tile([P, CHUNK_TILES, 2, I], F32, name="acc")
+        def product(n, c):
+            prod = work.tile([P, CHUNK], F32, name="prod%d" % c)
+            nc.vector.scalar_tensor_tensor(
+                out=prod[:], in0=chunks[n]["nd"][:, c, :], scalar=(-2.0 if c == SCALAR_BLOCK else 1.0 * c),
+                in1=chunks[n]["gb"][c][:],
+                op0=ALU.add, op1=ALU.mult,
+            )
+            chunks[n]["product"][c] = prod
+
+        def sum_blocks(n):
+            sums = ps_sum.tile([P, CHUNK_TILES, 2, FEATURES], F32, name="sums")
             for a in range(CHUNK_TILES):
-                for j in range(4):
+                for c in range(BLOCKS):
                     nc.tensor.matmul(
-                        acc[:, a, :, :].rearrange("p h i -> p (h i)"),
-                        lhsT=chk[n]["pr"][j][:, P * a : P * a + P],
+                        sums[:, a, :, :].rearrange("p h i -> p (h i)"),
+                        lhsT=chunks[n]["product"][c][:, P * a : P * a + P],
                         rhs=ident[:],
                         is_transpose=True,
-                        start=(j == 0),
-                        stop=(j == 3),
+                        start=(c == 0),
+                        stop=(c == BLOCKS - 1),
                     )
-            chk[n]["acc"] = acc
+            chunks[n]["sums"] = sums
 
-        def s_half(n):
-            halves = three.tile([P, CHUNK_TILES, 2, I], F32, name="halves")
+        def empty_sums(n):
+            halves = three.tile([P, CHUNK_TILES, 2, FEATURES], F32, name="halves")
             nc.scalar.copy(
-                out=halves[:].rearrange("p a h i -> p (a h i)"), in_=chk[n]["acc"][:].rearrange("p a h i -> p (a h i)")
+                out=halves[:].rearrange("p a h i -> p (a h i)"),
+                in_=chunks[n]["sums"][:].rearrange("p a h i -> p (a h i)"),
             )
-            chk[n]["halves"] = halves
+            chunks[n]["halves"] = halves
 
-        def v_pair(n):
-            both = work.tile([P, CHUNK_TILES, I], F32, name="both")
-            halves = chk[n]["halves"]
-            nc.vector.tensor_tensor(out=both[:], in0=halves[:, :, 0, :], in1=halves[:, :, 1, :], op=ALU.add)
-            chk[n]["both"] = both
+        def join_halves(n):
+            joined = work.tile([P, CHUNK_TILES, FEATURES], F32, name="joined")
+            halves = chunks[n]["halves"]
+            nc.vector.tensor_tensor(out=joined[:], in0=halves[:, :, 0, :], in1=halves[:, :, 1, :], op=ALU.add)
+            chunks[n]["joined"] = joined
 
-        def v_final(n):
-            g, t0 = n // 2, (n % 2) * CHUNK_TILES
+        def finish(n):
+            g, t0 = first_tile(n)
             if t0 == 0:
-                o_new = work.tile([P, GROUP_TILES, I], F32, name="o_sb")
-                pre[g]["o_sb"] = o_new
-            o_sb = pre[g]["o_sb"]
+                result = work.tile([P, GROUP_TILES, FEATURES], F32, name="result")
+                groups[g]["result"] = result
+            result = groups[g]["result"]
             nc.vector.scalar_tensor_tensor(
-                out=o_sb[:, t0 : t0 + CHUNK_TILES, :].rearrange("p a i -> p (a i)"),
-                in0=pre[g]["wq"][:, t0 * I : (t0 + CHUNK_TILES) * I],
+                out=result[:, t0 : t0 + CHUNK_TILES, :].rearrange("p a i -> p (a i)"),
+                in0=groups[g]["factor"][:, t0 * FEATURES : (t0 + CHUNK_TILES) * FEATURES],
                 scalar=INV_H,
-                in1=chk[n]["both"][:].rearrange("p a i -> p (a i)"),
+                in1=chunks[n]["joined"][:].rearrange("p a i -> p (a i)"),
                 op0=ALU.subtract,
                 op1=ALU.mult,
             )
             if t0 != 0:
                 nc.sync.dma_start(
                     out=out[g * GROUP : (g + 1) * GROUP, :].rearrange("(p t) i -> p t i", t=GROUP_TILES),
-                    in_=o_sb[:],
+                    in_=result[:],
                 )
 
-        def ok(n):
+        def is_chunk(n):
             return 0 <= n < N_CHUNKS
 
-        loaded = [0]
-
-        def groups_at(n, lead, floor_of):
-            return [g for g in range(N_GROUPS) if max(2 * g - lead, floor_of.get(g, -99)) == n]
+        def groups_in_round(n, lead, not_before):
+            return [g for g in range(N_GROUPS) if max(2 * g - lead, not_before.get(g, FIRST_ROUND)) == n]
 
         with tc.manual_schedule():
-            for n in range(-6, N_CHUNKS + 2):
-                while loaded[0] < N_GROUPS and 2 * loaded[0] - 7 <= n:
-                    load_group(loaded[0])
-                    if loaded[0] == 0:
-                        nc.sync.dma_start(out=x_sb[:, 2:N_GROUPS, :, :], in_=x_v[:, 2:N_GROUPS, :, :])
-                    loaded[0] += 1
-                first = groups_at(n, 6, {2: -1})
-                second = groups_at(n, 4, {})
-                third = groups_at(n, 3, {})
-                if ok(n + 1):
-                    pe_tau(n + 1)
-                if ok(n + 2):
-                    pe_grad(n + 2)
-                if ok(n - 1):
-                    pe_sel(n - 1)
-                if ok(n + 1):
-                    s_t1h(n + 1)
-                    for c in range(4):
-                        s_rb(n + 1, c)
-                if ok(n + 2):
-                    s_evac(n + 2)
-                if ok(n - 1):
-                    s_half(n - 1)
-                if n == -6:
-                    for k in range(4):
-                        c_copy(k)
-                if ok(n + 1):
-                    v_quant(n + 1)
-                if ok(n - 2):
-                    v_pair(n - 2)
-                if ok(n):
-                    v_nd(n)
-                if ok(n + 1):
-                    v_ca(n + 1, 0)
-                    v_ca(n + 1, 1)
-                    v_ca(n + 1, 2)
-                if ok(n):
-                    v_pr(n, 0)
-                    pe_mx(n, 3)
-                    v_pr(n, 1)
-                if ok(n + 1):
-                    pe_mx(n + 1, 0)
-                if ok(n):
-                    v_pr(n, 2)
-                if ok(n + 1):
-                    pe_mx(n + 1, 1)
-                if ok(n):
-                    v_pr(n, 3)
-                if ok(n + 1):
-                    pe_mx(n + 1, 2)
-                for g in second:
-                    prep_v2(g)
-                    prep_s2(g)
-                if n == -4:
-                    for k in range(4, NB):
-                        c_copy(k)
-                for g in third:
-                    prep_v3(g)
-                if n == -3:
-                    c_quant()
-                if ok(n + 1):
-                    v_ca(n + 1, 3)
-                for g in third:
-                    prep_v4(g)
-                    prep_s3(g)
-                for g in first:
-                    prep_s1(g)
-                if ok(n - 2):
-                    v_final(n - 2)
-                for g in third:
-                    prep_v5(g)
+            for n in range(FIRST_ROUND, N_CHUNKS + 2):
+                for g in groups_in_round(n, LEAD_LOAD, {}):
+                    load_grad(g)
+                    if g == 0:
+                        nc.sync.dma_start(out=x_sb[:, 2:N_GROUPS, :, :], in_=x_view[:, 2:N_GROUPS, :, :])
+                tanh_groups = groups_in_round(n, LEAD_TANH, TANH_NOT_BEFORE)
+                wrap_groups = groups_in_round(n, LEAD_WRAP, {})
+                warp_groups = groups_in_round(n, LEAD_WARP, {})
+
+                if is_chunk(n + 1):
+                    transpose_tau(n + 1)
+                if is_chunk(n + 2):
+                    transpose_grad(n + 2)
+                if is_chunk(n - 1):
+                    sum_blocks(n - 1)
+
+                if is_chunk(n + 1):
+                    halve_tau(n + 1)
+                    rise_first(n + 1)
+                    for c in range(BLOCKS):
+                        ramp_second(n + 1, c)
+                    rest_first(n + 1)
+                if is_chunk(n + 2):
+                    group_grad(n + 2)
+                if is_chunk(n - 1):
+                    empty_sums(n - 1)
+
+                if n == FIRST_ROUND:
+                    for k in range(BASES // 2):
+                        regroup_coeffs(k)
+                if is_chunk(n + 1):
+                    quantise_grad(n + 1)
+                if is_chunk(n):
+                    difference(n)
+                if is_chunk(n + 1):
+                    for c in range(GPSIMD_CLAMPS):
+                        clamp_first(n + 1, c)
+                if is_chunk(n - 2):
+                    join_halves(n - 2)
+                for c in range(BLOCKS):
+                    if is_chunk(n):
+                        product(n, c)
+                    ahead, block = (n, BLOCKS - 1) if c == 0 else (n + 1, c - 1)
+                    if is_chunk(ahead):
+                        multiply_mx(ahead, block)
+                for g in wrap_groups:
+                    wrap_step(g)
+                    abs_step(g)
+                if n == -LEAD_WRAP:
+                    for k in range(BASES // 2, BASES):
+                        regroup_coeffs(k)
+                for g in warp_groups:
+                    parabola_step(g)
+                if n == -LEAD_WARP:
+                    quantise_coeffs()
+                if is_chunk(n + 1):
+                    clamp_first(n + 1, GPSIMD_CLAMPS)
+                for g in warp_groups:
+                    tau_even_step(g)
+                if is_chunk(n - 2):
+                    finish(n - 2)
+                for g in warp_groups:
+                    tau_odd_step(g)
+                    tau_copy_step(g)
+                for g in tanh_groups:
+                    tanh_step(g)

@@ -25,11 +25,32 @@ GROUP_COLS = GROUP_TILES * FEATURES
 CHUNK_TILES = 4
 CHUNK = P * CHUNK_TILES
 N_CHUNKS = TOKENS // CHUNK
-BLOCKS = 4
 INV_H = 5.5
-GPSIMD_CLAMPS = 2
-VECTOR_CLAMPS = 1
-SCALAR_BLOCK = 3
+KNOTS_SPAN = 11.0
+
+N_UNITS = 2 * BASES + 1
+
+
+def unit_n(k):
+    return BASES - 1 - k
+
+
+def unit_c(k):
+    return 2 * BASES - 1 - k
+
+
+def make_blocks():
+    return (
+        (4, 3, 2.0, (unit_c(4), unit_n(3), unit_c(2))),
+        (6, 5, 2.0, (unit_c(6), unit_n(5), unit_c(4))),
+        (2, 1, 2.0, (unit_c(2), unit_n(1))),
+        (8, 7, 2.0, (unit_n(7), unit_c(6))),
+        (0, 7, 4.0, (unit_c(0),)),
+    )
+
+
+N_BLOCKS = 5
+W_BANKS = 4
 
 LEAD_LOAD = 7
 LEAD_TANH = 6
@@ -41,17 +62,17 @@ TANH_NOT_BEFORE = {2: -1}
 
 def tile_kan_layer_t_kernel(tc, x, spline_coeffs, grad_out, out):
     nc = tc.nc
+    BLOCKS = make_blocks()
     with ExitStack() as ctx:
         const = ctx.enter_context(tc.tile_pool(name="const", bufs=1))
         gpool = ctx.enter_context(tc.tile_pool(name="gpool", bufs=4))
         prep = ctx.enter_context(tc.tile_pool(name="prep", bufs=2))
         keep = ctx.enter_context(tc.tile_pool(name="keep", bufs=5))
         three = ctx.enter_context(tc.tile_pool(name="three", bufs=3))
-        one = ctx.enter_context(tc.tile_pool(name="one", bufs=1))
         work = ctx.enter_context(tc.tile_pool(name="work", bufs=2))
         ps_grad = ctx.enter_context(tc.psum_pool(name="ps_grad", bufs=2))
         ps_tau = ctx.enter_context(tc.psum_pool(name="ps_tau", bufs=1))
-        ps_gb = ctx.enter_context(tc.psum_pool(name="ps_gb", bufs=3))
+        ps_w = ctx.enter_context(tc.psum_pool(name="ps_w", bufs=W_BANKS))
         ps_sum = ctx.enter_context(tc.psum_pool(name="ps_sum", bufs=1))
 
         x_sb = const.tile([P, N_GROUPS, GROUP_TILES, FEATURES], BF16)
@@ -67,36 +88,40 @@ def tile_kan_layer_t_kernel(tc, x, spline_coeffs, grad_out, out):
 
         ident = const.tile([P, P], F32)
         make_identity(nc, ident[:])
-        five_half = const.tile([P, 1], F32)
-        nc.vector.memset(five_half[:], INV_H)
-        two = const.tile([P, 1], F32)
-        nc.vector.memset(two[:], 2.0)
-        ramp_bias = const.tile([P, BLOCKS], F32)
-        half_bias = const.tile([P, 1], F32)
-        rise_bias = const.tile([P, 1], F32)
-        for k2 in range(2):
-            rows = slice(64 * k2, 64 * k2 + 64)
-            own_shift = 0.5 * (2.0 * INV_H * k2 - k2)
-            nc.vector.memset(half_bias[rows, :], own_shift)
-            nc.vector.memset(rise_bias[rows, :], own_shift - SCALAR_BLOCK)
-            for c in range(BLOCKS):
-                nc.vector.memset(ramp_bias[rows, c : c + 1], 2.0 * INV_H * (1 - k2) - (2 * c + k2 + 1.0))
+        half_span = const.tile([P, 1], F32)
+        nc.vector.memset(half_span[:], 0.5 * INV_H)
+        ramp_bias = const.tile([P, N_BLOCKS], F32)
+        for b, (even_knot, odd_knot, width, units) in enumerate(BLOCKS):
+            nc.vector.memset(ramp_bias[0:64, b : b + 1], -1.0 * even_knot)
+            nc.vector.memset(ramp_bias[64:128, b : b + 1], KNOTS_SPAN - odd_knot)
 
-        c_grouped = const.tile([P, OUT_FEATURES, PACK], BF16, align_bytes=64)
-        c_grouped_by_k = c_grouped[:].rearrange("q (k i) t -> q k i t", k=BASES)
+        c_grouped = const.tile([P, N_UNITS * FEATURES * PACK], BF16, align_bytes=64)
+        c_grouped_by_unit = c_grouped[:].rearrange("q (s i t) -> q s i t", s=N_UNITS, t=PACK)
         c_rows_by_k = c_rows[:].rearrange("q t (i k) -> q k i t", k=BASES)
-        c_codes = const.tile([P, OUT_FEATURES], U32, align_bytes=64)
-        c_scales = const.tile([P, OUT_FEATURES], U8, align_bytes=64)
+        c_codes = const.tile([P, N_UNITS * FEATURES], U32, align_bytes=64)
+        c_scales = const.tile([P, N_UNITS * FEATURES], U8, align_bytes=64)
+        UNIT_IN = FEATURES * PACK
 
         def regroup_coeffs(k):
-            nc.vector.tensor_copy(out=c_grouped_by_k[:, k, :, :], in_=c_rows_by_k[:, k, :, :])
+            nc.vector.tensor_copy(out=c_grouped_by_unit[:, unit_c(k), :, :], in_=c_rows_by_k[:, k, :, :])
+
+        def scale_coeffs():
+            nc.vector.tensor_scalar(
+                out=c_grouped[:, 0 : BASES * UNIT_IN], in0=c_grouped[:, BASES * UNIT_IN : 2 * BASES * UNIT_IN],
+                scalar1=-2.0, scalar2=None, op0=ALU.mult,
+            )
+            nc.vector.tensor_copy(
+                out=c_grouped[:, 2 * BASES * UNIT_IN : N_UNITS * UNIT_IN],
+                in_=c_grouped[:, unit_c(BASES - 1) * UNIT_IN : (unit_c(BASES - 1) + 1) * UNIT_IN],
+            )
 
         def quantise_coeffs():
-            nc.vector.quantize_mx(
-                out=c_codes[:].bitcast(E4M3_X4),
-                scales=c_scales[:],
-                in_=c_grouped[:].rearrange("q c t -> q (c t)"),
-            )
+            for first, last in ((0, 2 * BASES), (2 * BASES, N_UNITS)):
+                nc.vector.quantize_mx(
+                    out=c_codes[:, first * FEATURES : last * FEATURES].bitcast(E4M3_X4),
+                    scales=c_scales[:, first * FEATURES : last * FEATURES],
+                    in_=c_grouped[:, first * UNIT_IN : last * UNIT_IN],
+                )
 
         grad_tiles = {}
         groups = {}
@@ -119,7 +144,7 @@ def tile_kan_layer_t_kernel(tc, x, spline_coeffs, grad_out, out):
             m_int = prep.tile([P, GROUP_COLS], U32, name="m_int")
             nc.scalar.activation(out=m_int[:], in_=th[:], func=ACT.Copy, bias=0.5 * INV_H, scale=0.5 * INV_H)
             factor = keep.tile([P, GROUP_COLS], F32, name="factor")
-            nc.scalar.activation(out=factor[:], in_=th[:], func=ACT.Square, scale=math.sqrt(INV_H))
+            nc.scalar.activation(out=factor[:], in_=th[:], func=ACT.Square, scale=math.sqrt(0.5 * INV_H))
             groups[g] = {"th": th, "factor": factor, "m_int": m_int}
 
         def wrap_step(g):
@@ -132,7 +157,9 @@ def tile_kan_layer_t_kernel(tc, x, spline_coeffs, grad_out, out):
 
         def abs_step(g):
             abs_y = prep.tile([P, GROUP_COLS], F32, name="abs_y")
-            nc.scalar.activation(out=abs_y[:], in_=groups[g]["y"][:], func=ACT.Abs, bias=five_half[:, 0:1], scale=INV_H)
+            nc.scalar.activation(
+                out=abs_y[:], in_=groups[g]["y"][:], func=ACT.Abs, bias=half_span[:, 0:1], scale=0.5 * INV_H
+            )
             groups[g]["abs_y"] = abs_y
 
         def parabola_step(g):
@@ -143,23 +170,19 @@ def tile_kan_layer_t_kernel(tc, x, spline_coeffs, grad_out, out):
             groups[g]["y_abs_y"] = y_abs_y
 
         def tau_even_step(g):
-            tau = prep.tile([P, GROUP_TILES, 3 * FEATURES], F32, name="tau")
+            tau = prep.tile([P, GROUP_TILES, 2 * FEATURES], F32, name="tau")
             nc.vector.scalar_tensor_tensor(
-                out=tau[:, :, 0:FEATURES], in0=by_tile(groups[g]["m_int"][:].bitcast(I32)), scalar=2.0 / INV_H,
+                out=tau[:, :, 0:FEATURES], in0=by_tile(groups[g]["m_int"][:].bitcast(I32)), scalar=2.0 / KNOTS_SPAN,
                 in1=by_tile(groups[g]["y_abs_y"][:]), op0=ALU.mult, op1=ALU.add,
             )
             groups[g]["tau"] = tau
 
         def tau_odd_step(g):
             tau = groups[g]["tau"]
-            nc.vector.scalar_tensor_tensor(
-                out=tau[:, :, FEATURES : 2 * FEATURES], in0=by_tile(groups[g]["th"][:]), scalar=2.0,
-                in1=tau[:, :, 0:FEATURES], op0=ALU.mult, op1=ALU.subtract,
+            nc.vector.tensor_tensor(
+                out=tau[:, :, FEATURES : 2 * FEATURES], in0=by_tile(groups[g]["th"][:]), in1=tau[:, :, 0:FEATURES],
+                op=ALU.subtract,
             )
-
-        def tau_copy_step(g):
-            tau = groups[g]["tau"]
-            nc.scalar.copy(out=tau[:, :, 2 * FEATURES : 3 * FEATURES], in_=tau[:, :, 0:FEATURES])
 
         def first_tile(n):
             return n // 2, (n % 2) * CHUNK_TILES
@@ -174,21 +197,15 @@ def tile_kan_layer_t_kernel(tc, x, spline_coeffs, grad_out, out):
                     for u in range(2):
                         nc.tensor.transpose(grad_t[:, a, u, :], words[:, P * u : P * u + P], ident[:])
                 banks.append(grad_t)
-            chunks[n] = {"grad_t": banks, "gb": {}, "product": {}}
+            chunks[n] = {"grad_t": banks, "w": {}, "product": {}}
 
         def transpose_tau(n):
             g, t0 = first_tile(n)
             tau = groups[g]["tau"]
-            tau_own = ps_tau.tile([P, CHUNK], F32, name="tau_own")
-            tau_next = ps_tau.tile([P, CHUNK], F32, name="tau_next")
+            tau_t = ps_tau.tile([P, CHUNK], F32, name="tau_t")
             for a in range(CHUNK_TILES):
-                nc.tensor.transpose(tau_own[:, P * a : P * a + P], tau[:, t0 + a, 0 : 2 * FEATURES], ident[:])
-            for a in range(CHUNK_TILES):
-                nc.tensor.transpose(
-                    tau_next[:, P * a : P * a + P], tau[:, t0 + a, FEATURES : 3 * FEATURES], ident[:]
-                )
-            chunks[n]["tau_own"] = tau_own
-            chunks[n]["tau_next"] = tau_next
+                nc.tensor.transpose(tau_t[:, P * a : P * a + P], tau[:, t0 + a, :], ident[:])
+            chunks[n]["tau_t"] = tau_t
 
         def group_grad(n):
             grouped = work.tile([P, PACK * CHUNK], BF16, align_bytes=64, name="grouped")
@@ -207,101 +224,60 @@ def tile_kan_layer_t_kernel(tc, x, spline_coeffs, grad_out, out):
             chunks[n]["g_codes"] = g_codes
             chunks[n]["g_scales"] = g_scales
 
-        def halve_tau(n):
-            half_tau = work.tile([P, CHUNK], F32, name="half_tau")
-            nc.scalar.activation(
-                out=half_tau[:], in_=chunks[n]["tau_own"][:], func=ACT.Identity, bias=half_bias[:, 0:1], scale=0.5 * INV_H
-            )
-            chunks[n]["half_tau"] = half_tau
-
-        def rise_first(n):
-            rise = work.tile([P, CHUNK], F32, name="rise")
-            nc.scalar.activation(
-                out=rise[:], in_=chunks[n]["tau_own"][:], func=ACT.Relu, bias=rise_bias[:, 0:1], scale=0.5 * INV_H
-            )
-            chunks[n]["rise"] = rise
-
-        def rest_first(n):
-            rest = work.tile([P, CHUNK], F32, name="rest")
-            nc.scalar.activation(out=rest[:], in_=chunks[n]["rise"][:], func=ACT.Relu, bias=two[:, 0:1], scale=-1.0)
-            chunks[n]["rest"] = rest
-
-        def ramp_second(n, c):
-            if c == 0:
-                ramp = work.tile([P, BLOCKS, CHUNK], F32, name="ramp")
+        def ramp_up(n, b):
+            if b == 0:
+                ramp = work.tile([P, N_BLOCKS, CHUNK], F32, name="ramp")
                 chunks[n]["ramp"] = ramp
             nc.scalar.activation(
-                out=chunks[n]["ramp"][:, c, :], in_=chunks[n]["tau_next"][:], func=ACT.Relu,
-                bias=ramp_bias[:, c : c + 1], scale=INV_H,
+                out=chunks[n]["ramp"][:, b, :], in_=chunks[n]["tau_t"][:], func=ACT.Relu,
+                bias=ramp_bias[:, b : b + 1], scale=KNOTS_SPAN,
             )
 
-        def multiply_mx(n, c):
-            gb = ps_gb.tile([P, CHUNK], F32, name="gb")
-            nc.tensor.matmul_mx(
-                out=gb[:],
-                lhsT=c_codes[:, P * c : P * c + P].bitcast(E4M3_X4),
-                lhsT_scale=c_scales[:, P * c : P * c + P],
-                rhs=chunks[n]["g_codes"][:].bitcast(E5M2_X4),
-                rhs_scale=chunks[n]["g_scales"][:],
-                start=True,
-                stop=True,
-            )
-            chunks[n]["gb"][c] = gb
+        def multiply_mx(n, b):
+            w = ps_w.tile([P, CHUNK], F32, name="w")
+            units = BLOCKS[b][3]
+            for s, unit in enumerate(units):
+                first = unit * FEATURES
+                nc.tensor.matmul_mx(
+                    out=w[:],
+                    lhsT=c_codes[:, first : first + P].bitcast(E4M3_X4),
+                    lhsT_scale=c_scales[:, first : first + P],
+                    rhs=chunks[n]["g_codes"][:].bitcast(E5M2_X4),
+                    rhs_scale=chunks[n]["g_scales"][:],
+                    start=(s == 0),
+                    stop=(s == len(units) - 1),
+                )
+            chunks[n]["w"][b] = w
 
-        def clamp_first(n, c):
-            if c == 0:
-                clamped = one.tile([P, SCALAR_BLOCK, CHUNK], F32, name="clamped")
-                chunks[n]["clamped"] = clamped
-            engine = nc.gpsimd if c < GPSIMD_CLAMPS else nc.vector
-            engine.tensor_scalar(
-                out=chunks[n]["clamped"][:, c, :], in0=chunks[n]["half_tau"][:], scalar1=c + 2.0, scalar2=1.0 * c,
-                op0=ALU.min, op1=ALU.max,
-            )
-
-        def difference(n):
-            nd = work.tile([P, BLOCKS, CHUNK], F32, name="nd")
+        def product(n, b):
+            prod = work.tile([P, CHUNK], F32, name="prod%d" % b)
             nc.vector.scalar_tensor_tensor(
-                out=nd[:, 0:SCALAR_BLOCK, :].rearrange("p c n -> p (c n)"),
-                in0=chunks[n]["ramp"][:, 0:SCALAR_BLOCK, :].rearrange("p c n -> p (c n)"),
-                scalar=2.0,
-                in1=chunks[n]["clamped"][:].rearrange("p c n -> p (c n)"),
-                op0=ALU.min,
-                op1=ALU.subtract,
+                out=prod[:], in0=chunks[n]["ramp"][:, b, :], scalar=BLOCKS[b][2], in1=chunks[n]["w"][b][:],
+                op0=ALU.min, op1=ALU.mult,
             )
-            nc.vector.scalar_tensor_tensor(
-                out=nd[:, SCALAR_BLOCK, :], in0=chunks[n]["ramp"][:, SCALAR_BLOCK, :], scalar=2.0,
-                in1=chunks[n]["rest"][:], op0=ALU.min, op1=ALU.add,
-            )
-            chunks[n]["nd"] = nd
-
-        def product(n, c):
-            prod = work.tile([P, CHUNK], F32, name="prod%d" % c)
-            nc.vector.scalar_tensor_tensor(
-                out=prod[:], in0=chunks[n]["nd"][:, c, :], scalar=(-2.0 if c == SCALAR_BLOCK else 1.0 * c),
-                in1=chunks[n]["gb"][c][:],
-                op0=ALU.add, op1=ALU.mult,
-            )
-            chunks[n]["product"][c] = prod
+            chunks[n]["product"][b] = prod
 
         def sum_blocks(n):
             sums = ps_sum.tile([P, CHUNK_TILES, 2, FEATURES], F32, name="sums")
             for a in range(CHUNK_TILES):
-                for c in range(BLOCKS):
+                for b in range(N_BLOCKS):
                     nc.tensor.matmul(
                         sums[:, a, :, :].rearrange("p h i -> p (h i)"),
-                        lhsT=chunks[n]["product"][c][:, P * a : P * a + P],
+                        lhsT=chunks[n]["product"][b][:, P * a : P * a + P],
                         rhs=ident[:],
                         is_transpose=True,
-                        start=(c == 0),
-                        stop=(c == BLOCKS - 1),
+                        start=(b == 0),
+                        stop=(b == N_BLOCKS - 1),
                     )
             chunks[n]["sums"] = sums
 
         def empty_sums(n):
             halves = three.tile([P, CHUNK_TILES, 2, FEATURES], F32, name="halves")
-            nc.scalar.copy(
+            nc.scalar.activation(
                 out=halves[:].rearrange("p a h i -> p (a h i)"),
                 in_=chunks[n]["sums"][:].rearrange("p a h i -> p (a h i)"),
+                func=ACT.Copy,
+                scale=-1.0,
             )
             chunks[n]["halves"] = halves
 
@@ -320,7 +296,7 @@ def tile_kan_layer_t_kernel(tc, x, spline_coeffs, grad_out, out):
             nc.vector.scalar_tensor_tensor(
                 out=result[:, t0 : t0 + CHUNK_TILES, :].rearrange("p a i -> p (a i)"),
                 in0=groups[g]["factor"][:, t0 * FEATURES : (t0 + CHUNK_TILES) * FEATURES],
-                scalar=INV_H,
+                scalar=0.5 * INV_H,
                 in1=chunks[n]["joined"][:].rearrange("p a i -> p (a i)"),
                 op0=ALU.subtract,
                 op1=ALU.mult,
@@ -355,52 +331,43 @@ def tile_kan_layer_t_kernel(tc, x, spline_coeffs, grad_out, out):
                     sum_blocks(n - 1)
 
                 if is_chunk(n + 1):
-                    halve_tau(n + 1)
-                    rise_first(n + 1)
-                    for c in range(BLOCKS):
-                        ramp_second(n + 1, c)
-                    rest_first(n + 1)
+                    for b in range(N_BLOCKS):
+                        ramp_up(n + 1, b)
                 if is_chunk(n + 2):
                     group_grad(n + 2)
                 if is_chunk(n - 1):
                     empty_sums(n - 1)
 
                 if n == FIRST_ROUND:
-                    for k in range(BASES // 2):
+                    for k in range(BASES):
                         regroup_coeffs(k)
+                if n == FIRST_ROUND + 1:
+                    scale_coeffs()
+                if n == -LEAD_WARP:
+                    quantise_coeffs()
+
                 if is_chunk(n + 1):
                     quantise_grad(n + 1)
-                if is_chunk(n):
-                    difference(n)
-                if is_chunk(n + 1):
-                    for c in range(GPSIMD_CLAMPS):
-                        clamp_first(n + 1, c)
-                if is_chunk(n - 2):
-                    join_halves(n - 2)
-                for c in range(BLOCKS):
-                    if is_chunk(n):
-                        product(n, c)
-                    ahead, block = (n, BLOCKS - 1) if c == 0 else (n + 1, c - 1)
-                    if is_chunk(ahead):
-                        multiply_mx(ahead, block)
                 for g in wrap_groups:
                     wrap_step(g)
                     abs_step(g)
-                if n == -LEAD_WRAP:
-                    for k in range(BASES // 2, BASES):
-                        regroup_coeffs(k)
                 for g in warp_groups:
                     parabola_step(g)
-                if n == -LEAD_WARP:
-                    quantise_coeffs()
-                if is_chunk(n + 1):
-                    clamp_first(n + 1, GPSIMD_CLAMPS)
-                for g in warp_groups:
-                    tau_even_step(g)
-                if is_chunk(n - 2):
-                    finish(n - 2)
-                for g in warp_groups:
-                    tau_odd_step(g)
-                    tau_copy_step(g)
+                for b in range(N_BLOCKS):
+                    if is_chunk(n):
+                        product(n, b)
+                    ahead, block = (n, N_BLOCKS - 1) if b == 0 else (n + 1, b - 1)
+                    if is_chunk(ahead):
+                        multiply_mx(ahead, block)
+                    if b == 0 and is_chunk(n - 2):
+                        join_halves(n - 2)
+                    if b == 1:
+                        for g in warp_groups:
+                            tau_even_step(g)
+                    if b == 2 and is_chunk(n - 2):
+                        finish(n - 2)
+                    if b == 3:
+                        for g in warp_groups:
+                            tau_odd_step(g)
                 for g in tanh_groups:
                     tanh_step(g)

@@ -197,7 +197,7 @@ def tile_kan_layer_t_kernel(tc, x, spline_coeffs, grad_out, out):
                     for u in range(2):
                         nc.tensor.transpose(grad_t[:, a, u, :], words[:, P * u : P * u + P], ident[:])
                 banks.append(grad_t)
-            chunks[n] = {"grad_t": banks, "w": {}, "product": {}}
+            chunks[n] = {"grad_t": banks, "w": {}, "product": {}, "terms": []}
 
         def transpose_tau(n):
             g, t0 = first_tile(n)
@@ -257,34 +257,39 @@ def tile_kan_layer_t_kernel(tc, x, spline_coeffs, grad_out, out):
             )
             chunks[n]["product"][b] = prod
 
+        def add_pair(n, b):
+            pair = work.tile([P, CHUNK], F32, name="pair%d" % b)
+            nc.gpsimd.tensor_tensor(
+                out=pair[:], in0=chunks[n]["product"][b - 1][:], in1=chunks[n]["product"][b][:], op=ALU.add
+            )
+            chunks[n]["terms"].append(pair)
+
         def sum_blocks(n):
             sums = ps_sum.tile([P, CHUNK_TILES, 2, FEATURES], F32, name="sums")
+            terms = chunks[n]["terms"] + [chunks[n]["product"][N_BLOCKS - 1]]
             for a in range(CHUNK_TILES):
-                for b in range(N_BLOCKS):
+                for s, term in enumerate(terms):
                     nc.tensor.matmul(
                         sums[:, a, :, :].rearrange("p h i -> p (h i)"),
-                        lhsT=chunks[n]["product"][b][:, P * a : P * a + P],
+                        lhsT=term[:, P * a : P * a + P],
                         rhs=ident[:],
                         is_transpose=True,
-                        start=(b == 0),
-                        stop=(b == N_BLOCKS - 1),
+                        start=(s == 0),
+                        stop=(s == len(terms) - 1),
                     )
             chunks[n]["sums"] = sums
 
-        def empty_sums(n):
-            halves = three.tile([P, CHUNK_TILES, 2, FEATURES], F32, name="halves")
-            nc.scalar.activation(
-                out=halves[:].rearrange("p a h i -> p (a h i)"),
-                in_=chunks[n]["sums"][:].rearrange("p a h i -> p (a h i)"),
-                func=ACT.Copy,
-                scale=-1.0,
-            )
-            chunks[n]["halves"] = halves
+        def empty_odd_half(n):
+            odd_half = three.tile([P, CHUNK_TILES, FEATURES], F32, name="odd_half")
+            nc.scalar.activation(out=odd_half[:], in_=chunks[n]["sums"][:, :, 1, :], func=ACT.Copy, scale=-1.0)
+            chunks[n]["odd_half"] = odd_half
 
         def join_halves(n):
             joined = work.tile([P, CHUNK_TILES, FEATURES], F32, name="joined")
-            halves = chunks[n]["halves"]
-            nc.vector.tensor_tensor(out=joined[:], in0=halves[:, :, 0, :], in1=halves[:, :, 1, :], op=ALU.add)
+            nc.vector.scalar_tensor_tensor(
+                out=joined[:], in0=chunks[n]["sums"][:, :, 0, :], scalar=-1.0, in1=chunks[n]["odd_half"][:],
+                op0=ALU.mult, op1=ALU.add,
+            )
             chunks[n]["joined"] = joined
 
         def finish(n):
@@ -314,7 +319,7 @@ def tile_kan_layer_t_kernel(tc, x, spline_coeffs, grad_out, out):
             return [g for g in range(N_GROUPS) if max(2 * g - lead, not_before.get(g, FIRST_ROUND)) == n]
 
         with tc.manual_schedule():
-            for n in range(FIRST_ROUND, N_CHUNKS + 2):
+            for n in range(FIRST_ROUND, N_CHUNKS + 1):
                 for g in groups_in_round(n, LEAD_LOAD, {}):
                     load_grad(g)
                     if g == 0:
@@ -336,7 +341,7 @@ def tile_kan_layer_t_kernel(tc, x, spline_coeffs, grad_out, out):
                 if is_chunk(n + 2):
                     group_grad(n + 2)
                 if is_chunk(n - 1):
-                    empty_sums(n - 1)
+                    empty_odd_half(n - 1)
 
                 if n == FIRST_ROUND:
                     for k in range(BASES):
@@ -354,20 +359,20 @@ def tile_kan_layer_t_kernel(tc, x, spline_coeffs, grad_out, out):
                 for g in warp_groups:
                     parabola_step(g)
                 for b in range(N_BLOCKS):
+                    if b == N_BLOCKS - 1 and is_chunk(n - 1):
+                        join_halves(n - 1)
                     if is_chunk(n):
                         product(n, b)
+                        if b in (1, 3):
+                            add_pair(n, b)
                     ahead, block = (n, N_BLOCKS - 1) if b == 0 else (n + 1, b - 1)
                     if is_chunk(ahead):
                         multiply_mx(ahead, block)
-                    if b == 0 and is_chunk(n - 2):
-                        join_halves(n - 2)
-                    if b == 1:
-                        for g in warp_groups:
-                            tau_even_step(g)
-                    if b == 2 and is_chunk(n - 2):
-                        finish(n - 2)
-                    if b == 3:
-                        for g in warp_groups:
-                            tau_odd_step(g)
+                for g in warp_groups:
+                    tau_even_step(g)
+                if is_chunk(n - 1):
+                    finish(n - 1)
+                for g in warp_groups:
+                    tau_odd_step(g)
                 for g in tanh_groups:
                     tanh_step(g)

@@ -52,12 +52,13 @@ def make_blocks():
 N_BLOCKS = 5
 W_BANKS = 4
 
-LEAD_LOAD = 7
-LEAD_TANH = 6
-LEAD_WRAP = 4
-LEAD_WARP = 3
+LEAD_LOAD = 8
+LEAD_TANH = 8
+LEAD_ROUND = 7
+LEAD_WRAP = 6
+LEAD_EVEN = 5
+LEAD_ODD = 4
 FIRST_ROUND = -LEAD_TANH
-TANH_NOT_BEFORE = {2: -1}
 
 
 def tile_kan_layer_t_kernel(tc, x, spline_coeffs, grad_out, out):
@@ -67,7 +68,7 @@ def tile_kan_layer_t_kernel(tc, x, spline_coeffs, grad_out, out):
         const = ctx.enter_context(tc.tile_pool(name="const", bufs=1))
         gpool = ctx.enter_context(tc.tile_pool(name="gpool", bufs=4))
         prep = ctx.enter_context(tc.tile_pool(name="prep", bufs=2))
-        keep = ctx.enter_context(tc.tile_pool(name="keep", bufs=5))
+        keep = ctx.enter_context(tc.tile_pool(name="keep", bufs=6))
         three = ctx.enter_context(tc.tile_pool(name="three", bufs=3))
         work = ctx.enter_context(tc.tile_pool(name="work", bufs=2))
         ps_grad = ctx.enter_context(tc.psum_pool(name="ps_grad", bufs=2))
@@ -139,13 +140,21 @@ def tile_kan_layer_t_kernel(tc, x, spline_coeffs, grad_out, out):
             return ap.rearrange("p (t i) -> p t i", i=FEATURES)
 
         def tanh_step(g):
-            th = prep.tile([P, GROUP_COLS], F32, name="th")
+            th = three.tile([P, GROUP_COLS], F32, name="th")
             nc.scalar.activation(out=th[:], in_=x_sb[:, g, :, :].rearrange("p t i -> p (t i)"), func=ACT.Tanh)
+            groups[g] = {"th": th}
+
+        def round_step(g):
             m_int = prep.tile([P, GROUP_COLS], U32, name="m_int")
-            nc.scalar.activation(out=m_int[:], in_=th[:], func=ACT.Copy, bias=0.5 * INV_H, scale=0.5 * INV_H)
+            nc.scalar.activation(
+                out=m_int[:], in_=groups[g]["th"][:], func=ACT.Copy, bias=0.5 * INV_H, scale=0.5 * INV_H
+            )
+            groups[g]["m_int"] = m_int
+
+        def factor_step(g):
             factor = keep.tile([P, GROUP_COLS], F32, name="factor")
-            nc.scalar.activation(out=factor[:], in_=th[:], func=ACT.Square, scale=math.sqrt(0.5 * INV_H))
-            groups[g] = {"th": th, "factor": factor, "m_int": m_int}
+            nc.scalar.activation(out=factor[:], in_=groups[g]["th"][:], func=ACT.Square, scale=math.sqrt(0.5 * INV_H))
+            groups[g]["factor"] = factor
 
         def wrap_step(g):
             y = prep.tile([P, GROUP_COLS], F32, name="y")
@@ -170,7 +179,7 @@ def tile_kan_layer_t_kernel(tc, x, spline_coeffs, grad_out, out):
             groups[g]["y_abs_y"] = y_abs_y
 
         def tau_even_step(g):
-            tau = prep.tile([P, GROUP_TILES, 2 * FEATURES], F32, name="tau")
+            tau = three.tile([P, GROUP_TILES, 2 * FEATURES], F32, name="tau")
             nc.vector.scalar_tensor_tensor(
                 out=tau[:, :, 0:FEATURES], in0=by_tile(groups[g]["m_int"][:].bitcast(I32)), scalar=2.0 / KNOTS_SPAN,
                 in1=by_tile(groups[g]["y_abs_y"][:]), op0=ALU.mult, op1=ALU.add,
@@ -208,7 +217,7 @@ def tile_kan_layer_t_kernel(tc, x, spline_coeffs, grad_out, out):
             chunks[n]["tau_t"] = tau_t
 
         def group_grad(n):
-            grouped = work.tile([P, PACK * CHUNK], BF16, align_bytes=64, name="grouped")
+            grouped = three.tile([P, PACK * CHUNK], BF16, align_bytes=64, name="grouped")
             grouped_words = grouped[:].bitcast(F32)
             for b in range(2):
                 nc.scalar.copy(
@@ -315,52 +324,57 @@ def tile_kan_layer_t_kernel(tc, x, spline_coeffs, grad_out, out):
         def is_chunk(n):
             return 0 <= n < N_CHUNKS
 
-        def groups_in_round(n, lead, not_before):
-            return [g for g in range(N_GROUPS) if max(2 * g - lead, not_before.get(g, FIRST_ROUND)) == n]
+        def groups_in_round(n, lead):
+            return [g for g in range(N_GROUPS) if max(2 * g - lead, FIRST_ROUND) == n]
 
         with tc.manual_schedule():
             for n in range(FIRST_ROUND, N_CHUNKS + 1):
-                for g in groups_in_round(n, LEAD_LOAD, {}):
+                for g in groups_in_round(n, LEAD_LOAD):
                     load_grad(g)
                     if g == 0:
-                        nc.sync.dma_start(out=x_sb[:, 2:N_GROUPS, :, :], in_=x_view[:, 2:N_GROUPS, :, :])
-                tanh_groups = groups_in_round(n, LEAD_TANH, TANH_NOT_BEFORE)
-                wrap_groups = groups_in_round(n, LEAD_WRAP, {})
-                warp_groups = groups_in_round(n, LEAD_WARP, {})
-
+                        nc.sync.dma_start(out=x_sb[:, 2:4, :, :], in_=x_view[:, 2:4, :, :])
+                    if g == 1:
+                        nc.sync.dma_start(out=x_sb[:, 4:N_GROUPS, :, :], in_=x_view[:, 4:N_GROUPS, :, :])
                 if is_chunk(n + 1):
                     transpose_tau(n + 1)
-                if is_chunk(n + 2):
-                    transpose_grad(n + 2)
+                if is_chunk(n + 3):
+                    transpose_grad(n + 3)
                 if is_chunk(n - 1):
                     sum_blocks(n - 1)
-
-                if is_chunk(n + 1):
-                    for b in range(N_BLOCKS):
-                        ramp_up(n + 1, b)
-                if is_chunk(n + 2):
-                    group_grad(n + 2)
-                if is_chunk(n - 1):
-                    empty_odd_half(n - 1)
 
                 if n == FIRST_ROUND:
                     for k in range(BASES):
                         regroup_coeffs(k)
                 if n == FIRST_ROUND + 1:
                     scale_coeffs()
-                if n == -LEAD_WARP:
+                if n == FIRST_ROUND + 3:
                     quantise_coeffs()
 
                 if is_chunk(n + 1):
                     quantise_grad(n + 1)
-                for g in wrap_groups:
+                for g in groups_in_round(n, LEAD_WRAP):
                     wrap_step(g)
-                    abs_step(g)
-                for g in warp_groups:
+                for g in groups_in_round(n, LEAD_EVEN):
                     parabola_step(g)
+
                 for b in range(N_BLOCKS):
-                    if b == N_BLOCKS - 1 and is_chunk(n - 1):
-                        join_halves(n - 1)
+                    if b == 3:
+                        if is_chunk(n - 1):
+                            empty_odd_half(n - 1)
+                        for g in groups_in_round(n, LEAD_WRAP):
+                            abs_step(g)
+                        for g in groups_in_round(n, LEAD_ROUND):
+                            round_step(g)
+                    if is_chunk(n + 1):
+                        ramp_up(n + 1, b)
+                if is_chunk(n + 3):
+                    group_grad(n + 3)
+                for g in groups_in_round(n, LEAD_ROUND):
+                    factor_step(g)
+                for g in groups_in_round(n, LEAD_TANH):
+                    tanh_step(g)
+
+                for b in range(N_BLOCKS):
                     if is_chunk(n):
                         product(n, b)
                         if b in (1, 3):
@@ -368,11 +382,11 @@ def tile_kan_layer_t_kernel(tc, x, spline_coeffs, grad_out, out):
                     ahead, block = (n, N_BLOCKS - 1) if b == 0 else (n + 1, b - 1)
                     if is_chunk(ahead):
                         multiply_mx(ahead, block)
-                for g in warp_groups:
+                if is_chunk(n - 1):
+                    join_halves(n - 1)
+                for g in groups_in_round(n, LEAD_EVEN):
                     tau_even_step(g)
+                for g in groups_in_round(n, LEAD_ODD):
+                    tau_odd_step(g)
                 if is_chunk(n - 1):
                     finish(n - 1)
-                for g in warp_groups:
-                    tau_odd_step(g)
-                for g in tanh_groups:
-                    tanh_step(g)

@@ -55,9 +55,9 @@ W_BANKS = 4
 LEAD_LOAD = 8
 LEAD_TANH = 8
 LEAD_ROUND = 7
-LEAD_WRAP = 6
-LEAD_EVEN = 5
-LEAD_ODD = 4
+LEAD_WRAP = 5
+LEAD_PARABOLA = 4
+LEAD_TAU = 3
 FIRST_ROUND = -LEAD_TANH
 
 
@@ -188,7 +188,7 @@ def tile_kan_layer_t_kernel(tc, x, spline_coeffs, grad_out, out):
 
         def tau_odd_step(g):
             tau = groups[g]["tau"]
-            nc.vector.tensor_tensor(
+            nc.gpsimd.tensor_tensor(
                 out=tau[:, :, FEATURES : 2 * FEATURES], in0=by_tile(groups[g]["th"][:]), in1=tau[:, :, 0:FEATURES],
                 op=ALU.subtract,
             )
@@ -267,16 +267,20 @@ def tile_kan_layer_t_kernel(tc, x, spline_coeffs, grad_out, out):
             chunks[n]["product"][b] = prod
 
         def add_pair(n, b):
-            pair = work.tile([P, CHUNK], F32, name="pair%d" % b)
+            cols = CHUNK if b == 1 else CHUNK // 2
+            pair = work.tile([P, cols], F32, name="pair%d" % b)
             nc.gpsimd.tensor_tensor(
-                out=pair[:], in0=chunks[n]["product"][b - 1][:], in1=chunks[n]["product"][b][:], op=ALU.add
+                out=pair[:], in0=chunks[n]["product"][b - 1][:, 0:cols], in1=chunks[n]["product"][b][:, 0:cols], op=ALU.add
             )
             chunks[n]["terms"].append(pair)
 
         def sum_blocks(n):
             sums = ps_sum.tile([P, CHUNK_TILES, 2, FEATURES], F32, name="sums")
-            terms = chunks[n]["terms"] + [chunks[n]["product"][N_BLOCKS - 1]]
             for a in range(CHUNK_TILES):
+                if a < CHUNK_TILES // 2:
+                    terms = chunks[n]["terms"] + [chunks[n]["product"][N_BLOCKS - 1]]
+                else:
+                    terms = chunks[n]["terms"][0:1] + [chunks[n]["product"][b] for b in range(2, N_BLOCKS)]
                 for s, term in enumerate(terms):
                     nc.tensor.matmul(
                         sums[:, a, :, :].rearrange("p h i -> p (h i)"),
@@ -352,16 +356,15 @@ def tile_kan_layer_t_kernel(tc, x, spline_coeffs, grad_out, out):
 
                 if is_chunk(n + 1):
                     quantise_grad(n + 1)
-                for g in groups_in_round(n, LEAD_WRAP):
-                    wrap_step(g)
-                for g in groups_in_round(n, LEAD_EVEN):
-                    parabola_step(g)
+                for g in groups_in_round(n, LEAD_TAU):
+                    tau_even_step(g)
+                    tau_odd_step(g)
 
                 for b in range(N_BLOCKS):
                     if b == 3:
                         if is_chunk(n - 1):
                             empty_odd_half(n - 1)
-                        for g in groups_in_round(n, LEAD_WRAP):
+                        for g in groups_in_round(n, LEAD_PARABOLA):
                             abs_step(g)
                         for g in groups_in_round(n, LEAD_ROUND):
                             round_step(g)
@@ -369,7 +372,7 @@ def tile_kan_layer_t_kernel(tc, x, spline_coeffs, grad_out, out):
                         ramp_up(n + 1, b)
                 if is_chunk(n + 3):
                     group_grad(n + 3)
-                for g in groups_in_round(n, LEAD_ROUND):
+                for g in groups_in_round(n, LEAD_WRAP):
                     factor_step(g)
                 for g in groups_in_round(n, LEAD_TANH):
                     tanh_step(g)
@@ -384,9 +387,9 @@ def tile_kan_layer_t_kernel(tc, x, spline_coeffs, grad_out, out):
                         multiply_mx(ahead, block)
                 if is_chunk(n - 1):
                     join_halves(n - 1)
-                for g in groups_in_round(n, LEAD_EVEN):
-                    tau_even_step(g)
-                for g in groups_in_round(n, LEAD_ODD):
-                    tau_odd_step(g)
+                for g in groups_in_round(n, LEAD_WRAP):
+                    wrap_step(g)
+                for g in groups_in_round(n, LEAD_PARABOLA):
+                    parabola_step(g)
                 if is_chunk(n - 1):
                     finish(n - 1)

@@ -53,11 +53,11 @@ N_BLOCKS = 5
 W_BANKS = 4
 
 LEAD_LOAD = 8
-LEAD_TANH = 8
-LEAD_ROUND = 7
-LEAD_WRAP = 5
-LEAD_PARABOLA = 4
-LEAD_TAU = 3
+LEAD_TANH = 5
+LEAD_ROUND = 4
+LEAD_WRAP = 4
+LEAD_PARABOLA = 3
+LEAD_TAU = 2
 FIRST_ROUND = -LEAD_TANH
 
 
@@ -349,30 +349,28 @@ def tile_kan_layer_t_kernel(tc, x, spline_coeffs, grad_out, out):
                 if n == FIRST_ROUND:
                     for k in range(BASES):
                         regroup_coeffs(k)
-                if n == FIRST_ROUND + 1:
-                    scale_coeffs()
-                if n == FIRST_ROUND + 3:
-                    quantise_coeffs()
 
                 if is_chunk(n + 1):
                     quantise_grad(n + 1)
                 for g in groups_in_round(n, LEAD_TAU):
                     tau_even_step(g)
                     tau_odd_step(g)
+                if n == -LEAD_TAU:
+                    quantise_coeffs()
 
+                for g in groups_in_round(n, LEAD_PARABOLA):
+                    abs_step(g)
                 for b in range(N_BLOCKS):
                     if b == 3:
                         if is_chunk(n - 1):
                             empty_odd_half(n - 1)
-                        for g in groups_in_round(n, LEAD_PARABOLA):
-                            abs_step(g)
                         for g in groups_in_round(n, LEAD_ROUND):
                             round_step(g)
                     if is_chunk(n + 1):
                         ramp_up(n + 1, b)
                 if is_chunk(n + 3):
                     group_grad(n + 3)
-                for g in groups_in_round(n, LEAD_WRAP):
+                for g in groups_in_round(n, LEAD_TAU):
                     factor_step(g)
                 for g in groups_in_round(n, LEAD_TANH):
                     tanh_step(g)
@@ -389,6 +387,8 @@ def tile_kan_layer_t_kernel(tc, x, spline_coeffs, grad_out, out):
                     join_halves(n - 1)
                 for g in groups_in_round(n, LEAD_WRAP):
                     wrap_step(g)
+                if n == -LEAD_WRAP:
+                    scale_coeffs()
                 for g in groups_in_round(n, LEAD_PARABOLA):
                     parabola_step(g)
                 if is_chunk(n - 1):

@@ -274,17 +274,28 @@ def tile_kan_layer_t_kernel(tc, x, spline_coeffs, grad_out, out):
             )
             chunks[n]["terms"].append(pair)
 
+        def add_rest(n):
+            rest = work.tile([P, CHUNK // 2], F32, name="rest")
+            nc.vector.tensor_tensor(
+                out=rest[:], in0=chunks[n]["product"][2][:, CHUNK // 2 : CHUNK], in1=chunks[n]["product"][3][:, CHUNK // 2 : CHUNK],
+                op=ALU.add,
+            )
+            chunks[n]["rest"] = rest
+
         def sum_blocks(n):
             sums = ps_sum.tile([P, CHUNK_TILES, 2, FEATURES], F32, name="sums")
             for a in range(CHUNK_TILES):
-                if a < CHUNK_TILES // 2:
-                    terms = chunks[n]["terms"] + [chunks[n]["product"][N_BLOCKS - 1]]
-                else:
-                    terms = chunks[n]["terms"][0:1] + [chunks[n]["product"][b] for b in range(2, N_BLOCKS)]
+                half = CHUNK_TILES // 2
+                second = chunks[n]["terms"][1] if a < half else chunks[n]["rest"]
+                terms = [
+                    chunks[n]["terms"][0][:, P * a : P * a + P],
+                    second[:, P * (a % half) : P * (a % half) + P],
+                    chunks[n]["product"][N_BLOCKS - 1][:, P * a : P * a + P],
+                ]
                 for s, term in enumerate(terms):
                     nc.tensor.matmul(
                         sums[:, a, :, :].rearrange("p h i -> p (h i)"),
-                        lhsT=term[:, P * a : P * a + P],
+                        lhsT=term,
                         rhs=ident[:],
                         is_transpose=True,
                         start=(s == 0),
@@ -385,6 +396,8 @@ def tile_kan_layer_t_kernel(tc, x, spline_coeffs, grad_out, out):
                         multiply_mx(ahead, block)
                 if is_chunk(n - 1):
                     join_halves(n - 1)
+                if is_chunk(n):
+                    add_rest(n)
                 for g in groups_in_round(n, LEAD_WRAP):
                     wrap_step(g)
                 if n == -LEAD_WRAP:

@@ -275,9 +275,9 @@ def tile_kan_layer_t_kernel(tc, x, spline_coeffs, grad_out, out):
             chunks[n]["terms"].append(pair)
 
         def add_rest(n):
-            rest = work.tile([P, CHUNK // 2], F32, name="rest")
+            rest = work.tile([P, P], F32, name="rest")
             nc.vector.tensor_tensor(
-                out=rest[:], in0=chunks[n]["product"][2][:, CHUNK // 2 : CHUNK], in1=chunks[n]["product"][3][:, CHUNK // 2 : CHUNK],
+                out=rest[:], in0=chunks[n]["product"][2][:, 2 * P : 3 * P], in1=chunks[n]["product"][3][:, 2 * P : 3 * P],
                 op=ALU.add,
             )
             chunks[n]["rest"] = rest
@@ -285,13 +285,14 @@ def tile_kan_layer_t_kernel(tc, x, spline_coeffs, grad_out, out):
         def sum_blocks(n):
             sums = ps_sum.tile([P, CHUNK_TILES, 2, FEATURES], F32, name="sums")
             for a in range(CHUNK_TILES):
-                half = CHUNK_TILES // 2
-                second = chunks[n]["terms"][1] if a < half else chunks[n]["rest"]
-                terms = [
-                    chunks[n]["terms"][0][:, P * a : P * a + P],
-                    second[:, P * (a % half) : P * (a % half) + P],
-                    chunks[n]["product"][N_BLOCKS - 1][:, P * a : P * a + P],
-                ]
+                cols = slice(P * a, P * a + P)
+                if a < 2:
+                    second = [chunks[n]["terms"][1][:, cols]]
+                elif a == 2:
+                    second = [chunks[n]["rest"][:]]
+                else:
+                    second = [chunks[n]["product"][2][:, cols], chunks[n]["product"][3][:, cols]]
+                terms = [chunks[n]["terms"][0][:, cols]] + second + [chunks[n]["product"][N_BLOCKS - 1][:, cols]]
                 for s, term in enumerate(terms):
                     nc.tensor.matmul(
                         sums[:, a, :, :].rearrange("p h i -> p (h i)"),

@@ -29,6 +29,7 @@ INV_H = 5.5
 KNOTS_SPAN = 11.0
 
 N_UNITS = 2 * BASES + 1
+UNIT_IN = FEATURES * PACK
 
 
 def unit_n(k):
@@ -52,25 +53,26 @@ def make_blocks():
 N_BLOCKS = 5
 W_BANKS = 4
 
+SECOND_PAIR_ON_GPSIMD = 2
+SECOND_PAIR_ON_VECTOR = 1
+
 LEAD_LOAD = 8
 LEAD_TANH = 5
-LEAD_ROUND = 4
 LEAD_WRAP = 4
 LEAD_PARABOLA = 3
 LEAD_TAU = 2
 FIRST_ROUND = -LEAD_TANH
+RELUS_BEFORE_SUMS = 3
 
 
 def tile_kan_layer_t_kernel(tc, x, spline_coeffs, grad_out, out):
     nc = tc.nc
-    BLOCKS = make_blocks()
+    blocks = make_blocks()
     with ExitStack() as ctx:
         const = ctx.enter_context(tc.tile_pool(name="const", bufs=1))
         gpool = ctx.enter_context(tc.tile_pool(name="gpool", bufs=4))
-        prep = ctx.enter_context(tc.tile_pool(name="prep", bufs=2))
-        keep = ctx.enter_context(tc.tile_pool(name="keep", bufs=6))
+        two = ctx.enter_context(tc.tile_pool(name="two", bufs=2))
         three = ctx.enter_context(tc.tile_pool(name="three", bufs=3))
-        work = ctx.enter_context(tc.tile_pool(name="work", bufs=2))
         ps_grad = ctx.enter_context(tc.psum_pool(name="ps_grad", bufs=2))
         ps_tau = ctx.enter_context(tc.psum_pool(name="ps_tau", bufs=1))
         ps_w = ctx.enter_context(tc.psum_pool(name="ps_w", bufs=W_BANKS))
@@ -92,16 +94,15 @@ def tile_kan_layer_t_kernel(tc, x, spline_coeffs, grad_out, out):
         half_span = const.tile([P, 1], F32)
         nc.vector.memset(half_span[:], 0.5 * INV_H)
         ramp_bias = const.tile([P, N_BLOCKS], F32)
-        for b, (even_knot, odd_knot, width, units) in enumerate(BLOCKS):
+        for b, (even_knot, odd_knot, width, units) in enumerate(blocks):
             nc.vector.memset(ramp_bias[0:64, b : b + 1], -1.0 * even_knot)
             nc.vector.memset(ramp_bias[64:128, b : b + 1], KNOTS_SPAN - odd_knot)
 
-        c_grouped = const.tile([P, N_UNITS * FEATURES * PACK], BF16, align_bytes=64)
+        c_grouped = const.tile([P, N_UNITS * UNIT_IN], BF16, align_bytes=64)
         c_grouped_by_unit = c_grouped[:].rearrange("q (s i t) -> q s i t", s=N_UNITS, t=PACK)
         c_rows_by_k = c_rows[:].rearrange("q t (i k) -> q k i t", k=BASES)
         c_codes = const.tile([P, N_UNITS * FEATURES], U32, align_bytes=64)
         c_scales = const.tile([P, N_UNITS * FEATURES], U8, align_bytes=64)
-        UNIT_IN = FEATURES * PACK
 
         def regroup_coeffs(k):
             nc.vector.tensor_copy(out=c_grouped_by_unit[:, unit_c(k), :, :], in_=c_rows_by_k[:, k, :, :])
@@ -139,59 +140,70 @@ def tile_kan_layer_t_kernel(tc, x, spline_coeffs, grad_out, out):
         def by_tile(ap):
             return ap.rearrange("p (t i) -> p t i", i=FEATURES)
 
+        def pieces(g):
+            if g == 0:
+                return (slice(0, GROUP_COLS // 2), slice(GROUP_COLS // 2, GROUP_COLS))
+            return (slice(0, GROUP_COLS),)
+
         def tanh_step(g):
             th = three.tile([P, GROUP_COLS], F32, name="th")
-            nc.scalar.activation(out=th[:], in_=x_sb[:, g, :, :].rearrange("p t i -> p (t i)"), func=ACT.Tanh)
+            x_cols = x_sb[:, g, :, :].rearrange("p t i -> p (t i)")
+            for cols in pieces(g):
+                nc.scalar.activation(out=th[:, cols], in_=x_cols[:, cols], func=ACT.Tanh)
             groups[g] = {"th": th}
 
         def round_step(g):
-            m_int = prep.tile([P, GROUP_COLS], U32, name="m_int")
-            nc.scalar.activation(
-                out=m_int[:], in_=groups[g]["th"][:], func=ACT.Copy, bias=0.5 * INV_H, scale=0.5 * INV_H
-            )
+            m_int = two.tile([P, GROUP_COLS], U32, name="m_int")
+            for cols in pieces(g):
+                nc.scalar.activation(
+                    out=m_int[:, cols], in_=groups[g]["th"][:, cols], func=ACT.Copy, bias=0.5 * INV_H, scale=0.5 * INV_H
+                )
             groups[g]["m_int"] = m_int
 
         def factor_step(g):
-            factor = keep.tile([P, GROUP_COLS], F32, name="factor")
+            factor = three.tile([P, GROUP_COLS], F32, name="factor")
             nc.scalar.activation(out=factor[:], in_=groups[g]["th"][:], func=ACT.Square, scale=math.sqrt(0.5 * INV_H))
             groups[g]["factor"] = factor
 
         def wrap_step(g):
-            y = prep.tile([P, GROUP_COLS], F32, name="y")
-            nc.vector.scalar_tensor_tensor(
-                out=y[:], in0=groups[g]["m_int"][:].bitcast(I32), scalar=-2.0 / INV_H, in1=groups[g]["th"][:],
-                op0=ALU.mult, op1=ALU.add,
-            )
+            y = two.tile([P, GROUP_COLS], F32, name="y")
+            for cols in pieces(g):
+                nc.vector.scalar_tensor_tensor(
+                    out=y[:, cols], in0=groups[g]["m_int"][:, cols].bitcast(I32), scalar=-2.0 / INV_H,
+                    in1=groups[g]["th"][:, cols], op0=ALU.mult, op1=ALU.add,
+                )
             groups[g]["y"] = y
 
         def abs_step(g):
-            abs_y = prep.tile([P, GROUP_COLS], F32, name="abs_y")
-            nc.scalar.activation(
-                out=abs_y[:], in_=groups[g]["y"][:], func=ACT.Abs, bias=half_span[:, 0:1], scale=0.5 * INV_H
-            )
+            abs_y = two.tile([P, GROUP_COLS], F32, name="abs_y")
+            for cols in pieces(g):
+                nc.scalar.activation(
+                    out=abs_y[:, cols], in_=groups[g]["y"][:, cols], func=ACT.Abs, bias=half_span[:, 0:1], scale=0.5 * INV_H
+                )
             groups[g]["abs_y"] = abs_y
 
         def parabola_step(g):
-            y_abs_y = prep.tile([P, GROUP_COLS], F32, name="y_abs_y")
-            nc.vector.scalar_tensor_tensor(
-                out=y_abs_y[:], in0=groups[g]["y"][:], scalar=1.0, in1=groups[g]["abs_y"][:], op0=ALU.add, op1=ALU.mult
-            )
+            y_abs_y = two.tile([P, GROUP_COLS], F32, name="y_abs_y")
+            for cols in pieces(g):
+                nc.vector.scalar_tensor_tensor(
+                    out=y_abs_y[:, cols], in0=groups[g]["y"][:, cols], scalar=1.0, in1=groups[g]["abs_y"][:, cols],
+                    op0=ALU.add, op1=ALU.mult,
+                )
             groups[g]["y_abs_y"] = y_abs_y
 
-        def tau_even_step(g):
+        def tau_step(g):
             tau = three.tile([P, GROUP_TILES, 2 * FEATURES], F32, name="tau")
-            nc.vector.scalar_tensor_tensor(
-                out=tau[:, :, 0:FEATURES], in0=by_tile(groups[g]["m_int"][:].bitcast(I32)), scalar=2.0 / KNOTS_SPAN,
-                in1=by_tile(groups[g]["y_abs_y"][:]), op0=ALU.mult, op1=ALU.add,
-            )
+            for cols in pieces(g):
+                tiles = slice(cols.start // FEATURES, cols.stop // FEATURES)
+                nc.vector.scalar_tensor_tensor(
+                    out=tau[:, tiles, 0:FEATURES], in0=by_tile(groups[g]["m_int"][:, cols].bitcast(I32)),
+                    scalar=2.0 / KNOTS_SPAN, in1=by_tile(groups[g]["y_abs_y"][:, cols]), op0=ALU.mult, op1=ALU.add,
+                )
+                nc.gpsimd.tensor_tensor(
+                    out=tau[:, tiles, FEATURES : 2 * FEATURES], in0=by_tile(groups[g]["th"][:, cols]),
+                    in1=tau[:, tiles, 0:FEATURES], op=ALU.subtract,
+                )
             groups[g]["tau"] = tau
-
-        def tau_odd_step(g):
-            tau = groups[g]["tau"]
-            nc.gpsimd.tensor_tensor(
-                out=tau[:, :, FEATURES : 2 * FEATURES], in0=by_tile(groups[g]["th"][:]), in1=tau[:, :, 0:FEATURES],
-                op=ALU.subtract,
-            )
 
         def first_tile(n):
             return n // 2, (n % 2) * CHUNK_TILES
@@ -206,7 +218,7 @@ def tile_kan_layer_t_kernel(tc, x, spline_coeffs, grad_out, out):
                     for u in range(2):
                         nc.tensor.transpose(grad_t[:, a, u, :], words[:, P * u : P * u + P], ident[:])
                 banks.append(grad_t)
-            chunks[n] = {"grad_t": banks, "w": {}, "product": {}, "terms": []}
+            chunks[n] = {"grad_t": banks, "w": {}, "product": {}}
 
         def transpose_tau(n):
             g, t0 = first_tile(n)
@@ -227,15 +239,15 @@ def tile_kan_layer_t_kernel(tc, x, spline_coeffs, grad_out, out):
             chunks[n]["grouped"] = grouped
 
         def quantise_grad(n):
-            g_codes = work.tile([P, CHUNK], U32, align_bytes=64, name="g_codes")
-            g_scales = work.tile([P, CHUNK], U8, align_bytes=64, name="g_scales")
+            g_codes = two.tile([P, CHUNK], U32, align_bytes=64, name="g_codes")
+            g_scales = two.tile([P, CHUNK], U8, align_bytes=64, name="g_scales")
             nc.vector.quantize_mx(out=g_codes[:].bitcast(E5M2_X4), scales=g_scales[:], in_=chunks[n]["grouped"][:])
             chunks[n]["g_codes"] = g_codes
             chunks[n]["g_scales"] = g_scales
 
         def ramp_up(n, b):
             if b == 0:
-                ramp = work.tile([P, N_BLOCKS, CHUNK], F32, name="ramp")
+                ramp = two.tile([P, N_BLOCKS, CHUNK], F32, name="ramp")
                 chunks[n]["ramp"] = ramp
             nc.scalar.activation(
                 out=chunks[n]["ramp"][:, b, :], in_=chunks[n]["tau_t"][:], func=ACT.Relu,
@@ -244,7 +256,7 @@ def tile_kan_layer_t_kernel(tc, x, spline_coeffs, grad_out, out):
 
         def multiply_mx(n, b):
             w = ps_w.tile([P, CHUNK], F32, name="w")
-            units = BLOCKS[b][3]
+            units = blocks[b][3]
             for s, unit in enumerate(units):
                 first = unit * FEATURES
                 nc.tensor.matmul_mx(
@@ -259,26 +271,26 @@ def tile_kan_layer_t_kernel(tc, x, spline_coeffs, grad_out, out):
             chunks[n]["w"][b] = w
 
         def product(n, b):
-            prod = work.tile([P, CHUNK], F32, name="prod%d" % b)
+            prod = two.tile([P, CHUNK], F32, name="prod%d" % b)
             nc.vector.scalar_tensor_tensor(
-                out=prod[:], in0=chunks[n]["ramp"][:, b, :], scalar=BLOCKS[b][2], in1=chunks[n]["w"][b][:],
+                out=prod[:], in0=chunks[n]["ramp"][:, b, :], scalar=blocks[b][2], in1=chunks[n]["w"][b][:],
                 op0=ALU.min, op1=ALU.mult,
             )
             chunks[n]["product"][b] = prod
 
-        def add_pair(n, b):
-            cols = CHUNK if b == 1 else CHUNK // 2
-            pair = work.tile([P, cols], F32, name="pair%d" % b)
+        def add_on_gpsimd(n, b, n_tiles):
+            pair = two.tile([P, P * n_tiles], F32, name="pair%d" % b)
             nc.gpsimd.tensor_tensor(
-                out=pair[:], in0=chunks[n]["product"][b - 1][:, 0:cols], in1=chunks[n]["product"][b][:, 0:cols], op=ALU.add
+                out=pair[:], in0=chunks[n]["product"][b - 1][:, 0 : P * n_tiles],
+                in1=chunks[n]["product"][b][:, 0 : P * n_tiles], op=ALU.add,
             )
-            chunks[n]["terms"].append(pair)
+            chunks[n]["pair%d" % b] = pair
 
-        def add_rest(n):
-            rest = work.tile([P, P], F32, name="rest")
+        def add_on_vector(n):
+            cols = slice(P * SECOND_PAIR_ON_GPSIMD, P * (SECOND_PAIR_ON_GPSIMD + SECOND_PAIR_ON_VECTOR))
+            rest = two.tile([P, P * SECOND_PAIR_ON_VECTOR], F32, name="rest")
             nc.vector.tensor_tensor(
-                out=rest[:], in0=chunks[n]["product"][2][:, 2 * P : 3 * P], in1=chunks[n]["product"][3][:, 2 * P : 3 * P],
-                op=ALU.add,
+                out=rest[:], in0=chunks[n]["product"][2][:, cols], in1=chunks[n]["product"][3][:, cols], op=ALU.add
             )
             chunks[n]["rest"] = rest
 
@@ -286,13 +298,14 @@ def tile_kan_layer_t_kernel(tc, x, spline_coeffs, grad_out, out):
             sums = ps_sum.tile([P, CHUNK_TILES, 2, FEATURES], F32, name="sums")
             for a in range(CHUNK_TILES):
                 cols = slice(P * a, P * a + P)
-                if a < 2:
-                    second = [chunks[n]["terms"][1][:, cols]]
-                elif a == 2:
-                    second = [chunks[n]["rest"][:]]
+                after_gpsimd = a - SECOND_PAIR_ON_GPSIMD
+                if after_gpsimd < 0:
+                    second_pair = [chunks[n]["pair3"][:, cols]]
+                elif after_gpsimd < SECOND_PAIR_ON_VECTOR:
+                    second_pair = [chunks[n]["rest"][:, P * after_gpsimd : P * after_gpsimd + P]]
                 else:
-                    second = [chunks[n]["product"][2][:, cols], chunks[n]["product"][3][:, cols]]
-                terms = [chunks[n]["terms"][0][:, cols]] + second + [chunks[n]["product"][N_BLOCKS - 1][:, cols]]
+                    second_pair = [chunks[n]["product"][2][:, cols], chunks[n]["product"][3][:, cols]]
+                terms = [chunks[n]["pair1"][:, cols]] + second_pair + [chunks[n]["product"][N_BLOCKS - 1][:, cols]]
                 for s, term in enumerate(terms):
                     nc.tensor.matmul(
                         sums[:, a, :, :].rearrange("p h i -> p (h i)"),
@@ -310,7 +323,7 @@ def tile_kan_layer_t_kernel(tc, x, spline_coeffs, grad_out, out):
             chunks[n]["odd_half"] = odd_half
 
         def join_halves(n):
-            joined = work.tile([P, CHUNK_TILES, FEATURES], F32, name="joined")
+            joined = two.tile([P, CHUNK_TILES, FEATURES], F32, name="joined")
             nc.vector.scalar_tensor_tensor(
                 out=joined[:], in0=chunks[n]["sums"][:, :, 0, :], scalar=-1.0, in1=chunks[n]["odd_half"][:],
                 op0=ALU.mult, op1=ALU.add,
@@ -320,7 +333,7 @@ def tile_kan_layer_t_kernel(tc, x, spline_coeffs, grad_out, out):
         def finish(n):
             g, t0 = first_tile(n)
             if t0 == 0:
-                result = work.tile([P, GROUP_TILES, FEATURES], F32, name="result")
+                result = two.tile([P, GROUP_TILES, FEATURES], F32, name="result")
                 groups[g]["result"] = result
             result = groups[g]["result"]
             nc.vector.scalar_tensor_tensor(
@@ -365,18 +378,17 @@ def tile_kan_layer_t_kernel(tc, x, spline_coeffs, grad_out, out):
                 if is_chunk(n + 1):
                     quantise_grad(n + 1)
                 for g in groups_in_round(n, LEAD_TAU):
-                    tau_even_step(g)
-                    tau_odd_step(g)
+                    tau_step(g)
                 if n == -LEAD_TAU:
                     quantise_coeffs()
 
                 for g in groups_in_round(n, LEAD_PARABOLA):
                     abs_step(g)
                 for b in range(N_BLOCKS):
-                    if b == 3:
+                    if b == RELUS_BEFORE_SUMS:
                         if is_chunk(n - 1):
                             empty_odd_half(n - 1)
-                        for g in groups_in_round(n, LEAD_ROUND):
+                        for g in groups_in_round(n, LEAD_WRAP):
                             round_step(g)
                     if is_chunk(n + 1):
                         ramp_up(n + 1, b)
@@ -388,17 +400,19 @@ def tile_kan_layer_t_kernel(tc, x, spline_coeffs, grad_out, out):
                     tanh_step(g)
 
                 for b in range(N_BLOCKS):
+                    if b == N_BLOCKS - 1 and is_chunk(n - 1):
+                        join_halves(n - 1)
                     if is_chunk(n):
                         product(n, b)
-                        if b in (1, 3):
-                            add_pair(n, b)
+                        if b == 1:
+                            add_on_gpsimd(n, b, CHUNK_TILES)
+                        if b == 3:
+                            add_on_gpsimd(n, b, SECOND_PAIR_ON_GPSIMD)
                     ahead, block = (n, N_BLOCKS - 1) if b == 0 else (n + 1, b - 1)
                     if is_chunk(ahead):
                         multiply_mx(ahead, block)
-                if is_chunk(n - 1):
-                    join_halves(n - 1)
                 if is_chunk(n):
-                    add_rest(n)
+                    add_on_vector(n)
                 for g in groups_in_round(n, LEAD_WRAP):
                     wrap_step(g)
                 if n == -LEAD_WRAP:

@@ -28,8 +28,10 @@ N_CHUNKS = TOKENS // CHUNK
 INV_H = 5.5
 KNOTS_SPAN = 11.0
 
-N_UNITS = 2 * BASES + 1
+N_UNITS = 2 * BASES
+N_WINDOWS = BASES
 UNIT_IN = FEATURES * PACK
+SCALE_STRIDE = 256
 
 
 def unit_n(k):
@@ -37,7 +39,7 @@ def unit_n(k):
 
 
 def unit_c(k):
-    return 2 * BASES - 1 - k
+    return BASES + (BASES - k) % BASES
 
 
 def make_blocks():
@@ -98,31 +100,29 @@ def tile_kan_layer_t_kernel(tc, x, spline_coeffs, grad_out, out):
             nc.vector.memset(ramp_bias[0:64, b : b + 1], -1.0 * even_knot)
             nc.vector.memset(ramp_bias[64:128, b : b + 1], KNOTS_SPAN - odd_knot)
 
-        c_grouped = const.tile([P, N_UNITS * UNIT_IN], BF16, align_bytes=64)
+        c_grouped = const.tile([P, N_UNITS * UNIT_IN], BF16, align_bytes=256)
         c_grouped_by_unit = c_grouped[:].rearrange("q (s i t) -> q s i t", s=N_UNITS, t=PACK)
         c_rows_by_k = c_rows[:].rearrange("q t (i k) -> q k i t", k=BASES)
-        c_codes = const.tile([P, N_UNITS * FEATURES], U32, align_bytes=64)
-        c_scales = const.tile([P, N_UNITS * FEATURES], U8, align_bytes=64)
+        c_codes = const.tile([P, N_WINDOWS, P], U32, align_bytes=256)
+        c_scales = const.tile([P, N_WINDOWS, SCALE_STRIDE], U8, align_bytes=256)
 
         def regroup_coeffs(k):
             nc.vector.tensor_copy(out=c_grouped_by_unit[:, unit_c(k), :, :], in_=c_rows_by_k[:, k, :, :])
 
         def scale_coeffs():
-            nc.vector.tensor_scalar(
-                out=c_grouped[:, 0 : BASES * UNIT_IN], in0=c_grouped[:, BASES * UNIT_IN : 2 * BASES * UNIT_IN],
-                scalar1=-2.0, scalar2=None, op0=ALU.mult,
-            )
-            nc.vector.tensor_copy(
-                out=c_grouped[:, 2 * BASES * UNIT_IN : N_UNITS * UNIT_IN],
-                in_=c_grouped[:, unit_c(BASES - 1) * UNIT_IN : (unit_c(BASES - 1) + 1) * UNIT_IN],
-            )
+            for k, units in ((BASES - 1, BASES - 1), (0, 1)):
+                nc.vector.tensor_scalar(
+                    out=c_grouped[:, unit_n(k) * UNIT_IN : (unit_n(k) + units) * UNIT_IN],
+                    in0=c_grouped[:, unit_c(k) * UNIT_IN : (unit_c(k) + units) * UNIT_IN],
+                    scalar1=-2.0, scalar2=None, op0=ALU.mult,
+                )
 
         def quantise_coeffs():
-            for first, last in ((0, 2 * BASES), (2 * BASES, N_UNITS)):
+            for v in range(N_WINDOWS):
                 nc.vector.quantize_mx(
-                    out=c_codes[:, first * FEATURES : last * FEATURES].bitcast(E4M3_X4),
-                    scales=c_scales[:, first * FEATURES : last * FEATURES],
-                    in_=c_grouped[:, first * UNIT_IN : last * UNIT_IN],
+                    out=c_codes[:, v, :].bitcast(E4M3_X4),
+                    scales=c_scales[:, v, 0:P],
+                    in_=c_grouped[:, 2 * v * UNIT_IN : (2 * v + 2) * UNIT_IN],
                 )
 
         grad_tiles = {}
@@ -229,7 +229,7 @@ def tile_kan_layer_t_kernel(tc, x, spline_coeffs, grad_out, out):
             chunks[n]["tau_t"] = tau_t
 
         def group_grad(n):
-            grouped = three.tile([P, PACK * CHUNK], BF16, align_bytes=64, name="grouped")
+            grouped = three.tile([P, PACK * CHUNK], BF16, align_bytes=256, name="grouped")
             grouped_words = grouped[:].bitcast(F32)
             for b in range(2):
                 nc.scalar.copy(
@@ -239,8 +239,8 @@ def tile_kan_layer_t_kernel(tc, x, spline_coeffs, grad_out, out):
             chunks[n]["grouped"] = grouped
 
         def quantise_grad(n):
-            g_codes = two.tile([P, CHUNK], U32, align_bytes=64, name="g_codes")
-            g_scales = two.tile([P, CHUNK], U8, align_bytes=64, name="g_scales")
+            g_codes = two.tile([P, CHUNK], U32, align_bytes=256, name="g_codes")
+            g_scales = two.tile([P, CHUNK], U8, align_bytes=256, name="g_scales")
             nc.vector.quantize_mx(out=g_codes[:].bitcast(E5M2_X4), scales=g_scales[:], in_=chunks[n]["grouped"][:])
             chunks[n]["g_codes"] = g_codes
             chunks[n]["g_scales"] = g_scales
@@ -258,11 +258,11 @@ def tile_kan_layer_t_kernel(tc, x, spline_coeffs, grad_out, out):
             w = ps_w.tile([P, CHUNK], F32, name="w")
             units = blocks[b][3]
             for s, unit in enumerate(units):
-                first = unit * FEATURES
+                v = unit // 2
                 nc.tensor.matmul_mx(
                     out=w[:],
-                    lhsT=c_codes[:, first : first + P].bitcast(E4M3_X4),
-                    lhsT_scale=c_scales[:, first : first + P],
+                    lhsT=c_codes[:, v, :].bitcast(E4M3_X4),
+                    lhsT_scale=c_scales[:, v, 0:P],
                     rhs=chunks[n]["g_codes"][:].bitcast(E5M2_X4),
                     rhs_scale=chunks[n]["g_scales"][:],
                     start=(s == 0),

@@ -28,8 +28,8 @@ N_CHUNKS = TOKENS // CHUNK
 INV_H = 5.5
 KNOTS_SPAN = 11.0
 
-N_UNITS = 2 * BASES
-N_WINDOWS = BASES
+N_UNITS = 2 * BASES + 2
+N_WINDOWS = BASES + 1
 UNIT_IN = FEATURES * PACK
 SCALE_STRIDE = 256
 
@@ -42,29 +42,48 @@ def unit_c(k):
     return BASES + (BASES - k) % BASES
 
 
+def unit_p(k):
+    return 2 * BASES + (BASES - 1 - k)
+
+
 def make_blocks():
     return (
-        (4, 3, 2.0, (unit_c(4), unit_n(3), unit_c(2))),
-        (6, 5, 2.0, (unit_c(6), unit_n(5), unit_c(4))),
-        (2, 1, 2.0, (unit_c(2), unit_n(1))),
-        (8, 7, 2.0, (unit_n(7), unit_c(6))),
-        (0, 7, 4.0, (unit_c(0),)),
+        (0, 2.0, (unit_c(4), unit_n(3), unit_c(2))),
+        (1, 2.0, (unit_c(4), unit_n(5), unit_p(7))),
+        (2, 2.0, (unit_c(2), unit_n(1))),
+        (1, 4.0, (unit_c(6), unit_n(7))),
+        (3, 4.0, (unit_c(0),)),
     )
+
+
+RAMP_KNOTS = ((4, 3), (6, 5), (2, 1), (0, 7))
+N_RAMPS = 4
 
 
 N_BLOCKS = 5
 W_BANKS = 4
 
-SECOND_PAIR_ON_GPSIMD = 2
-SECOND_PAIR_ON_VECTOR = 1
+GA = (4, 4)
+GB = (1, 2)
+VB = (4, 4)
+V3 = (0, 0)
+V01 = (0, 0)
+GRAD_LEAD = 3
+JOIN_AT = 4
+T_ORDER = (0, 1, 2)
+S_TANH = (5, 3)
+S_M = (4, 1)
+S_ABS = (3, 0)
+S_FACTOR = (0, 3)
+V_Y = (4, 1)
+V_YY = (3, 1)
+REST_FIRST = True
+FINISH_LAST = False
+ODD_AT = 3
 
 LEAD_LOAD = 8
-LEAD_TANH = 5
-LEAD_WRAP = 4
-LEAD_PARABOLA = 3
 LEAD_TAU = 2
-FIRST_ROUND = -LEAD_TANH
-RELUS_BEFORE_SUMS = 3
+FIRST_ROUND = -9
 
 
 def tile_kan_layer_t_kernel(tc, x, spline_coeffs, grad_out, out):
@@ -75,6 +94,8 @@ def tile_kan_layer_t_kernel(tc, x, spline_coeffs, grad_out, out):
         gpool = ctx.enter_context(tc.tile_pool(name="gpool", bufs=4))
         two = ctx.enter_context(tc.tile_pool(name="two", bufs=2))
         three = ctx.enter_context(tc.tile_pool(name="three", bufs=3))
+        four = ctx.enter_context(tc.tile_pool(name="four", bufs=5))
+        results = ctx.enter_context(tc.tile_pool(name="results", bufs=N_GROUPS))
         ps_grad = ctx.enter_context(tc.psum_pool(name="ps_grad", bufs=2))
         ps_tau = ctx.enter_context(tc.psum_pool(name="ps_tau", bufs=1))
         ps_w = ctx.enter_context(tc.psum_pool(name="ps_w", bufs=W_BANKS))
@@ -96,7 +117,7 @@ def tile_kan_layer_t_kernel(tc, x, spline_coeffs, grad_out, out):
         half_span = const.tile([P, 1], F32)
         nc.vector.memset(half_span[:], 0.5 * INV_H)
         ramp_bias = const.tile([P, N_BLOCKS], F32)
-        for b, (even_knot, odd_knot, width, units) in enumerate(blocks):
+        for b, (even_knot, odd_knot) in enumerate(RAMP_KNOTS):
             nc.vector.memset(ramp_bias[0:64, b : b + 1], -1.0 * even_knot)
             nc.vector.memset(ramp_bias[64:128, b : b + 1], KNOTS_SPAN - odd_knot)
 
@@ -116,6 +137,11 @@ def tile_kan_layer_t_kernel(tc, x, spline_coeffs, grad_out, out):
                     in0=c_grouped[:, unit_c(k) * UNIT_IN : (unit_c(k) + units) * UNIT_IN],
                     scalar1=-2.0, scalar2=None, op0=ALU.mult,
                 )
+            nc.vector.tensor_scalar(
+                out=c_grouped[:, unit_p(7) * UNIT_IN : (unit_p(7) + 2) * UNIT_IN],
+                in0=c_grouped[:, unit_c(7) * UNIT_IN : (unit_c(7) + 2) * UNIT_IN],
+                scalar1=2.0, scalar2=None, op0=ALU.mult,
+            )
 
         def quantise_coeffs():
             for v in range(N_WINDOWS):
@@ -146,14 +172,14 @@ def tile_kan_layer_t_kernel(tc, x, spline_coeffs, grad_out, out):
             return (slice(0, GROUP_COLS),)
 
         def tanh_step(g):
-            th = three.tile([P, GROUP_COLS], F32, name="th")
+            th = four.tile([P, GROUP_COLS], F32, name="th")
             x_cols = x_sb[:, g, :, :].rearrange("p t i -> p (t i)")
             for cols in pieces(g):
                 nc.scalar.activation(out=th[:, cols], in_=x_cols[:, cols], func=ACT.Tanh)
             groups[g] = {"th": th}
 
         def round_step(g):
-            m_int = two.tile([P, GROUP_COLS], U32, name="m_int")
+            m_int = three.tile([P, GROUP_COLS], U32, name="m_int")
             for cols in pieces(g):
                 nc.scalar.activation(
                     out=m_int[:, cols], in_=groups[g]["th"][:, cols], func=ACT.Copy, bias=0.5 * INV_H, scale=0.5 * INV_H
@@ -166,7 +192,7 @@ def tile_kan_layer_t_kernel(tc, x, spline_coeffs, grad_out, out):
             groups[g]["factor"] = factor
 
         def wrap_step(g):
-            y = two.tile([P, GROUP_COLS], F32, name="y")
+            y = three.tile([P, GROUP_COLS], F32, name="y")
             for cols in pieces(g):
                 nc.vector.scalar_tensor_tensor(
                     out=y[:, cols], in0=groups[g]["m_int"][:, cols].bitcast(I32), scalar=-2.0 / INV_H,
@@ -175,7 +201,7 @@ def tile_kan_layer_t_kernel(tc, x, spline_coeffs, grad_out, out):
             groups[g]["y"] = y
 
         def abs_step(g):
-            abs_y = two.tile([P, GROUP_COLS], F32, name="abs_y")
+            abs_y = three.tile([P, GROUP_COLS], F32, name="abs_y")
             for cols in pieces(g):
                 nc.scalar.activation(
                     out=abs_y[:, cols], in_=groups[g]["y"][:, cols], func=ACT.Abs, bias=half_span[:, 0:1], scale=0.5 * INV_H
@@ -183,7 +209,7 @@ def tile_kan_layer_t_kernel(tc, x, spline_coeffs, grad_out, out):
             groups[g]["abs_y"] = abs_y
 
         def parabola_step(g):
-            y_abs_y = two.tile([P, GROUP_COLS], F32, name="y_abs_y")
+            y_abs_y = three.tile([P, GROUP_COLS], F32, name="y_abs_y")
             for cols in pieces(g):
                 nc.vector.scalar_tensor_tensor(
                     out=y_abs_y[:, cols], in0=groups[g]["y"][:, cols], scalar=1.0, in1=groups[g]["abs_y"][:, cols],
@@ -218,7 +244,7 @@ def tile_kan_layer_t_kernel(tc, x, spline_coeffs, grad_out, out):
                     for u in range(2):
                         nc.tensor.transpose(grad_t[:, a, u, :], words[:, P * u : P * u + P], ident[:])
                 banks.append(grad_t)
-            chunks[n] = {"grad_t": banks, "w": {}, "product": {}}
+            chunks[n] = {"grad_t": banks, "w": {}, "product": {}, "sum_of": {}, "ap": {}}
 
         def transpose_tau(n):
             g, t0 = first_tile(n)
@@ -247,7 +273,8 @@ def tile_kan_layer_t_kernel(tc, x, spline_coeffs, grad_out, out):
 
         def ramp_up(n, b):
             if b == 0:
-                ramp = two.tile([P, N_BLOCKS, CHUNK], F32, name="ramp")
+                chunks[n]["terms"] = [[(k,) for k in range(N_BLOCKS)] for a in range(CHUNK_TILES)]
+                ramp = two.tile([P, N_RAMPS, CHUNK], F32, name="ramp")
                 chunks[n]["ramp"] = ramp
             nc.scalar.activation(
                 out=chunks[n]["ramp"][:, b, :], in_=chunks[n]["tau_t"][:], func=ACT.Relu,
@@ -256,7 +283,7 @@ def tile_kan_layer_t_kernel(tc, x, spline_coeffs, grad_out, out):
 
         def multiply_mx(n, b):
             w = ps_w.tile([P, CHUNK], F32, name="w")
-            units = blocks[b][3]
+            units = blocks[b][2]
             for s, unit in enumerate(units):
                 v = unit // 2
                 nc.tensor.matmul_mx(
@@ -273,47 +300,41 @@ def tile_kan_layer_t_kernel(tc, x, spline_coeffs, grad_out, out):
         def product(n, b):
             prod = two.tile([P, CHUNK], F32, name="prod%d" % b)
             nc.vector.scalar_tensor_tensor(
-                out=prod[:], in0=chunks[n]["ramp"][:, b, :], scalar=blocks[b][2], in1=chunks[n]["w"][b][:],
+                out=prod[:], in0=chunks[n]["ramp"][:, blocks[b][0], :], scalar=blocks[b][1], in1=chunks[n]["w"][b][:],
                 op0=ALU.min, op1=ALU.mult,
             )
             chunks[n]["product"][b] = prod
 
-        def add_on_gpsimd(n, b, n_tiles):
-            pair = two.tile([P, P * n_tiles], F32, name="pair%d" % b)
-            nc.gpsimd.tensor_tensor(
-                out=pair[:], in0=chunks[n]["product"][b - 1][:, 0 : P * n_tiles],
-                in1=chunks[n]["product"][b][:, 0 : P * n_tiles], op=ALU.add,
-            )
-            chunks[n]["pair%d" % b] = pair
-
-        def add_on_vector(n):
-            cols = slice(P * SECOND_PAIR_ON_GPSIMD, P * (SECOND_PAIR_ON_GPSIMD + SECOND_PAIR_ON_VECTOR))
-            rest = two.tile([P, P * SECOND_PAIR_ON_VECTOR], F32, name="rest")
-            nc.vector.tensor_tensor(
-                out=rest[:], in0=chunks[n]["product"][2][:, cols], in1=chunks[n]["product"][3][:, cols], op=ALU.add
-            )
-            chunks[n]["rest"] = rest
+        def add(n, engine, first, second, tiles, tag):
+            if tiles[1] <= tiles[0]:
+                return
+            key = first + second
+            total = two.tile([P, CHUNK], F32, name=tag, tag=tag)
+            cols = slice(P * tiles[0], P * tiles[1])
+            terms = [chunks[n]["sum_of"][b] if b in chunks[n]["sum_of"] else chunks[n]["product"][b[0]][:] for b in (first, second)]
+            engine.tensor_tensor(out=total[:, cols], in0=terms[0][:, cols], in1=terms[1][:, cols], op=ALU.add)
+            for a in range(tiles[0], tiles[1]):
+                left = chunks[n]["terms"][a]
+                left.remove(first)
+                left.remove(second)
+                left.append(key)
+                chunks[n]["ap"][key, a] = total[:, P * a : P * a + P]
+            chunks[n]["sum_of"][key] = total[:]
 
         def sum_blocks(n):
             sums = ps_sum.tile([P, CHUNK_TILES, 2, FEATURES], F32, name="sums")
             for a in range(CHUNK_TILES):
                 cols = slice(P * a, P * a + P)
-                after_gpsimd = a - SECOND_PAIR_ON_GPSIMD
-                if after_gpsimd < 0:
-                    second_pair = [chunks[n]["pair3"][:, cols]]
-                elif after_gpsimd < SECOND_PAIR_ON_VECTOR:
-                    second_pair = [chunks[n]["rest"][:, P * after_gpsimd : P * after_gpsimd + P]]
-                else:
-                    second_pair = [chunks[n]["product"][2][:, cols], chunks[n]["product"][3][:, cols]]
-                terms = [chunks[n]["pair1"][:, cols]] + second_pair + [chunks[n]["product"][N_BLOCKS - 1][:, cols]]
-                for s, term in enumerate(terms):
+                left = sorted(chunks[n]["terms"][a], key=lambda b: (b != (4,), -len(b), -b[-1]))
+                for s, b in enumerate(left):
+                    term = chunks[n]["ap"][b, a] if len(b) > 1 else chunks[n]["product"][b[0]][:, cols]
                     nc.tensor.matmul(
                         sums[:, a, :, :].rearrange("p h i -> p (h i)"),
                         lhsT=term,
                         rhs=ident[:],
                         is_transpose=True,
                         start=(s == 0),
-                        stop=(s == len(terms) - 1),
+                        stop=(s == len(left) - 1),
                     )
             chunks[n]["sums"] = sums
 
@@ -333,7 +354,7 @@ def tile_kan_layer_t_kernel(tc, x, spline_coeffs, grad_out, out):
         def finish(n):
             g, t0 = first_tile(n)
             if t0 == 0:
-                result = two.tile([P, GROUP_TILES, FEATURES], F32, name="result")
+                result = results.tile([P, GROUP_TILES, FEATURES], F32, name="result")
                 groups[g]["result"] = result
             result = groups[g]["result"]
             nc.vector.scalar_tensor_tensor(
@@ -356,6 +377,29 @@ def tile_kan_layer_t_kernel(tc, x, spline_coeffs, grad_out, out):
         def groups_in_round(n, lead):
             return [g for g in range(N_GROUPS) if max(2 * g - lead, FIRST_ROUND) == n]
 
+        def vector_adds(n):
+            gb, vb, v3 = GB[n % 2], VB[n % 2], V3[n % 2]
+            add(n, nc.vector, (2,), (3,), (gb, vb), "rest")
+            if V01[n % 2]:
+                add(n, nc.vector, (0, 1), (4,), (0, V01[n % 2]), "sum014")
+            if v3:
+                if vb > gb:
+                    add(n, nc.vector, (2, 3), (4,), (vb - v3, vb), "rest4")
+                else:
+                    add(n, nc.vector, (3,), (4,), (4 - v3, 4), "rest4")
+
+        def scalar_prep(n, slot):
+            for (lead, where), step in ((S_ABS, abs_step), (S_M, round_step), (S_FACTOR, factor_step), (S_TANH, tanh_step)):
+                if where == slot:
+                    for g in groups_in_round(n, lead):
+                        step(g)
+
+        def vector_prep(n, slot):
+            for (lead, where), step in ((V_YY, parabola_step), (V_Y, wrap_step)):
+                if where == slot:
+                    for g in groups_in_round(n, lead):
+                        step(g)
+
         with tc.manual_schedule():
             for n in range(FIRST_ROUND, N_CHUNKS + 1):
                 for g in groups_in_round(n, LEAD_LOAD):
@@ -364,60 +408,61 @@ def tile_kan_layer_t_kernel(tc, x, spline_coeffs, grad_out, out):
                         nc.sync.dma_start(out=x_sb[:, 2:4, :, :], in_=x_view[:, 2:4, :, :])
                     if g == 1:
                         nc.sync.dma_start(out=x_sb[:, 4:N_GROUPS, :, :], in_=x_view[:, 4:N_GROUPS, :, :])
-                if is_chunk(n + 1):
-                    transpose_tau(n + 1)
-                if is_chunk(n + 3):
-                    transpose_grad(n + 3)
-                if is_chunk(n - 1):
-                    sum_blocks(n - 1)
-
+                for step in T_ORDER:
+                    if step == 0 and is_chunk(n + 1):
+                        transpose_tau(n + 1)
+                    if step == 1 and is_chunk(n + GRAD_LEAD):
+                        transpose_grad(n + GRAD_LEAD)
+                    if step == 2 and is_chunk(n - 1):
+                        sum_blocks(n - 1)
                 if n == FIRST_ROUND:
                     for k in range(BASES):
                         regroup_coeffs(k)
-
                 if is_chunk(n + 1):
                     quantise_grad(n + 1)
+                vector_prep(n, 0)
                 for g in groups_in_round(n, LEAD_TAU):
                     tau_step(g)
                 if n == -LEAD_TAU:
                     quantise_coeffs()
-
-                for g in groups_in_round(n, LEAD_PARABOLA):
-                    abs_step(g)
-                for b in range(N_BLOCKS):
-                    if b == RELUS_BEFORE_SUMS:
+                scalar_prep(n, 0)
+                for b in range(N_RAMPS):
+                    if b == ODD_AT:
                         if is_chunk(n - 1):
                             empty_odd_half(n - 1)
-                        for g in groups_in_round(n, LEAD_WRAP):
-                            round_step(g)
+                        scalar_prep(n, 1)
                     if is_chunk(n + 1):
                         ramp_up(n + 1, b)
-                if is_chunk(n + 3):
-                    group_grad(n + 3)
-                for g in groups_in_round(n, LEAD_TAU):
-                    factor_step(g)
-                for g in groups_in_round(n, LEAD_TANH):
-                    tanh_step(g)
-
+                if ODD_AT == N_RAMPS:
+                    if is_chunk(n - 1):
+                        empty_odd_half(n - 1)
+                    scalar_prep(n, 1)
+                scalar_prep(n, 2)
+                if is_chunk(n + GRAD_LEAD):
+                    group_grad(n + GRAD_LEAD)
+                scalar_prep(n, 3)
                 for b in range(N_BLOCKS):
-                    if b == N_BLOCKS - 1 and is_chunk(n - 1):
+                    if b == JOIN_AT and is_chunk(n - 1):
                         join_halves(n - 1)
                     if is_chunk(n):
                         product(n, b)
                         if b == 1:
-                            add_on_gpsimd(n, b, CHUNK_TILES)
+                            add(n, nc.gpsimd, (0,), (1,), (0, GA[n % 2]), "pair1")
                         if b == 3:
-                            add_on_gpsimd(n, b, SECOND_PAIR_ON_GPSIMD)
+                            add(n, nc.gpsimd, (2,), (3,), (0, GB[n % 2]), "pair3")
                     ahead, block = (n, N_BLOCKS - 1) if b == 0 else (n + 1, b - 1)
                     if is_chunk(ahead):
                         multiply_mx(ahead, block)
-                if is_chunk(n):
-                    add_on_vector(n)
-                for g in groups_in_round(n, LEAD_WRAP):
-                    wrap_step(g)
-                if n == -LEAD_WRAP:
+                if JOIN_AT == 5 and is_chunk(n - 1):
+                    join_halves(n - 1)
+                if REST_FIRST and is_chunk(n):
+                    vector_adds(n)
+                if not FINISH_LAST and is_chunk(n - 1):
+                    finish(n - 1)
+                vector_prep(n, 1)
+                if n == -5:
                     scale_coeffs()
-                for g in groups_in_round(n, LEAD_PARABOLA):
-                    parabola_step(g)
-                if is_chunk(n - 1):
+                if not REST_FIRST and is_chunk(n):
+                    vector_adds(n)
+                if FINISH_LAST and is_chunk(n - 1):
                     finish(n - 1)

@@ -64,8 +64,8 @@ N_BLOCKS = 5
 W_BANKS = 4
 
 GA = (4, 4)
-GB = (1, 2)
-VB = (4, 4)
+GB = (2, 2)
+VB = (3, 3)
 V3 = (0, 0)
 V01 = (0, 0)
 GRAD_LEAD = 3
@@ -74,7 +74,7 @@ T_ORDER = (0, 1, 2)
 S_TANH = (5, 3)
 S_M = (4, 1)
 S_ABS = (3, 0)
-S_FACTOR = (0, 3)
+S_FACTOR = (2, 3)
 V_Y = (4, 1)
 V_YY = (3, 1)
 REST_FIRST = True

@@ -27,6 +27,8 @@ CHUNK = P * CHUNK_TILES
 N_CHUNKS = TOKENS // CHUNK
 INV_H = 5.5
 KNOTS_SPAN = 11.0
+COORD_SCALE = 22.0
+YY_ON_G = True
 
 N_UNITS = 2 * BASES + 2
 N_WINDOWS = BASES + 1
@@ -64,19 +66,19 @@ N_BLOCKS = 5
 W_BANKS = 4
 
 GA = (4, 4)
-GB = (2, 2)
-VB = (3, 3)
+GB = (1, 2)
+VB = (4, 4)
 V3 = (0, 0)
 V01 = (0, 0)
 GRAD_LEAD = 3
 JOIN_AT = 4
 T_ORDER = (0, 1, 2)
-S_TANH = (5, 3)
-S_M = (4, 1)
-S_ABS = (3, 0)
+S_TANH = (7, 3)
+S_M = (6, 3)
+S_ABS = (4, 3)
 S_FACTOR = (2, 3)
-V_Y = (4, 1)
-V_YY = (3, 1)
+V_Y = (5, 1)
+V_YY = (3, 0)
 REST_FIRST = True
 FINISH_LAST = False
 ODD_AT = 3
@@ -115,11 +117,11 @@ def tile_kan_layer_t_kernel(tc, x, spline_coeffs, grad_out, out):
         ident = const.tile([P, P], F32)
         make_identity(nc, ident[:])
         half_span = const.tile([P, 1], F32)
-        nc.vector.memset(half_span[:], 0.5 * INV_H)
+        nc.vector.memset(half_span[:], -1.0)
         ramp_bias = const.tile([P, N_BLOCKS], F32)
         for b, (even_knot, odd_knot) in enumerate(RAMP_KNOTS):
             nc.vector.memset(ramp_bias[0:64, b : b + 1], -1.0 * even_knot)
-            nc.vector.memset(ramp_bias[64:128, b : b + 1], KNOTS_SPAN - odd_knot)
+            nc.vector.memset(ramp_bias[64:128, b : b + 1], -1.0 * odd_knot)
 
         c_grouped = const.tile([P, N_UNITS * UNIT_IN], BF16, align_bytes=256)
         c_grouped_by_unit = c_grouped[:].rearrange("q (s i t) -> q s i t", s=N_UNITS, t=PACK)
@@ -175,27 +177,27 @@ def tile_kan_layer_t_kernel(tc, x, spline_coeffs, grad_out, out):
             th = four.tile([P, GROUP_COLS], F32, name="th")
             x_cols = x_sb[:, g, :, :].rearrange("p t i -> p (t i)")
             for cols in pieces(g):
-                nc.scalar.activation(out=th[:, cols], in_=x_cols[:, cols], func=ACT.Tanh)
+                nc.scalar.activation(out=th[:, cols], in_=x_cols[:, cols], func=ACT.Sigmoid, scale=2.0)
             groups[g] = {"th": th}
 
         def round_step(g):
             m_int = three.tile([P, GROUP_COLS], U32, name="m_int")
             for cols in pieces(g):
                 nc.scalar.activation(
-                    out=m_int[:, cols], in_=groups[g]["th"][:, cols], func=ACT.Copy, bias=0.5 * INV_H, scale=0.5 * INV_H
+                    out=m_int[:, cols], in_=groups[g]["th"][:, cols], func=ACT.Copy, scale=0.5 * KNOTS_SPAN
                 )
             groups[g]["m_int"] = m_int
 
         def factor_step(g):
             factor = three.tile([P, GROUP_COLS], F32, name="factor")
-            nc.scalar.activation(out=factor[:], in_=groups[g]["th"][:], func=ACT.Square, scale=math.sqrt(0.5 * INV_H))
+            nc.scalar.activation(out=factor[:], in_=groups[g]["th"][:], func=ACT.Square, bias=half_span[:, 0:1], scale=2.0)
             groups[g]["factor"] = factor
 
         def wrap_step(g):
             y = three.tile([P, GROUP_COLS], F32, name="y")
             for cols in pieces(g):
                 nc.vector.scalar_tensor_tensor(
-                    out=y[:, cols], in0=groups[g]["m_int"][:, cols].bitcast(I32), scalar=-2.0 / INV_H,
+                    out=y[:, cols], in0=groups[g]["m_int"][:, cols].bitcast(I32), scalar=-2.0 / KNOTS_SPAN,
                     in1=groups[g]["th"][:, cols], op0=ALU.mult, op1=ALU.add,
                 )
             groups[g]["y"] = y
@@ -204,17 +206,18 @@ def tile_kan_layer_t_kernel(tc, x, spline_coeffs, grad_out, out):
             abs_y = three.tile([P, GROUP_COLS], F32, name="abs_y")
             for cols in pieces(g):
                 nc.scalar.activation(
-                    out=abs_y[:, cols], in_=groups[g]["y"][:, cols], func=ACT.Abs, bias=half_span[:, 0:1], scale=0.5 * INV_H
+                    out=abs_y[:, cols], in_=groups[g]["y"][:, cols], func=ACT.Abs, scale=0.5 * KNOTS_SPAN
                 )
             groups[g]["abs_y"] = abs_y
 
         def parabola_step(g):
             y_abs_y = three.tile([P, GROUP_COLS], F32, name="y_abs_y")
             for cols in pieces(g):
-                nc.vector.scalar_tensor_tensor(
-                    out=y_abs_y[:, cols], in0=groups[g]["y"][:, cols], scalar=1.0, in1=groups[g]["abs_y"][:, cols],
-                    op0=ALU.add, op1=ALU.mult,
-                )
+                if YY_ON_G and g > 1:
+                    nc.vector.memset(y_abs_y[:, 0:1], 0.0)
+                    nc.gpsimd.tensor_tensor(out=y_abs_y[:, cols], in0=groups[g]["y"][:, cols], in1=groups[g]["abs_y"][:, cols], op=ALU.mult)
+                else:
+                    nc.vector.tensor_tensor(out=y_abs_y[:, cols], in0=groups[g]["y"][:, cols], in1=groups[g]["abs_y"][:, cols], op=ALU.mult)
             groups[g]["y_abs_y"] = y_abs_y
 
         def tau_step(g):
@@ -223,7 +226,7 @@ def tile_kan_layer_t_kernel(tc, x, spline_coeffs, grad_out, out):
                 tiles = slice(cols.start // FEATURES, cols.stop // FEATURES)
                 nc.vector.scalar_tensor_tensor(
                     out=tau[:, tiles, 0:FEATURES], in0=by_tile(groups[g]["m_int"][:, cols].bitcast(I32)),
-                    scalar=2.0 / KNOTS_SPAN, in1=by_tile(groups[g]["y_abs_y"][:, cols]), op0=ALU.mult, op1=ALU.add,
+                    scalar=2.0 / COORD_SCALE, in1=by_tile(groups[g]["y_abs_y"][:, cols]), op0=ALU.mult, op1=ALU.add,
                 )
                 nc.gpsimd.tensor_tensor(
                     out=tau[:, tiles, FEATURES : 2 * FEATURES], in0=by_tile(groups[g]["th"][:, cols]),
@@ -278,7 +281,7 @@ def tile_kan_layer_t_kernel(tc, x, spline_coeffs, grad_out, out):
                 chunks[n]["ramp"] = ramp
             nc.scalar.activation(
                 out=chunks[n]["ramp"][:, b, :], in_=chunks[n]["tau_t"][:], func=ACT.Relu,
-                bias=ramp_bias[:, b : b + 1], scale=KNOTS_SPAN,
+                bias=ramp_bias[:, b : b + 1], scale=COORD_SCALE,
             )
 
         def multiply_mx(n, b):
@@ -340,13 +343,13 @@ def tile_kan_layer_t_kernel(tc, x, spline_coeffs, grad_out, out):
 
         def empty_odd_half(n):
             odd_half = three.tile([P, CHUNK_TILES, FEATURES], F32, name="odd_half")
-            nc.scalar.activation(out=odd_half[:], in_=chunks[n]["sums"][:, :, 1, :], func=ACT.Copy, scale=-1.0)
+            nc.scalar.activation(out=odd_half[:], in_=chunks[n]["sums"][:, :, 1, :], func=ACT.Copy, scale=-0.5 * INV_H)
             chunks[n]["odd_half"] = odd_half
 
         def join_halves(n):
             joined = two.tile([P, CHUNK_TILES, FEATURES], F32, name="joined")
             nc.vector.scalar_tensor_tensor(
-                out=joined[:], in0=chunks[n]["sums"][:, :, 0, :], scalar=-1.0, in1=chunks[n]["odd_half"][:],
+                out=joined[:], in0=chunks[n]["sums"][:, :, 0, :], scalar=-0.5 * INV_H, in1=chunks[n]["odd_half"][:],
                 op0=ALU.mult, op1=ALU.add,
             )
             chunks[n]["joined"] = joined
@@ -360,7 +363,7 @@ def tile_kan_layer_t_kernel(tc, x, spline_coeffs, grad_out, out):
             nc.vector.scalar_tensor_tensor(
                 out=result[:, t0 : t0 + CHUNK_TILES, :].rearrange("p a i -> p (a i)"),
                 in0=groups[g]["factor"][:, t0 * FEATURES : (t0 + CHUNK_TILES) * FEATURES],
-                scalar=0.5 * INV_H,
+                scalar=1.0,
                 in1=chunks[n]["joined"][:].rearrange("p a i -> p (a i)"),
                 op0=ALU.subtract,
                 op1=ALU.mult,
@@ -460,7 +463,7 @@ def tile_kan_layer_t_kernel(tc, x, spline_coeffs, grad_out, out):
                 if not FINISH_LAST and is_chunk(n - 1):
                     finish(n - 1)
                 vector_prep(n, 1)
-                if n == -5:
+                if n == -4:
                     scale_coeffs()
                 if not REST_FIRST and is_chunk(n):
                     vector_adds(n)

@@ -1,4 +1,3 @@
-import math
 from contextlib import ExitStack
 
 import concourse.mybir as mybir
@@ -25,10 +24,10 @@ GROUP_COLS = GROUP_TILES * FEATURES
 CHUNK_TILES = 4
 CHUNK = P * CHUNK_TILES
 N_CHUNKS = TOKENS // CHUNK
+LAST_CHUNK = N_CHUNKS - 1
 INV_H = 5.5
 KNOTS_SPAN = 11.0
 COORD_SCALE = 22.0
-YY_ON_G = True
 
 N_UNITS = 2 * BASES + 2
 N_WINDOWS = BASES + 1
@@ -65,27 +64,16 @@ N_RAMPS = 4
 N_BLOCKS = 5
 W_BANKS = 4
 
-GA = (4, 4)
-GB = (1, 2)
-VB = (4, 4)
-V3 = (0, 0)
-V01 = (0, 0)
-GRAD_LEAD = 3
-JOIN_AT = 4
-T_ORDER = (0, 1, 2)
-S_TANH = (7, 3)
-S_M = (6, 3)
-S_ABS = (4, 3)
-S_FACTOR = (2, 3)
-V_Y = (5, 1)
-V_YY = (3, 0)
-REST_FIRST = True
-FINISH_LAST = False
-ODD_AT = 3
+SECOND_PAIR_ON_GPSIMD = (1, 2)
+SECOND_PAIR_ENDS = (4, 4)
 
 LEAD_LOAD = 8
+LEAD_TANH = 7
+LEAD_WRAP = 5
+LEAD_PARABOLA = 3
 LEAD_TAU = 2
-FIRST_ROUND = -9
+FIRST_ROUND = -LEAD_TANH
+RELUS_BEFORE_SUMS = 3
 
 
 def tile_kan_layer_t_kernel(tc, x, spline_coeffs, grad_out, out):
@@ -96,7 +84,6 @@ def tile_kan_layer_t_kernel(tc, x, spline_coeffs, grad_out, out):
         gpool = ctx.enter_context(tc.tile_pool(name="gpool", bufs=4))
         two = ctx.enter_context(tc.tile_pool(name="two", bufs=2))
         three = ctx.enter_context(tc.tile_pool(name="three", bufs=3))
-        four = ctx.enter_context(tc.tile_pool(name="four", bufs=5))
         results = ctx.enter_context(tc.tile_pool(name="results", bufs=N_GROUPS))
         ps_grad = ctx.enter_context(tc.psum_pool(name="ps_grad", bufs=2))
         ps_tau = ctx.enter_context(tc.psum_pool(name="ps_tau", bufs=1))
@@ -116,8 +103,8 @@ def tile_kan_layer_t_kernel(tc, x, spline_coeffs, grad_out, out):
 
         ident = const.tile([P, P], F32)
         make_identity(nc, ident[:])
-        half_span = const.tile([P, 1], F32)
-        nc.vector.memset(half_span[:], -1.0)
+        minus_one = const.tile([P, 1], F32)
+        nc.vector.memset(minus_one[:], -1.0)
         ramp_bias = const.tile([P, N_BLOCKS], F32)
         for b, (even_knot, odd_knot) in enumerate(RAMP_KNOTS):
             nc.vector.memset(ramp_bias[0:64, b : b + 1], -1.0 * even_knot)
@@ -130,7 +117,8 @@ def tile_kan_layer_t_kernel(tc, x, spline_coeffs, grad_out, out):
         c_scales = const.tile([P, N_WINDOWS, SCALE_STRIDE], U8, align_bytes=256)
 
         def regroup_coeffs(k):
-            nc.vector.tensor_copy(out=c_grouped_by_unit[:, unit_c(k), :, :], in_=c_rows_by_k[:, k, :, :])
+            copy = nc.scalar.copy if k in (0, 6, 7) else nc.vector.tensor_copy
+            copy(out=c_grouped_by_unit[:, unit_c(k), :, :], in_=c_rows_by_k[:, k, :, :])
 
         def scale_coeffs():
             for k, units in ((BASES - 1, BASES - 1), (0, 1)):
@@ -145,8 +133,8 @@ def tile_kan_layer_t_kernel(tc, x, spline_coeffs, grad_out, out):
                 scalar1=2.0, scalar2=None, op0=ALU.mult,
             )
 
-        def quantise_coeffs():
-            for v in range(N_WINDOWS):
+        def quantise_coeffs(units):
+            for v in [unit // 2 for unit in units]:
                 nc.vector.quantize_mx(
                     out=c_codes[:, v, :].bitcast(E4M3_X4),
                     scales=c_scales[:, v, 0:P],
@@ -159,10 +147,9 @@ def tile_kan_layer_t_kernel(tc, x, spline_coeffs, grad_out, out):
 
         def load_grad(g):
             grad_sb = gpool.tile([P, GROUP_TILES, OUT_FEATURES], BF16, name="grad_sb")
-            nc.sync.dma_start(
-                out=grad_sb[:],
-                in_=grad_out[g * GROUP : (g + 1) * GROUP, :].rearrange("(p t) o -> p t o", t=GROUP_TILES),
-            )
+            view = grad_out[g * GROUP : (g + 1) * GROUP, :].rearrange("(p t) o -> p t o", t=GROUP_TILES)
+            for tiles in (slice(0, CHUNK_TILES), slice(CHUNK_TILES, GROUP_TILES)) if g == 0 else (slice(0, GROUP_TILES),):
+                nc.sync.dma_start(out=grad_sb[:, tiles, :], in_=view[:, tiles, :])
             grad_tiles[g] = grad_sb
 
         def by_tile(ap):
@@ -174,14 +161,14 @@ def tile_kan_layer_t_kernel(tc, x, spline_coeffs, grad_out, out):
             return (slice(0, GROUP_COLS),)
 
         def tanh_step(g):
-            th = four.tile([P, GROUP_COLS], F32, name="th")
+            th = three.tile([P, GROUP_COLS], F32, name="th")
             x_cols = x_sb[:, g, :, :].rearrange("p t i -> p (t i)")
             for cols in pieces(g):
                 nc.scalar.activation(out=th[:, cols], in_=x_cols[:, cols], func=ACT.Sigmoid, scale=2.0)
             groups[g] = {"th": th}
 
         def round_step(g):
-            m_int = three.tile([P, GROUP_COLS], U32, name="m_int")
+            m_int = two.tile([P, GROUP_COLS], U32, name="m_int")
             for cols in pieces(g):
                 nc.scalar.activation(
                     out=m_int[:, cols], in_=groups[g]["th"][:, cols], func=ACT.Copy, scale=0.5 * KNOTS_SPAN
@@ -190,11 +177,11 @@ def tile_kan_layer_t_kernel(tc, x, spline_coeffs, grad_out, out):
 
         def factor_step(g):
             factor = three.tile([P, GROUP_COLS], F32, name="factor")
-            nc.scalar.activation(out=factor[:], in_=groups[g]["th"][:], func=ACT.Square, bias=half_span[:, 0:1], scale=2.0)
+            nc.scalar.activation(out=factor[:], in_=groups[g]["th"][:], func=ACT.Square, bias=minus_one[:, 0:1], scale=2.0)
             groups[g]["factor"] = factor
 
         def wrap_step(g):
-            y = three.tile([P, GROUP_COLS], F32, name="y")
+            y = two.tile([P, GROUP_COLS], F32, name="y")
             for cols in pieces(g):
                 nc.vector.scalar_tensor_tensor(
                     out=y[:, cols], in0=groups[g]["m_int"][:, cols].bitcast(I32), scalar=-2.0 / KNOTS_SPAN,
@@ -203,7 +190,7 @@ def tile_kan_layer_t_kernel(tc, x, spline_coeffs, grad_out, out):
             groups[g]["y"] = y
 
         def abs_step(g):
-            abs_y = three.tile([P, GROUP_COLS], F32, name="abs_y")
+            abs_y = two.tile([P, GROUP_COLS], F32, name="abs_y")
             for cols in pieces(g):
                 nc.scalar.activation(
                     out=abs_y[:, cols], in_=groups[g]["y"][:, cols], func=ACT.Abs, scale=0.5 * KNOTS_SPAN
@@ -211,24 +198,25 @@ def tile_kan_layer_t_kernel(tc, x, spline_coeffs, grad_out, out):
             groups[g]["abs_y"] = abs_y
 
         def parabola_step(g):
-            y_abs_y = three.tile([P, GROUP_COLS], F32, name="y_abs_y")
+            y_abs_y = two.tile([P, GROUP_COLS], F32, name="y_abs_y")
             for cols in pieces(g):
-                if YY_ON_G and g > 1:
+                if g > 1:
                     nc.vector.memset(y_abs_y[:, 0:1], 0.0)
-                    nc.gpsimd.tensor_tensor(out=y_abs_y[:, cols], in0=groups[g]["y"][:, cols], in1=groups[g]["abs_y"][:, cols], op=ALU.mult)
-                else:
-                    nc.vector.tensor_tensor(out=y_abs_y[:, cols], in0=groups[g]["y"][:, cols], in1=groups[g]["abs_y"][:, cols], op=ALU.mult)
+                (nc.gpsimd if g > 1 else nc.vector).tensor_tensor(
+                    out=y_abs_y[:, cols], in0=groups[g]["y"][:, cols], in1=groups[g]["abs_y"][:, cols], op=ALU.mult
+                )
             groups[g]["y_abs_y"] = y_abs_y
 
         def tau_step(g):
             tau = three.tile([P, GROUP_TILES, 2 * FEATURES], F32, name="tau")
-            for cols in pieces(g):
-                tiles = slice(cols.start // FEATURES, cols.stop // FEATURES)
+            all_tiles = [slice(cols.start // FEATURES, cols.stop // FEATURES) for cols in pieces(g)]
+            for cols, tiles in zip(pieces(g), all_tiles):
                 nc.vector.scalar_tensor_tensor(
                     out=tau[:, tiles, 0:FEATURES], in0=by_tile(groups[g]["m_int"][:, cols].bitcast(I32)),
                     scalar=2.0 / COORD_SCALE, in1=by_tile(groups[g]["y_abs_y"][:, cols]), op0=ALU.mult, op1=ALU.add,
                 )
-                nc.gpsimd.tensor_tensor(
+            for cols, tiles in zip(pieces(g), all_tiles):
+                (nc.gpsimd if g > 0 else nc.vector).tensor_tensor(
                     out=tau[:, tiles, FEATURES : 2 * FEATURES], in0=by_tile(groups[g]["th"][:, cols]),
                     in1=tau[:, tiles, 0:FEATURES], op=ALU.subtract,
                 )
@@ -247,7 +235,7 @@ def tile_kan_layer_t_kernel(tc, x, spline_coeffs, grad_out, out):
                     for u in range(2):
                         nc.tensor.transpose(grad_t[:, a, u, :], words[:, P * u : P * u + P], ident[:])
                 banks.append(grad_t)
-            chunks[n] = {"grad_t": banks, "w": {}, "product": {}, "sum_of": {}, "ap": {}}
+            chunks[n] = {"grad_t": banks, "w": {}, "product": {}}
 
         def transpose_tau(n):
             g, t0 = first_tile(n)
@@ -276,7 +264,6 @@ def tile_kan_layer_t_kernel(tc, x, spline_coeffs, grad_out, out):
 
         def ramp_up(n, b):
             if b == 0:
-                chunks[n]["terms"] = [[(k,) for k in range(N_BLOCKS)] for a in range(CHUNK_TILES)]
                 ramp = two.tile([P, N_RAMPS, CHUNK], F32, name="ramp")
                 chunks[n]["ramp"] = ramp
             nc.scalar.activation(
@@ -308,38 +295,81 @@ def tile_kan_layer_t_kernel(tc, x, spline_coeffs, grad_out, out):
             )
             chunks[n]["product"][b] = prod
 
-        def add(n, engine, first, second, tiles, tag):
-            if tiles[1] <= tiles[0]:
-                return
-            key = first + second
-            total = two.tile([P, CHUNK], F32, name=tag, tag=tag)
-            cols = slice(P * tiles[0], P * tiles[1])
-            terms = [chunks[n]["sum_of"][b] if b in chunks[n]["sum_of"] else chunks[n]["product"][b[0]][:] for b in (first, second)]
-            engine.tensor_tensor(out=total[:, cols], in0=terms[0][:, cols], in1=terms[1][:, cols], op=ALU.add)
-            for a in range(tiles[0], tiles[1]):
-                left = chunks[n]["terms"][a]
-                left.remove(first)
-                left.remove(second)
-                left.append(key)
-                chunks[n]["ap"][key, a] = total[:, P * a : P * a + P]
-            chunks[n]["sum_of"][key] = total[:]
+        def add_on_gpsimd(n, b, n_tiles):
+            pair = two.tile([P, CHUNK], F32, name="pair%d" % b)
+            nc.gpsimd.tensor_tensor(
+                out=pair[:, 0 : P * n_tiles], in0=chunks[n]["product"][b - 1][:, 0 : P * n_tiles],
+                in1=chunks[n]["product"][b][:, 0 : P * n_tiles], op=ALU.add,
+            )
+            chunks[n]["pair%d" % b] = pair
+
+        def add_on_vector(n):
+            cols = slice(P * SECOND_PAIR_ON_GPSIMD[n % 2], P * SECOND_PAIR_ENDS[n % 2])
+            rest = two.tile([P, CHUNK], F32, name="rest")
+            nc.vector.tensor_tensor(
+                out=rest[:, cols], in0=chunks[n]["product"][2][:, cols], in1=chunks[n]["product"][3][:, cols], op=ALU.add
+            )
+            chunks[n]["rest"] = rest
 
         def sum_blocks(n):
             sums = ps_sum.tile([P, CHUNK_TILES, 2, FEATURES], F32, name="sums")
             for a in range(CHUNK_TILES):
                 cols = slice(P * a, P * a + P)
-                left = sorted(chunks[n]["terms"][a], key=lambda b: (b != (4,), -len(b), -b[-1]))
-                for s, b in enumerate(left):
-                    term = chunks[n]["ap"][b, a] if len(b) > 1 else chunks[n]["product"][b[0]][:, cols]
+                if a < SECOND_PAIR_ON_GPSIMD[n % 2]:
+                    second_pair = [chunks[n]["pair3"][:, cols]]
+                elif a < SECOND_PAIR_ENDS[n % 2]:
+                    second_pair = [chunks[n]["rest"][:, cols]]
+                else:
+                    second_pair = [chunks[n]["product"][2][:, cols], chunks[n]["product"][3][:, cols]]
+                terms = [chunks[n]["pair1"][:, cols]] + second_pair + [chunks[n]["product"][N_BLOCKS - 1][:, cols]]
+                for s, term in enumerate(terms):
                     nc.tensor.matmul(
                         sums[:, a, :, :].rearrange("p h i -> p (h i)"),
                         lhsT=term,
                         rhs=ident[:],
                         is_transpose=True,
                         start=(s == 0),
-                        stop=(s == len(left) - 1),
+                        stop=(s == len(terms) - 1),
                     )
             chunks[n]["sums"] = sums
+
+        def sum_last(n):
+            keys = ["pair1", 2, 3, N_BLOCKS - 1]
+            halves = []
+            for a in range(CHUNK_TILES):
+                if a < CHUNK_TILES - 1:
+                    bank = ps_w.tile([P, CHUNK], F32, name="w")
+                    halves.append(bank[:, 0:P].rearrange("p (h i) -> p h i", h=2))
+                else:
+                    bank = ps_sum.tile([P, CHUNK_TILES, 2, FEATURES], F32, name="sums")
+                    halves.append(bank[:, 0, :, :])
+            for part in (slice(0, 3), slice(3, 4)):
+                for a in range(CHUNK_TILES):
+                    for key in keys[part]:
+                        term = chunks[n]["pair1"] if key == "pair1" else chunks[n]["product"][key]
+                        nc.tensor.matmul(
+                            halves[a].rearrange("p h i -> p (h i)"),
+                            lhsT=term[:, P * a : P * a + P],
+                            rhs=ident[:],
+                            is_transpose=True,
+                            start=(key == keys[0]),
+                            stop=(key == keys[-1]),
+                        )
+            chunks[n]["halves"] = halves
+
+        def join_last(n):
+            odd_half = three.tile([P, CHUNK_TILES, FEATURES], F32, name="odd_half")
+            joined = two.tile([P, CHUNK_TILES, FEATURES], F32, name="joined")
+            for a in range(CHUNK_TILES):
+                nc.scalar.activation(
+                    out=odd_half[:, a, :], in_=chunks[n]["halves"][a][:, 1, :], func=ACT.Copy, scale=-0.5 * INV_H
+                )
+            for a in range(CHUNK_TILES):
+                nc.vector.scalar_tensor_tensor(
+                    out=joined[:, a, :], in0=chunks[n]["halves"][a][:, 0, :], scalar=-0.5 * INV_H,
+                    in1=odd_half[:, a, :], op0=ALU.mult, op1=ALU.add,
+                )
+            chunks[n]["joined"] = joined
 
         def empty_odd_half(n):
             odd_half = three.tile([P, CHUNK_TILES, FEATURES], F32, name="odd_half")
@@ -368,40 +398,19 @@ def tile_kan_layer_t_kernel(tc, x, spline_coeffs, grad_out, out):
                 op0=ALU.subtract,
                 op1=ALU.mult,
             )
-            if t0 != 0:
+            rows = out[g * GROUP : (g + 1) * GROUP, :].rearrange("(p t) i -> p t i", t=GROUP_TILES)
+            if g == N_GROUPS - 1:
                 nc.sync.dma_start(
-                    out=out[g * GROUP : (g + 1) * GROUP, :].rearrange("(p t) i -> p t i", t=GROUP_TILES),
-                    in_=result[:],
+                    out=rows[:, t0 : t0 + CHUNK_TILES, :], in_=result[:, t0 : t0 + CHUNK_TILES, :]
                 )
+            elif t0 != 0:
+                nc.sync.dma_start(out=rows, in_=result[:])
 
         def is_chunk(n):
             return 0 <= n < N_CHUNKS
 
         def groups_in_round(n, lead):
             return [g for g in range(N_GROUPS) if max(2 * g - lead, FIRST_ROUND) == n]
-
-        def vector_adds(n):
-            gb, vb, v3 = GB[n % 2], VB[n % 2], V3[n % 2]
-            add(n, nc.vector, (2,), (3,), (gb, vb), "rest")
-            if V01[n % 2]:
-                add(n, nc.vector, (0, 1), (4,), (0, V01[n % 2]), "sum014")
-            if v3:
-                if vb > gb:
-                    add(n, nc.vector, (2, 3), (4,), (vb - v3, vb), "rest4")
-                else:
-                    add(n, nc.vector, (3,), (4,), (4 - v3, 4), "rest4")
-
-        def scalar_prep(n, slot):
-            for (lead, where), step in ((S_ABS, abs_step), (S_M, round_step), (S_FACTOR, factor_step), (S_TANH, tanh_step)):
-                if where == slot:
-                    for g in groups_in_round(n, lead):
-                        step(g)
-
-        def vector_prep(n, slot):
-            for (lead, where), step in ((V_YY, parabola_step), (V_Y, wrap_step)):
-                if where == slot:
-                    for g in groups_in_round(n, lead):
-                        step(g)
 
         with tc.manual_schedule():
             for n in range(FIRST_ROUND, N_CHUNKS + 1):
@@ -411,61 +420,66 @@ def tile_kan_layer_t_kernel(tc, x, spline_coeffs, grad_out, out):
                         nc.sync.dma_start(out=x_sb[:, 2:4, :, :], in_=x_view[:, 2:4, :, :])
                     if g == 1:
                         nc.sync.dma_start(out=x_sb[:, 4:N_GROUPS, :, :], in_=x_view[:, 4:N_GROUPS, :, :])
-                for step in T_ORDER:
-                    if step == 0 and is_chunk(n + 1):
-                        transpose_tau(n + 1)
-                    if step == 1 and is_chunk(n + GRAD_LEAD):
-                        transpose_grad(n + GRAD_LEAD)
-                    if step == 2 and is_chunk(n - 1):
-                        sum_blocks(n - 1)
-                if n == FIRST_ROUND:
-                    for k in range(BASES):
-                        regroup_coeffs(k)
+                if is_chunk(n + 1):
+                    transpose_tau(n + 1)
+                if is_chunk(n + 3):
+                    transpose_grad(n + 3)
+                if n == N_CHUNKS:
+                    sum_last(n - 1)
+                elif is_chunk(n - 1):
+                    sum_blocks(n - 1)
+
                 if is_chunk(n + 1):
                     quantise_grad(n + 1)
-                vector_prep(n, 0)
+                for g in groups_in_round(n, LEAD_PARABOLA):
+                    abs_step(g)
+                    parabola_step(g)
                 for g in groups_in_round(n, LEAD_TAU):
                     tau_step(g)
                 if n == -LEAD_TAU:
-                    quantise_coeffs()
-                scalar_prep(n, 0)
+                    quantise_coeffs((unit_c(4), unit_n(3), unit_c(2), unit_n(5), unit_p(7)))
+                if n == -1:
+                    quantise_coeffs((unit_n(1), unit_c(6), unit_n(7), unit_c(0)))
+
                 for b in range(N_RAMPS):
-                    if b == ODD_AT:
-                        if is_chunk(n - 1):
+                    if b == RELUS_BEFORE_SUMS:
+                        if is_chunk(n - 1) and n < N_CHUNKS:
                             empty_odd_half(n - 1)
-                        scalar_prep(n, 1)
+                        for g in groups_in_round(n, LEAD_WRAP):
+                            round_step(g)
                     if is_chunk(n + 1):
                         ramp_up(n + 1, b)
-                if ODD_AT == N_RAMPS:
-                    if is_chunk(n - 1):
-                        empty_odd_half(n - 1)
-                    scalar_prep(n, 1)
-                scalar_prep(n, 2)
-                if is_chunk(n + GRAD_LEAD):
-                    group_grad(n + GRAD_LEAD)
-                scalar_prep(n, 3)
+                if is_chunk(n + 3):
+                    group_grad(n + 3)
+                for g in groups_in_round(n, LEAD_TAU):
+                    factor_step(g)
+                for g in groups_in_round(n, LEAD_TANH):
+                    tanh_step(g)
+
                 for b in range(N_BLOCKS):
-                    if b == JOIN_AT and is_chunk(n - 1):
+                    if b == N_BLOCKS - 1 and is_chunk(n - 1) and n < LAST_CHUNK:
                         join_halves(n - 1)
                     if is_chunk(n):
                         product(n, b)
                         if b == 1:
-                            add(n, nc.gpsimd, (0,), (1,), (0, GA[n % 2]), "pair1")
-                        if b == 3:
-                            add(n, nc.gpsimd, (2,), (3,), (0, GB[n % 2]), "pair3")
+                            add_on_gpsimd(n, b, CHUNK_TILES)
+                        if b == 3 and n < LAST_CHUNK:
+                            add_on_gpsimd(n, b, SECOND_PAIR_ON_GPSIMD[n % 2])
                     ahead, block = (n, N_BLOCKS - 1) if b == 0 else (n + 1, b - 1)
                     if is_chunk(ahead):
                         multiply_mx(ahead, block)
-                if JOIN_AT == 5 and is_chunk(n - 1):
+                if n == LAST_CHUNK:
                     join_halves(n - 1)
-                if REST_FIRST and is_chunk(n):
-                    vector_adds(n)
-                if not FINISH_LAST and is_chunk(n - 1):
-                    finish(n - 1)
-                vector_prep(n, 1)
+                elif n == N_CHUNKS:
+                    join_last(n - 1)
+                elif is_chunk(n):
+                    add_on_vector(n)
+                for g in groups_in_round(n, LEAD_WRAP):
+                    wrap_step(g)
+                if n == -LEAD_WRAP:
+                    for k in range(BASES):
+                        regroup_coeffs(k)
                 if n == -4:
                     scale_coeffs()
-                if not REST_FIRST and is_chunk(n):
-                    vector_adds(n)
-                if FINISH_LAST and is_chunk(n - 1):
+                if is_chunk(n - 1):
                     finish(n - 1)

from contextlib import ExitStack

import concourse.mybir as mybir
from concourse.masks import make_identity

F32 = mybir.dt.float32
BF16 = mybir.dt.bfloat16
I32 = mybir.dt.int32
U32 = mybir.dt.uint32
U8 = mybir.dt.uint8
E4M3_X4 = mybir.dt.float8_e4m3fn_x4
E5M2_X4 = mybir.dt.float8_e5m2_x4
ALU = mybir.AluOpType
ACT = mybir.ActivationFunctionType

TOKENS, FEATURES, OUT_FEATURES, BASES = 16384, 64, 512, 8
FLOPS = 2 * TOKENS * OUT_FEATURES * FEATURES * BASES
P = 128
PACK = 4
GROUP_TILES = 8
GROUP = P * GROUP_TILES
N_GROUPS = TOKENS // GROUP
GROUP_COLS = GROUP_TILES * FEATURES
CHUNK_TILES = 4
CHUNK = P * CHUNK_TILES
N_CHUNKS = TOKENS // CHUNK
LAST_CHUNK = N_CHUNKS - 1
INV_H = 5.5
KNOTS_SPAN = 11.0
COORD_SCALE = 22.0

N_UNITS = 2 * BASES + 2
N_WINDOWS = BASES + 1
UNIT_IN = FEATURES * PACK
SCALE_STRIDE = 256


def unit_n(k):
    return BASES - 1 - k


def unit_c(k):
    return BASES + (BASES - k) % BASES


def unit_p(k):
    return 2 * BASES + (BASES - 1 - k)


def make_blocks():
    return (
        (0, 2.0, (unit_c(4), unit_n(3), unit_c(2))),
        (1, 2.0, (unit_c(4), unit_n(5), unit_p(7))),
        (2, 2.0, (unit_c(2), unit_n(1))),
        (1, 4.0, (unit_c(6), unit_n(7))),
        (3, 4.0, (unit_c(0),)),
    )


RAMP_KNOTS = ((4, 3), (6, 5), (2, 1), (0, 7))
N_RAMPS = 4


N_BLOCKS = 5
W_BANKS = 4

SECOND_PAIR_ON_GPSIMD = (1, 2)
SECOND_PAIR_ENDS = (4, 4)

LEAD_LOAD = 8
LEAD_TANH = 7
LEAD_WRAP = 5
LEAD_PARABOLA = 3
LEAD_TAU = 2
FIRST_ROUND = -LEAD_TANH
RELUS_BEFORE_SUMS = 3


def tile_kan_layer_t_kernel(tc, x, spline_coeffs, grad_out, out):
    nc = tc.nc
    blocks = make_blocks()
    with ExitStack() as ctx:
        const = ctx.enter_context(tc.tile_pool(name="const", bufs=1))
        gpool = ctx.enter_context(tc.tile_pool(name="gpool", bufs=4))
        two = ctx.enter_context(tc.tile_pool(name="two", bufs=2))
        three = ctx.enter_context(tc.tile_pool(name="three", bufs=3))
        results = ctx.enter_context(tc.tile_pool(name="results", bufs=N_GROUPS))
        ps_grad = ctx.enter_context(tc.psum_pool(name="ps_grad", bufs=2))
        ps_tau = ctx.enter_context(tc.psum_pool(name="ps_tau", bufs=1))
        ps_w = ctx.enter_context(tc.psum_pool(name="ps_w", bufs=W_BANKS))
        ps_sum = ctx.enter_context(tc.psum_pool(name="ps_sum", bufs=1))

        x_sb = const.tile([P, N_GROUPS, GROUP_TILES, FEATURES], BF16)
        x_view = x.rearrange("(g p t) i -> p g t i", p=P, t=GROUP_TILES)
        nc.sync.dma_start(out=x_sb[:, 0:2, :, :], in_=x_view[:, 0:2, :, :])
        coeffs = spline_coeffs.rearrange("o i k -> o (i k)")
        c_rows = const.tile([P, PACK, OUT_FEATURES], BF16)
        for u in range(2):
            nc.sync.dma_start(
                out=c_rows[:, 2 * u : 2 * u + 2, :],
                in_=coeffs[256 * u : 256 * u + 256, :].rearrange("(q e) c -> q e c", e=2),
            )

        ident = const.tile([P, P], F32)
        make_identity(nc, ident[:])
        minus_one = const.tile([P, 1], F32)
        nc.vector.memset(minus_one[:], -1.0)
        ramp_bias = const.tile([P, N_BLOCKS], F32)
        for b, (even_knot, odd_knot) in enumerate(RAMP_KNOTS):
            nc.vector.memset(ramp_bias[0:64, b : b + 1], -1.0 * even_knot)
            nc.vector.memset(ramp_bias[64:128, b : b + 1], -1.0 * odd_knot)

        c_grouped = const.tile([P, N_UNITS * UNIT_IN], BF16, align_bytes=256)
        c_grouped_by_unit = c_grouped[:].rearrange("q (s i t) -> q s i t", s=N_UNITS, t=PACK)
        c_rows_by_k = c_rows[:].rearrange("q t (i k) -> q k i t", k=BASES)
        c_codes = const.tile([P, N_WINDOWS, P], U32, align_bytes=256)
        c_scales = const.tile([P, N_WINDOWS, SCALE_STRIDE], U8, align_bytes=256)

        def regroup_coeffs(k):
            copy = nc.scalar.copy if k in (0, 6, 7) else nc.vector.tensor_copy
            copy(out=c_grouped_by_unit[:, unit_c(k), :, :], in_=c_rows_by_k[:, k, :, :])

        def scale_coeffs():
            for k, units in ((BASES - 1, BASES - 1), (0, 1)):
                nc.vector.tensor_scalar(
                    out=c_grouped[:, unit_n(k) * UNIT_IN : (unit_n(k) + units) * UNIT_IN],
                    in0=c_grouped[:, unit_c(k) * UNIT_IN : (unit_c(k) + units) * UNIT_IN],
                    scalar1=-2.0, scalar2=None, op0=ALU.mult,
                )
            nc.vector.tensor_scalar(
                out=c_grouped[:, unit_p(7) * UNIT_IN : (unit_p(7) + 2) * UNIT_IN],
                in0=c_grouped[:, unit_c(7) * UNIT_IN : (unit_c(7) + 2) * UNIT_IN],
                scalar1=2.0, scalar2=None, op0=ALU.mult,
            )

        def quantise_coeffs(units):
            for v in [unit // 2 for unit in units]:
                nc.vector.quantize_mx(
                    out=c_codes[:, v, :].bitcast(E4M3_X4),
                    scales=c_scales[:, v, 0:P],
                    in_=c_grouped[:, 2 * v * UNIT_IN : (2 * v + 2) * UNIT_IN],
                )

        grad_tiles = {}
        groups = {}
        chunks = {}

        def load_grad(g):
            grad_sb = gpool.tile([P, GROUP_TILES, OUT_FEATURES], BF16, name="grad_sb")
            view = grad_out[g * GROUP : (g + 1) * GROUP, :].rearrange("(p t) o -> p t o", t=GROUP_TILES)
            for tiles in (slice(0, CHUNK_TILES), slice(CHUNK_TILES, GROUP_TILES)) if g == 0 else (slice(0, GROUP_TILES),):
                nc.sync.dma_start(out=grad_sb[:, tiles, :], in_=view[:, tiles, :])
            grad_tiles[g] = grad_sb

        def by_tile(ap):
            return ap.rearrange("p (t i) -> p t i", i=FEATURES)

        def pieces(g):
            if g == 0:
                return (slice(0, GROUP_COLS // 2), slice(GROUP_COLS // 2, GROUP_COLS))
            return (slice(0, GROUP_COLS),)

        def tanh_step(g):
            th = three.tile([P, GROUP_COLS], F32, name="th")
            x_cols = x_sb[:, g, :, :].rearrange("p t i -> p (t i)")
            for cols in pieces(g):
                nc.scalar.activation(out=th[:, cols], in_=x_cols[:, cols], func=ACT.Sigmoid, scale=2.0)
            groups[g] = {"th": th}

        def round_step(g):
            m_int = two.tile([P, GROUP_COLS], U32, name="m_int")
            for cols in pieces(g):
                nc.scalar.activation(
                    out=m_int[:, cols], in_=groups[g]["th"][:, cols], func=ACT.Copy, scale=0.5 * KNOTS_SPAN
                )
            groups[g]["m_int"] = m_int

        def factor_step(g):
            factor = three.tile([P, GROUP_COLS], F32, name="factor")
            nc.scalar.activation(out=factor[:], in_=groups[g]["th"][:], func=ACT.Square, bias=minus_one[:, 0:1], scale=2.0)
            groups[g]["factor"] = factor

        def wrap_step(g):
            y = two.tile([P, GROUP_COLS], F32, name="y")
            for cols in pieces(g):
                nc.vector.scalar_tensor_tensor(
                    out=y[:, cols], in0=groups[g]["m_int"][:, cols].bitcast(I32), scalar=-2.0 / KNOTS_SPAN,
                    in1=groups[g]["th"][:, cols], op0=ALU.mult, op1=ALU.add,
                )
            groups[g]["y"] = y

        def abs_step(g):
            abs_y = two.tile([P, GROUP_COLS], F32, name="abs_y")
            for cols in pieces(g):
                nc.scalar.activation(
                    out=abs_y[:, cols], in_=groups[g]["y"][:, cols], func=ACT.Abs, scale=0.5 * KNOTS_SPAN
                )
            groups[g]["abs_y"] = abs_y

        def parabola_step(g):
            y_abs_y = two.tile([P, GROUP_COLS], F32, name="y_abs_y")
            for cols in pieces(g):
                if g > 1:
                    nc.vector.memset(y_abs_y[:, 0:1], 0.0)
                (nc.gpsimd if g > 1 else nc.vector).tensor_tensor(
                    out=y_abs_y[:, cols], in0=groups[g]["y"][:, cols], in1=groups[g]["abs_y"][:, cols], op=ALU.mult
                )
            groups[g]["y_abs_y"] = y_abs_y

        def tau_step(g):
            tau = three.tile([P, GROUP_TILES, 2 * FEATURES], F32, name="tau")
            all_tiles = [slice(cols.start // FEATURES, cols.stop // FEATURES) for cols in pieces(g)]
            for cols, tiles in zip(pieces(g), all_tiles):
                nc.vector.scalar_tensor_tensor(
                    out=tau[:, tiles, 0:FEATURES], in0=by_tile(groups[g]["m_int"][:, cols].bitcast(I32)),
                    scalar=2.0 / COORD_SCALE, in1=by_tile(groups[g]["y_abs_y"][:, cols]), op0=ALU.mult, op1=ALU.add,
                )
            for cols, tiles in zip(pieces(g), all_tiles):
                (nc.gpsimd if g > 0 else nc.vector).tensor_tensor(
                    out=tau[:, tiles, FEATURES : 2 * FEATURES], in0=by_tile(groups[g]["th"][:, cols]),
                    in1=tau[:, tiles, 0:FEATURES], op=ALU.subtract,
                )
            groups[g]["tau"] = tau

        def first_tile(n):
            return n // 2, (n % 2) * CHUNK_TILES

        def transpose_grad(n):
            g, t0 = first_tile(n)
            banks = []
            for b in range(2):
                grad_t = ps_grad.tile([P, 2, 2, P], F32, name="grad_t")
                for a in range(2):
                    words = grad_tiles[g][:, t0 + 2 * b + a, :].bitcast(F32)
                    for u in range(2):
                        nc.tensor.transpose(grad_t[:, a, u, :], words[:, P * u : P * u + P], ident[:])
                banks.append(grad_t)
            chunks[n] = {"grad_t": banks, "w": {}, "product": {}}

        def transpose_tau(n):
            g, t0 = first_tile(n)
            tau = groups[g]["tau"]
            tau_t = ps_tau.tile([P, CHUNK], F32, name="tau_t")
            for a in range(CHUNK_TILES):
                nc.tensor.transpose(tau_t[:, P * a : P * a + P], tau[:, t0 + a, :], ident[:])
            chunks[n]["tau_t"] = tau_t

        def group_grad(n):
            grouped = three.tile([P, PACK * CHUNK], BF16, align_bytes=256, name="grouped")
            grouped_words = grouped[:].bitcast(F32)
            for b in range(2):
                nc.scalar.copy(
                    out=grouped_words[:, 512 * b : 512 * b + 512].rearrange("p (a r u) -> p a r u", a=2, u=2),
                    in_=chunks[n]["grad_t"][b][:].rearrange("p a u r -> p a r u"),
                )
            chunks[n]["grouped"] = grouped

        def quantise_grad(n):
            g_codes = two.tile([P, CHUNK], U32, align_bytes=256, name="g_codes")
            g_scales = two.tile([P, CHUNK], U8, align_bytes=256, name="g_scales")
            nc.vector.quantize_mx(out=g_codes[:].bitcast(E5M2_X4), scales=g_scales[:], in_=chunks[n]["grouped"][:])
            chunks[n]["g_codes"] = g_codes
            chunks[n]["g_scales"] = g_scales

        def ramp_up(n, b):
            if b == 0:
                ramp = two.tile([P, N_RAMPS, CHUNK], F32, name="ramp")
                chunks[n]["ramp"] = ramp
            nc.scalar.activation(
                out=chunks[n]["ramp"][:, b, :], in_=chunks[n]["tau_t"][:], func=ACT.Relu,
                bias=ramp_bias[:, b : b + 1], scale=COORD_SCALE,
            )

        def multiply_mx(n, b):
            w = ps_w.tile([P, CHUNK], F32, name="w")
            units = blocks[b][2]
            for s, unit in enumerate(units):
                v = unit // 2
                nc.tensor.matmul_mx(
                    out=w[:],
                    lhsT=c_codes[:, v, :].bitcast(E4M3_X4),
                    lhsT_scale=c_scales[:, v, 0:P],
                    rhs=chunks[n]["g_codes"][:].bitcast(E5M2_X4),
                    rhs_scale=chunks[n]["g_scales"][:],
                    start=(s == 0),
                    stop=(s == len(units) - 1),
                )
            chunks[n]["w"][b] = w

        def product(n, b):
            prod = two.tile([P, CHUNK], F32, name="prod%d" % b)
            nc.vector.scalar_tensor_tensor(
                out=prod[:], in0=chunks[n]["ramp"][:, blocks[b][0], :], scalar=blocks[b][1], in1=chunks[n]["w"][b][:],
                op0=ALU.min, op1=ALU.mult,
            )
            chunks[n]["product"][b] = prod

        def add_on_gpsimd(n, b, n_tiles):
            pair = two.tile([P, CHUNK], F32, name="pair%d" % b)
            nc.gpsimd.tensor_tensor(
                out=pair[:, 0 : P * n_tiles], in0=chunks[n]["product"][b - 1][:, 0 : P * n_tiles],
                in1=chunks[n]["product"][b][:, 0 : P * n_tiles], op=ALU.add,
            )
            chunks[n]["pair%d" % b] = pair

        def add_on_vector(n):
            cols = slice(P * SECOND_PAIR_ON_GPSIMD[n % 2], P * SECOND_PAIR_ENDS[n % 2])
            rest = two.tile([P, CHUNK], F32, name="rest")
            nc.vector.tensor_tensor(
                out=rest[:, cols], in0=chunks[n]["product"][2][:, cols], in1=chunks[n]["product"][3][:, cols], op=ALU.add
            )
            chunks[n]["rest"] = rest

        def sum_blocks(n):
            sums = ps_sum.tile([P, CHUNK_TILES, 2, FEATURES], F32, name="sums")
            for a in range(CHUNK_TILES):
                cols = slice(P * a, P * a + P)
                if a < SECOND_PAIR_ON_GPSIMD[n % 2]:
                    second_pair = [chunks[n]["pair3"][:, cols]]
                elif a < SECOND_PAIR_ENDS[n % 2]:
                    second_pair = [chunks[n]["rest"][:, cols]]
                else:
                    second_pair = [chunks[n]["product"][2][:, cols], chunks[n]["product"][3][:, cols]]
                terms = [chunks[n]["pair1"][:, cols]] + second_pair + [chunks[n]["product"][N_BLOCKS - 1][:, cols]]
                for s, term in enumerate(terms):
                    nc.tensor.matmul(
                        sums[:, a, :, :].rearrange("p h i -> p (h i)"),
                        lhsT=term,
                        rhs=ident[:],
                        is_transpose=True,
                        start=(s == 0),
                        stop=(s == len(terms) - 1),
                    )
            chunks[n]["sums"] = sums

        def sum_last(n):
            keys = ["pair1", 2, 3, N_BLOCKS - 1]
            halves = []
            for a in range(CHUNK_TILES):
                if a < CHUNK_TILES - 1:
                    bank = ps_w.tile([P, CHUNK], F32, name="w")
                    halves.append(bank[:, 0:P].rearrange("p (h i) -> p h i", h=2))
                else:
                    bank = ps_sum.tile([P, CHUNK_TILES, 2, FEATURES], F32, name="sums")
                    halves.append(bank[:, 0, :, :])
            for part in (slice(0, 3), slice(3, 4)):
                for a in range(CHUNK_TILES):
                    for key in keys[part]:
                        term = chunks[n]["pair1"] if key == "pair1" else chunks[n]["product"][key]
                        nc.tensor.matmul(
                            halves[a].rearrange("p h i -> p (h i)"),
                            lhsT=term[:, P * a : P * a + P],
                            rhs=ident[:],
                            is_transpose=True,
                            start=(key == keys[0]),
                            stop=(key == keys[-1]),
                        )
            chunks[n]["halves"] = halves

        def join_last(n):
            odd_half = three.tile([P, CHUNK_TILES, FEATURES], F32, name="odd_half")
            joined = two.tile([P, CHUNK_TILES, FEATURES], F32, name="joined")
            for a in range(CHUNK_TILES):
                nc.scalar.activation(
                    out=odd_half[:, a, :], in_=chunks[n]["halves"][a][:, 1, :], func=ACT.Copy, scale=-0.5 * INV_H
                )
            for a in range(CHUNK_TILES):
                nc.vector.scalar_tensor_tensor(
                    out=joined[:, a, :], in0=chunks[n]["halves"][a][:, 0, :], scalar=-0.5 * INV_H,
                    in1=odd_half[:, a, :], op0=ALU.mult, op1=ALU.add,
                )
            chunks[n]["joined"] = joined

        def empty_odd_half(n):
            odd_half = three.tile([P, CHUNK_TILES, FEATURES], F32, name="odd_half")
            nc.scalar.activation(out=odd_half[:], in_=chunks[n]["sums"][:, :, 1, :], func=ACT.Copy, scale=-0.5 * INV_H)
            chunks[n]["odd_half"] = odd_half

        def join_halves(n):
            joined = two.tile([P, CHUNK_TILES, FEATURES], F32, name="joined")
            nc.vector.scalar_tensor_tensor(
                out=joined[:], in0=chunks[n]["sums"][:, :, 0, :], scalar=-0.5 * INV_H, in1=chunks[n]["odd_half"][:],
                op0=ALU.mult, op1=ALU.add,
            )
            chunks[n]["joined"] = joined

        def finish(n):
            g, t0 = first_tile(n)
            if t0 == 0:
                result = results.tile([P, GROUP_TILES, FEATURES], F32, name="result")
                groups[g]["result"] = result
            result = groups[g]["result"]
            nc.vector.scalar_tensor_tensor(
                out=result[:, t0 : t0 + CHUNK_TILES, :].rearrange("p a i -> p (a i)"),
                in0=groups[g]["factor"][:, t0 * FEATURES : (t0 + CHUNK_TILES) * FEATURES],
                scalar=1.0,
                in1=chunks[n]["joined"][:].rearrange("p a i -> p (a i)"),
                op0=ALU.subtract,
                op1=ALU.mult,
            )
            rows = out[g * GROUP : (g + 1) * GROUP, :].rearrange("(p t) i -> p t i", t=GROUP_TILES)
            if g == N_GROUPS - 1:
                nc.sync.dma_start(
                    out=rows[:, t0 : t0 + CHUNK_TILES, :], in_=result[:, t0 : t0 + CHUNK_TILES, :]
                )
            elif t0 != 0:
                nc.sync.dma_start(out=rows, in_=result[:])

        def is_chunk(n):
            return 0 <= n < N_CHUNKS

        def groups_in_round(n, lead):
            return [g for g in range(N_GROUPS) if max(2 * g - lead, FIRST_ROUND) == n]

        with tc.manual_schedule():
            for n in range(FIRST_ROUND, N_CHUNKS + 1):
                for g in groups_in_round(n, LEAD_LOAD):
                    load_grad(g)
                    if g == 0:
                        nc.sync.dma_start(out=x_sb[:, 2:4, :, :], in_=x_view[:, 2:4, :, :])
                    if g == 1:
                        nc.sync.dma_start(out=x_sb[:, 4:N_GROUPS, :, :], in_=x_view[:, 4:N_GROUPS, :, :])
                if is_chunk(n + 1):
                    transpose_tau(n + 1)
                if is_chunk(n + 3):
                    transpose_grad(n + 3)
                if n == N_CHUNKS:
                    sum_last(n - 1)
                elif is_chunk(n - 1):
                    sum_blocks(n - 1)

                if is_chunk(n + 1):
                    quantise_grad(n + 1)
                for g in groups_in_round(n, LEAD_PARABOLA):
                    abs_step(g)
                    parabola_step(g)
                for g in groups_in_round(n, LEAD_TAU):
                    tau_step(g)
                if n == -LEAD_TAU:
                    quantise_coeffs((unit_c(4), unit_n(3), unit_c(2), unit_n(5), unit_p(7)))
                if n == -1:
                    quantise_coeffs((unit_n(1), unit_c(6), unit_n(7), unit_c(0)))

                for b in range(N_RAMPS):
                    if b == RELUS_BEFORE_SUMS:
                        if is_chunk(n - 1) and n < N_CHUNKS:
                            empty_odd_half(n - 1)
                        for g in groups_in_round(n, LEAD_WRAP):
                            round_step(g)
                    if is_chunk(n + 1):
                        ramp_up(n + 1, b)
                if is_chunk(n + 3):
                    group_grad(n + 3)
                for g in groups_in_round(n, LEAD_TAU):
                    factor_step(g)
                for g in groups_in_round(n, LEAD_TANH):
                    tanh_step(g)

                for b in range(N_BLOCKS):
                    if b == N_BLOCKS - 1 and is_chunk(n - 1) and n < LAST_CHUNK:
                        join_halves(n - 1)
                    if is_chunk(n):
                        product(n, b)
                        if b == 1:
                            add_on_gpsimd(n, b, CHUNK_TILES)
                        if b == 3 and n < LAST_CHUNK:
                            add_on_gpsimd(n, b, SECOND_PAIR_ON_GPSIMD[n % 2])
                    ahead, block = (n, N_BLOCKS - 1) if b == 0 else (n + 1, b - 1)
                    if is_chunk(ahead):
                        multiply_mx(ahead, block)
                if n == LAST_CHUNK:
                    join_halves(n - 1)
                elif n == N_CHUNKS:
                    join_last(n - 1)
                elif is_chunk(n):
                    add_on_vector(n)
                for g in groups_in_round(n, LEAD_WRAP):
                    wrap_step(g)
                if n == -LEAD_WRAP:
                    for k in range(BASES):
                        regroup_coeffs(k)
                if n == -4:
                    scale_coeffs()
                if is_chunk(n - 1):
                    finish(n - 1)
